import numpy as np
import ml_dtypes


def mxq(x, axis, fmt="e4m3"):
    dtype, down = {"e4m3": (ml_dtypes.float8_e4m3fn, 7), "e5m2": (ml_dtypes.float8_e5m2, 14)}[fmt]
    v = np.moveaxis(np.asarray(x, np.float32).astype(ml_dtypes.bfloat16).astype(np.float64), axis, -1)
    blocks = v.reshape(v.shape[:-1] + (-1, 32))
    amax = np.abs(blocks).max(-1, keepdims=True)
    byte = np.maximum(np.where(amax > 0, np.frexp(amax)[1] - 1 + 127, 0) - down, 1)
    scale = np.exp2(byte - 127.0)
    codes = (blocks / scale).astype(np.float32).astype(dtype).astype(np.float64)
    return np.moveaxis((codes * scale).reshape(v.shape), -1, axis)


WIDE = False


def mx_kscale(k):
    if not WIDE:
        return np.ones(k)
    levels = np.array([20, -20, 10, -10, 0])
    a = np.random.permutation(np.resize(levels, k // 512 * 4)).reshape(k // 512, 4)
    idx = np.arange(k)
    return np.exp2(a[idx // 512, idx % 128 // 32])


BF16 = ml_dtypes.bfloat16


def bf(x):
    return np.asarray(x, np.float32).astype(BF16)


def f64(x):
    return np.asarray(x).astype(np.float64)


B, C, H, W, KL = 2, 512, 64, 64, 7
N = B * H * W


def sigmoid(v):
    return 1.0 / (1.0 + np.exp(-v))


def local_crf(F_w, Q, k):
    pad = k // 2
    Qp = np.pad(Q, ((0, 0), (0, 0), (pad, pad), (pad, pad)))
    out = np.zeros_like(Q)
    for p in range(k * k):
        di, dj = p // k, p % k
        out = out + F_w[:, p:p + 1] * Qp[:, :, di:di + H, dj:dj + W]
    return out


def setup_inputs():
    s = mx_kscale(N).reshape(B, 1, H, W)
    Fw = np.random.uniform(0.0, 1.0, (B, KL * KL, H, W)) * 12.0 / (KL * KL) * s
    lg = np.random.standard_normal((B, C, H, W)) * 0.8 * np.sqrt(2.0 * np.log(C))
    cp = np.random.uniform(-0.05, 0.05, (C, C, 1, 1))
    g = np.random.standard_normal((B, C, H, W)) * np.exp2(np.random.randint(-12, 1, (B, 1, H, W))) / s
    return {"input_F": bf(Fw), "input_logit": bf(lg), "compatibility": bf(cp), "grad_out": bf(g)}


def reference(input_F, input_logit, compatibility, grad_out):
    x = f64(input_logit)
    e = np.exp(x - x.max(axis=1, keepdims=True))
    Q = e / e.sum(axis=1, keepdims=True)
    m = local_crf(f64(input_F), Q, KL)
    M = m.transpose(1, 0, 2, 3).reshape(C, N)
    G = f64(grad_out).transpose(1, 0, 2, 3).reshape(C, N)
    P = mxq(G, 1, "e5m2") @ mxq(M, 1, "e4m3").T
    comp = sigmoid(100.0 * f64(compatibility))[:, :, 0, 0]
    return (-100.0 * comp * (1.0 - comp) * P).reshape(C, C, 1, 1)

@@ -1,0 +1,217 @@
+from contextlib import ExitStack
+
+import concourse.mybir as mybir
+from concourse.masks import make_identity
+
+F32 = mybir.dt.float32
+BF16 = mybir.dt.bfloat16
+U32 = mybir.dt.uint32
+U8 = mybir.dt.uint8
+E4M3_X4 = mybir.dt.float8_e4m3fn_x4
+E5M2_X4 = mybir.dt.float8_e5m2_x4
+FUNC = mybir.ActivationFunctionType
+ALU = mybir.AluOpType
+AXIS = mybir.AxisListType
+
+P = 128
+IMAGES, CHANNELS, HEIGHT, WIDTH, KERNEL = 2, 512, 64, 64, 7
+REACH = KERNEL // 2
+TAPS = KERNEL * KERNEL
+PIXELS = HEIGHT * WIDTH
+CHUNKS = CHANNELS // P
+TILE_ROWS = P // WIDTH
+TILES = PIXELS // P
+PACK = 4
+PASS_PIXELS = P * PACK
+PASS_ROWS = PASS_PIXELS // WIDTH
+PASSES = PIXELS // PASS_PIXELS
+PAD = 68
+SOFTMAX_LEAD = 2
+SCALAR_EVERY = 3
+
+FLOPS = 2 * CHANNELS * CHANNELS * IMAGES * PIXELS + 2 * TAPS * CHANNELS * IMAGES * PIXELS
+
+
+def tile_localcrf_kernel(tc, input_F, input_logit, compatibility, grad_out, out):
+    nc = tc.nc
+    logit_view = input_logit.rearrange("b (k c) i j -> b c k (i j)", c=P)
+    grad_view = grad_out.rearrange("b (k o) i j -> b o k (i j)", o=P)
+    comp_view = compatibility.rearrange("(k o) c a b -> o k (c a b)", o=P)
+    out_view = out.rearrange("(k o) c a b -> o k (c a b)", o=P)
+
+    with ExitStack() as stack:
+        keep = stack.enter_context(tc.tile_pool(name="keep", bufs=1))
+        slabs = stack.enter_context(tc.tile_pool(name="slabs", bufs=2))
+        soft = stack.enter_context(tc.tile_pool(name="soft", bufs=3))
+        sums = stack.enter_context(tc.tile_pool(name="sums", bufs=6))
+        products = stack.enter_context(tc.tile_pool(name="products", bufs=8))
+        operands = stack.enter_context(tc.tile_pool(name="operands", bufs=2))
+        psum_p = stack.enter_context(tc.psum_pool(name="psum_p", bufs=1))
+        psum_vector = stack.enter_context(tc.psum_pool(name="psum_vector", bufs=2))
+        psum_scalar = stack.enter_context(tc.psum_pool(name="psum_scalar", bufs=2))
+
+        ident_bf = keep.tile([P, P], BF16)
+        make_identity(nc, ident_bf[:])
+        ident_f32 = keep.tile([P, P], F32)
+        make_identity(nc, ident_f32[:])
+
+        comp_bf = keep.tile([P, CHUNKS, CHANNELS], BF16)
+        nc.sync.dma_start(out=comp_bf[:], in_=comp_view)
+        factor = keep.tile([P, CHUNKS, CHANNELS], F32)
+        one_minus = keep.tile([P, CHUNKS, CHANNELS], F32)
+        nc.scalar.activation(out=factor[:], in_=comp_bf[:], func=FUNC.Sigmoid, scale=100.0)
+        nc.scalar.activation(out=one_minus[:], in_=comp_bf[:], func=FUNC.Sigmoid, scale=-100.0)
+        nc.vector.scalar_tensor_tensor(
+            out=factor[:], in0=factor[:], scalar=-100.0, in1=one_minus[:], op0=ALU.mult, op1=ALU.mult
+        )
+
+        f_raw = keep.tile([P, IMAGES * PIXELS], BF16)
+        nc.vector.memset(f_raw[:], 0.0)
+        for b in range(IMAGES):
+            f_rows = f_raw[:, b * PIXELS : (b + 1) * PIXELS].rearrange("p (i j) -> p i j", j=WIDTH)
+            for dj in range(KERNEL):
+                lo = max(0, REACH - dj)
+                hi = WIDTH - max(0, dj - REACH)
+                nc.scalar.dma_start(out=f_rows[dj:TAPS:KERNEL, :, lo:hi], in_=input_F[b, dj:TAPS:KERNEL, :, lo:hi])
+        taps = keep.tile([P, IMAGES * TILES, TAPS], F32)
+        per_bank = 8
+        for first in range(0, IMAGES * TILES, per_bank):
+            f_px = psum_scalar.tile([P, per_bank, P], BF16, tag="scalar_bank")
+            for n in range(per_bank):
+                nc.tensor.transpose(f_px[:, n, :], f_raw[:, (first + n) * P : (first + n + 1) * P], ident_bf[:])
+            nc.scalar.copy(out=taps[:, first : first + per_bank, :], in_=f_px[:, :, 0:TAPS])
+
+        q_chan = keep.tile([P, CHUNKS, PAD + PIXELS + PAD], F32)
+        nc.vector.memset(q_chan[:, :, 0:PAD], 0.0)
+        nc.vector.memset(q_chan[:, :, PAD + PIXELS :], 0.0)
+
+        def softmax_pass(b, s):
+            x_slab = slabs.tile([P, CHUNKS, PASS_PIXELS], BF16)
+            nc.sync.dma_start(out=x_slab[:], in_=logit_view[b][:, :, s * PASS_PIXELS : (s + 1) * PASS_PIXELS])
+            for t in range(PACK):
+                x_px = psum_scalar.tile([P, CHANNELS], BF16, tag="scalar_bank")
+                for k in range(CHUNKS):
+                    nc.tensor.transpose(x_px[:, k * P : (k + 1) * P], x_slab[:, k, t * P : (t + 1) * P], ident_bf[:])
+                top = soft.tile([P, 1], F32)
+                nc.vector.reduce_max(out=top[:], in_=x_px[:], axis=AXIS.X)
+                minus_top = soft.tile([P, 1], F32)
+                nc.vector.tensor_scalar_mul(out=minus_top[:], in0=top[:], scalar1=-1.0)
+                q_px = soft.tile([P, CHANNELS], F32)
+                total = soft.tile([P, 1], F32)
+                nc.scalar.activation(
+                    out=q_px[:], in_=x_px[:], func=FUNC.Exp, bias=minus_top[:], scale=1.0, accum_out=total[:]
+                )
+                inverse = soft.tile([P, 1], F32)
+                nc.vector.reciprocal(out=inverse[:], in_=total[:])
+                nc.scalar.activation(out=q_px[:], in_=q_px[:], func=FUNC.Copy, scale=inverse[:])
+                q_back = psum_scalar.tile([P, CHUNKS, P], F32, tag="scalar_bank")
+                for k in range(CHUNKS):
+                    nc.tensor.transpose(q_back[:, k, :], q_px[:, k * P : (k + 1) * P], ident_f32[:])
+                start = PAD + s * PASS_PIXELS + t * P
+                nc.scalar.copy(out=q_chan[:, :, start : start + P], in_=q_back[:])
+
+        def grad_pass(b, s):
+            g_slab = slabs.tile([P, CHUNKS, PASS_PIXELS], BF16)
+            nc.sync.dma_start(out=g_slab[:], in_=grad_view[b][:, :, s * PASS_PIXELS : (s + 1) * PASS_PIXELS])
+            g_grouped = operands.tile([P, CHANNELS, PACK], BF16, align_bytes=64)
+            half = CHANNELS // 2
+            for h in range(2):
+                g_px = psum_scalar.tile([P, PACK, half], BF16, tag="scalar_bank")
+                for t in range(PACK):
+                    for k in range(half // P):
+                        nc.tensor.transpose(
+                            g_px[:, t, k * P : (k + 1) * P],
+                            g_slab[:, h * (half // P) + k, t * P : (t + 1) * P],
+                            ident_bf[:],
+                        )
+                nc.scalar.copy(out=g_grouped[:, h * half : (h + 1) * half, :], in_=g_px[:].rearrange("p t o -> p o t"))
+            g_words = operands.tile([P, CHANNELS], U32, align_bytes=64)
+            g_scales = operands.tile([P, CHANNELS], U8, align_bytes=64)
+            nc.vector.quantize_mx(
+                out=g_words[:].bitcast(E5M2_X4), scales=g_scales[:], in_=g_grouped[:].rearrange("p o t -> p (o t)")
+            )
+            return g_words, g_scales
+
+        p_banks = [psum_p.tile([P, CHANNELS], F32, name="p_bank%d" % k) for k in range(CHUNKS)]
+
+        for s in range(SOFTMAX_LEAD):
+            softmax_pass(0, s)
+
+        window_count = 0
+        for b in range(IMAGES):
+            sum_vector = {}
+            sum_gpsimd = {}
+            grad_operand = {}
+            m_rows = None
+            for r in range(-1, HEIGHT):
+                if r % PASS_ROWS == 0:
+                    ahead = b * PASSES + r // PASS_ROWS + SOFTMAX_LEAD
+                    if ahead < IMAGES * PASSES:
+                        softmax_pass(ahead // PASSES, ahead % PASSES)
+                if r % PASS_ROWS == PASS_ROWS // 2:
+                    grad_operand[r // PASS_ROWS] = grad_pass(b, r // PASS_ROWS)
+
+                first_tile = max(0, (r - REACH + 1) // TILE_ROWS)
+                last_tile = min(TILES - 1, (r + REACH) // TILE_ROWS)
+                for dj in range(KERNEL):
+                    to_scalar = window_count % SCALAR_EVERY == SCALAR_EVERY - 1
+                    window_count += 1
+                    start = PAD + r * WIDTH + dj - REACH
+                    if to_scalar:
+                        window = psum_scalar.tile([P, CHANNELS], F32, tag="scalar_bank")
+                    else:
+                        window = psum_vector.tile([P, CHANNELS], F32, tag="vector_bank")
+                    for k in range(CHUNKS):
+                        nc.tensor.transpose(window[:, k * P : (k + 1) * P], q_chan[:, k, start : start + P], ident_f32[:])
+                    for i in range(first_tile, last_tile + 1):
+                        tap = (r - TILE_ROWS * i + REACH) * KERNEL + dj
+                        weight = taps[:, b * TILES + i, tap : tap + 1]
+                        if to_scalar and i not in sum_gpsimd:
+                            partial = sums.tile([P, CHANNELS], F32, tag="sum_gpsimd")
+                            sum_gpsimd[i] = partial
+                            nc.scalar.activation(out=partial[:], in_=window[:], func=FUNC.Copy, scale=weight)
+                        elif to_scalar:
+                            product = products.tile([P, CHANNELS], F32)
+                            nc.scalar.activation(out=product[:], in_=window[:], func=FUNC.Copy, scale=weight)
+                            nc.gpsimd.tensor_tensor(out=sum_gpsimd[i][:], in0=sum_gpsimd[i][:], in1=product[:], op=ALU.add)
+                        elif i not in sum_vector:
+                            partial = sums.tile([P, CHANNELS], F32, tag="sum_vector")
+                            sum_vector[i] = partial
+                            nc.vector.tensor_scalar_mul(out=partial[:], in0=window[:], scalar1=weight)
+                        else:
+                            nc.vector.scalar_tensor_tensor(
+                                out=sum_vector[i][:], in0=window[:], scalar=weight, in1=sum_vector[i][:],
+                                op0=ALU.mult, op1=ALU.add,
+                            )
+
+                for i in range(TILES):
+                    if min(TILE_ROWS * i + REACH, HEIGHT - 1) != r:
+                        continue
+                    s, t = divmod(i, PACK)
+                    if t == 0:
+                        m_rows = operands.tile([P, PACK, CHANNELS], BF16)
+                    nc.vector.tensor_tensor(out=m_rows[:, t, :], in0=sum_vector[i][:], in1=sum_gpsimd[i][:], op=ALU.add)
+                    if t < PACK - 1:
+                        continue
+                    m_grouped = operands.tile([P, CHANNELS, PACK], BF16, align_bytes=64)
+                    nc.scalar.copy(out=m_grouped[:], in_=m_rows[:].rearrange("p t c -> p c t"))
+                    m_words = operands.tile([P, CHANNELS], U32, align_bytes=64)
+                    m_scales = operands.tile([P, CHANNELS], U8, align_bytes=64)
+                    nc.vector.quantize_mx(
+                        out=m_words[:].bitcast(E4M3_X4), scales=m_scales[:], in_=m_grouped[:].rearrange("p c t -> p (c t)")
+                    )
+                    g_words, g_scales = grad_operand[s]
+                    for k in range(CHUNKS):
+                        nc.tensor.matmul_mx(
+                            out=p_banks[k][:],
+                            lhsT=g_words[:, k * P : (k + 1) * P].bitcast(E5M2_X4),
+                            lhsT_scale=g_scales[:, k * P : (k + 1) * P],
+                            rhs=m_words[:].bitcast(E4M3_X4),
+                            rhs_scale=m_scales[:],
+                            start=(b == 0 and s == 0),
+                            stop=(b == IMAGES - 1 and s == PASSES - 1),
+                        )
+
+        for k in range(CHUNKS):
+            nc.vector.tensor_tensor(out=factor[:, k, :], in0=p_banks[k][:], in1=factor[:, k, :], op=ALU.mult)
+            nc.sync.dma_start(out=out_view[:, k, :], in_=factor[:, k, :])

@@ -42,52 +42,55 @@ def tile_localcrf_kernel(tc, input_F, input_logit, compatibility, grad_out, out)
     with ExitStack() as stack:
         keep = stack.enter_context(tc.tile_pool(name="keep", bufs=1))
         slabs = stack.enter_context(tc.tile_pool(name="slabs", bufs=2))
-        soft = stack.enter_context(tc.tile_pool(name="soft", bufs=3))
-        sums = stack.enter_context(tc.tile_pool(name="sums", bufs=6))
-        products = stack.enter_context(tc.tile_pool(name="products", bufs=8))
-        operands = stack.enter_context(tc.tile_pool(name="operands", bufs=2))
-        psum_p = stack.enter_context(tc.psum_pool(name="psum_p", bufs=1))
-        psum_vector = stack.enter_context(tc.psum_pool(name="psum_vector", bufs=2))
-        psum_scalar = stack.enter_context(tc.psum_pool(name="psum_scalar", bufs=2))
+        soft = stack.enter_context(tc.tile_pool(name="soft", bufs=6))
+        sums = stack.enter_context(tc.tile_pool(name="sums", bufs=2))
+        psum_vector = stack.enter_context(tc.psum_pool(name="psum_vector", bufs=4))
+        psum_scalar = stack.enter_context(tc.psum_pool(name="psum_scalar", bufs=4))
 
         ident_bf = keep.tile([P, P], BF16)
         make_identity(nc, ident_bf[:])
         ident_f32 = keep.tile([P, P], F32)
         make_identity(nc, ident_f32[:])
 
-        comp_bf = keep.tile([P, CHUNKS, CHANNELS], BF16)
-        nc.sync.dma_start(out=comp_bf[:], in_=comp_view)
+        q_chan = [keep.tile([P, PAD + PIXELS + PAD], F32, name="q_chan%d" % k) for k in range(CHUNKS)]
+        for k in range(CHUNKS):
+            nc.vector.memset(q_chan[k][:, 0:PAD], 0.0)
+            nc.vector.memset(q_chan[k][:, PAD + PIXELS :], 0.0)
+
         factor = keep.tile([P, CHUNKS, CHANNELS], F32)
-        one_minus = keep.tile([P, CHUNKS, CHANNELS], F32)
-        nc.scalar.activation(out=factor[:], in_=comp_bf[:], func=FUNC.Sigmoid, scale=100.0)
-        nc.scalar.activation(out=one_minus[:], in_=comp_bf[:], func=FUNC.Sigmoid, scale=-100.0)
-        nc.vector.scalar_tensor_tensor(
-            out=factor[:], in0=factor[:], scalar=-100.0, in1=one_minus[:], op0=ALU.mult, op1=ALU.mult
-        )
-
-        f_raw = keep.tile([P, IMAGES * PIXELS], BF16)
-        nc.vector.memset(f_raw[:], 0.0)
-        for b in range(IMAGES):
-            f_rows = f_raw[:, b * PIXELS : (b + 1) * PIXELS].rearrange("p (i j) -> p i j", j=WIDTH)
-            for dj in range(KERNEL):
-                lo = max(0, REACH - dj)
-                hi = WIDTH - max(0, dj - REACH)
-                nc.scalar.dma_start(out=f_rows[dj:TAPS:KERNEL, :, lo:hi], in_=input_F[b, dj:TAPS:KERNEL, :, lo:hi])
         taps = keep.tile([P, IMAGES * TILES, TAPS], F32)
-        per_bank = 8
-        for first in range(0, IMAGES * TILES, per_bank):
-            f_px = psum_scalar.tile([P, per_bank, P], BF16, tag="scalar_bank")
-            for n in range(per_bank):
-                nc.tensor.transpose(f_px[:, n, :], f_raw[:, (first + n) * P : (first + n + 1) * P], ident_bf[:])
-            nc.scalar.copy(out=taps[:, first : first + per_bank, :], in_=f_px[:, :, 0:TAPS])
+        with tc.tile_pool(name="setup", bufs=1) as setup:
+            comp_bf = setup.tile([P, CHUNKS, CHANNELS], BF16)
+            nc.sync.dma_start(out=comp_bf[:], in_=comp_view)
+            one_minus = setup.tile([P, CHUNKS, CHANNELS], F32)
+            nc.scalar.activation(out=factor[:], in_=comp_bf[:], func=FUNC.Sigmoid, scale=100.0)
+            nc.scalar.activation(out=one_minus[:], in_=comp_bf[:], func=FUNC.Sigmoid, scale=-100.0)
+            nc.vector.scalar_tensor_tensor(
+                out=factor[:], in0=factor[:], scalar=-100.0, in1=one_minus[:], op0=ALU.mult, op1=ALU.mult
+            )
 
-        q_chan = keep.tile([P, CHUNKS, PAD + PIXELS + PAD], F32)
-        nc.vector.memset(q_chan[:, :, 0:PAD], 0.0)
-        nc.vector.memset(q_chan[:, :, PAD + PIXELS :], 0.0)
+            f_raw = setup.tile([P, IMAGES * PIXELS], BF16)
+            nc.vector.memset(f_raw[:], 0.0)
+            for b in range(IMAGES):
+                f_rows = f_raw[:, b * PIXELS : (b + 1) * PIXELS].rearrange("p (i j) -> p i j", j=WIDTH)
+                for dj in range(KERNEL):
+                    lo = max(0, REACH - dj)
+                    hi = WIDTH - max(0, dj - REACH)
+                    nc.scalar.dma_start(out=f_rows[dj:TAPS:KERNEL, :, lo:hi], in_=input_F[b, dj:TAPS:KERNEL, :, lo:hi])
+            per_bank = 8
+            for first in range(0, IMAGES * TILES, per_bank):
+                f_px = psum_scalar.tile([P, per_bank, P], BF16, tag="scalar_bank")
+                for n in range(per_bank):
+                    nc.tensor.transpose(f_px[:, n, :], f_raw[:, (first + n) * P : (first + n + 1) * P], ident_bf[:])
+                nc.scalar.copy(out=taps[:, first : first + per_bank, :], in_=f_px[:, :, 0:TAPS])
+
+        products = stack.enter_context(tc.tile_pool(name="products", bufs=4))
+        operands = stack.enter_context(tc.tile_pool(name="operands", bufs=2))
 
         def softmax_pass(b, s):
             x_slab = slabs.tile([P, CHUNKS, PASS_PIXELS], BF16)
             nc.sync.dma_start(out=x_slab[:], in_=logit_view[b][:, :, s * PASS_PIXELS : (s + 1) * PASS_PIXELS])
+            q_px = []
             for t in range(PACK):
                 x_px = psum_scalar.tile([P, CHANNELS], BF16, tag="scalar_bank")
                 for k in range(CHUNKS):
@@ -96,19 +99,20 @@ def tile_localcrf_kernel(tc, input_F, input_logit, compatibility, grad_out, out)
                 nc.vector.reduce_max(out=top[:], in_=x_px[:], axis=AXIS.X)
                 minus_top = soft.tile([P, 1], F32)
                 nc.vector.tensor_scalar_mul(out=minus_top[:], in0=top[:], scalar1=-1.0)
-                q_px = soft.tile([P, CHANNELS], F32)
+                q_px.append(soft.tile([P, CHANNELS], F32, name="q_px"))
                 total = soft.tile([P, 1], F32)
                 nc.scalar.activation(
-                    out=q_px[:], in_=x_px[:], func=FUNC.Exp, bias=minus_top[:], scale=1.0, accum_out=total[:]
+                    out=q_px[t][:], in_=x_px[:], func=FUNC.Exp, bias=minus_top[:], scale=1.0, accum_out=total[:]
                 )
                 inverse = soft.tile([P, 1], F32)
                 nc.vector.reciprocal(out=inverse[:], in_=total[:])
-                nc.scalar.activation(out=q_px[:], in_=q_px[:], func=FUNC.Copy, scale=inverse[:])
-                q_back = psum_scalar.tile([P, CHUNKS, P], F32, tag="scalar_bank")
-                for k in range(CHUNKS):
-                    nc.tensor.transpose(q_back[:, k, :], q_px[:, k * P : (k + 1) * P], ident_f32[:])
-                start = PAD + s * PASS_PIXELS + t * P
-                nc.scalar.copy(out=q_chan[:, :, start : start + P], in_=q_back[:])
+                nc.scalar.activation(out=q_px[t][:], in_=q_px[t][:], func=FUNC.Copy, scale=inverse[:])
+            start = PAD + s * PASS_PIXELS
+            for k in range(CHUNKS):
+                q_back = psum_scalar.tile([P, PASS_PIXELS], F32, tag="scalar_bank")
+                for t in range(PACK):
+                    nc.tensor.transpose(q_back[:, t * P : (t + 1) * P], q_px[t][:, k * P : (k + 1) * P], ident_f32[:])
+                nc.scalar.copy(out=q_chan[k][:, start : start + PASS_PIXELS], in_=q_back[:])
 
         def grad_pass(b, s):
             g_slab = slabs.tile([P, CHUNKS, PASS_PIXELS], BF16)
@@ -132,17 +136,19 @@ def tile_localcrf_kernel(tc, input_F, input_logit, compatibility, grad_out, out)
             )
             return g_words, g_scales
 
-        p_banks = [psum_p.tile([P, CHANNELS], F32, name="p_bank%d" % k) for k in range(CHUNKS)]
+        p_sum = keep.tile([P, CHUNKS, CHANNELS], F32)
 
         for s in range(SOFTMAX_LEAD):
             softmax_pass(0, s)
 
+        last_row_of_pass = [min(TILE_ROWS * (PACK * s + PACK - 1) + REACH, HEIGHT - 1) for s in range(PASSES)]
         window_count = 0
         for b in range(IMAGES):
             sum_vector = {}
             sum_gpsimd = {}
+            begun_vector = set()
+            begun_gpsimd = set()
             grad_operand = {}
-            m_rows = None
             for r in range(-1, HEIGHT):
                 if r % PASS_ROWS == 0:
                     ahead = b * PASSES + r // PASS_ROWS + SOFTMAX_LEAD
@@ -153,6 +159,10 @@ def tile_localcrf_kernel(tc, input_F, input_logit, compatibility, grad_out, out)
 
                 first_tile = max(0, (r - REACH + 1) // TILE_ROWS)
                 last_tile = min(TILES - 1, (r + REACH) // TILE_ROWS)
+                for s in range(first_tile // PACK, last_tile // PACK + 1):
+                    if s not in sum_vector:
+                        sum_vector[s] = sums.tile([P, PACK, CHANNELS], F32, name="sum_vector")
+                        sum_gpsimd[s] = sums.tile([P, PACK, CHANNELS], F32, name="sum_gpsimd")
                 for dj in range(KERNEL):
                     to_scalar = window_count % SCALAR_EVERY == SCALAR_EVERY - 1
                     window_count += 1
@@ -162,56 +172,71 @@ def tile_localcrf_kernel(tc, input_F, input_logit, compatibility, grad_out, out)
                     else:
                         window = psum_vector.tile([P, CHANNELS], F32, tag="vector_bank")
                     for k in range(CHUNKS):
-                        nc.tensor.transpose(window[:, k * P : (k + 1) * P], q_chan[:, k, start : start + P], ident_f32[:])
-                    for i in range(first_tile, last_tile + 1):
-                        tap = (r - TILE_ROWS * i + REACH) * KERNEL + dj
-                        weight = taps[:, b * TILES + i, tap : tap + 1]
-                        if to_scalar and i not in sum_gpsimd:
-                            partial = sums.tile([P, CHANNELS], F32, tag="sum_gpsimd")
-                            sum_gpsimd[i] = partial
-                            nc.scalar.activation(out=partial[:], in_=window[:], func=FUNC.Copy, scale=weight)
-                        elif to_scalar:
-                            product = products.tile([P, CHANNELS], F32)
-                            nc.scalar.activation(out=product[:], in_=window[:], func=FUNC.Copy, scale=weight)
-                            nc.gpsimd.tensor_tensor(out=sum_gpsimd[i][:], in0=sum_gpsimd[i][:], in1=product[:], op=ALU.add)
-                        elif i not in sum_vector:
-                            partial = sums.tile([P, CHANNELS], F32, tag="sum_vector")
-                            sum_vector[i] = partial
-                            nc.vector.tensor_scalar_mul(out=partial[:], in0=window[:], scalar1=weight)
-                        else:
-                            nc.vector.scalar_tensor_tensor(
-                                out=sum_vector[i][:], in0=window[:], scalar=weight, in1=sum_vector[i][:],
-                                op0=ALU.mult, op1=ALU.add,
-                            )
+                        nc.tensor.transpose(window[:, k * P : (k + 1) * P], q_chan[k][:, start : start + P], ident_f32[:])
 
-                for i in range(TILES):
-                    if min(TILE_ROWS * i + REACH, HEIGHT - 1) != r:
-                        continue
-                    s, t = divmod(i, PACK)
-                    if t == 0:
-                        m_rows = operands.tile([P, PACK, CHANNELS], BF16)
-                    nc.vector.tensor_tensor(out=m_rows[:, t, :], in0=sum_vector[i][:], in1=sum_gpsimd[i][:], op=ALU.add)
-                    if t < PACK - 1:
-                        continue
-                    m_grouped = operands.tile([P, CHANNELS, PACK], BF16, align_bytes=64)
-                    nc.scalar.copy(out=m_grouped[:], in_=m_rows[:].rearrange("p t c -> p c t"))
-                    m_words = operands.tile([P, CHANNELS], U32, align_bytes=64)
-                    m_scales = operands.tile([P, CHANNELS], U8, align_bytes=64)
-                    nc.vector.quantize_mx(
-                        out=m_words[:].bitcast(E4M3_X4), scales=m_scales[:], in_=m_grouped[:].rearrange("p c t -> p (c t)")
+                    if to_scalar:
+                        last_begun = max([i for i in range(first_tile, last_tile + 1) if i in begun_gpsimd], default=-1)
+                        if last_begun >= first_tile:
+                            product = products.tile([P, PACK, CHANNELS], F32)
+                        for i in range(first_tile, last_tile + 1):
+                            tap = (r - TILE_ROWS * i + REACH) * KERNEL + dj
+                            if i <= last_begun:
+                                target = product[:, i - first_tile, :]
+                            else:
+                                target = sum_gpsimd[i // PACK][:, i % PACK, :]
+                                begun_gpsimd.add(i)
+                            nc.scalar.activation(
+                                out=target, in_=window[:], func=FUNC.Copy, scale=taps[:, b * TILES + i, tap : tap + 1]
+                            )
+                        for s in range(first_tile // PACK, last_begun // PACK + 1):
+                            lo = max(first_tile, s * PACK)
+                            hi = min(last_begun, s * PACK + PACK - 1)
+                            running = sum_gpsimd[s][:, lo - s * PACK : hi - s * PACK + 1, :]
+                            nc.gpsimd.tensor_tensor(
+                                out=running, in0=running, in1=product[:, lo - first_tile : hi - first_tile + 1, :], op=ALU.add
+                            )
+                    else:
+                        for i in range(first_tile, last_tile + 1):
+                            tap = (r - TILE_ROWS * i + REACH) * KERNEL + dj
+                            weight = taps[:, b * TILES + i, tap : tap + 1]
+                            running = sum_vector[i // PACK][:, i % PACK, :]
+                            if i in begun_vector:
+                                nc.vector.scalar_tensor_tensor(
+                                    out=running, in0=window[:], scalar=weight, in1=running, op0=ALU.mult, op1=ALU.add
+                                )
+                            else:
+                                nc.vector.tensor_scalar_mul(out=running, in0=window[:], scalar1=weight)
+                                begun_vector.add(i)
+
+                if r not in last_row_of_pass:
+                    continue
+                s = last_row_of_pass.index(r)
+                m_rows = operands.tile([P, PACK, CHANNELS], BF16)
+                nc.vector.tensor_tensor(out=m_rows[:], in0=sum_vector[s][:], in1=sum_gpsimd[s][:], op=ALU.add)
+                m_grouped = operands.tile([P, CHANNELS, PACK], BF16, align_bytes=64)
+                nc.scalar.copy(out=m_grouped[:], in_=m_rows[:].rearrange("p t c -> p c t"))
+                m_words = operands.tile([P, CHANNELS], U32, align_bytes=64)
+                m_scales = operands.tile([P, CHANNELS], U8, align_bytes=64)
+                nc.vector.quantize_mx(
+                    out=m_words[:].bitcast(E4M3_X4), scales=m_scales[:], in_=m_grouped[:].rearrange("p c t -> p (c t)")
+                )
+                g_words, g_scales = grad_operand[s]
+                for k in range(CHUNKS):
+                    p_pass = psum_vector.tile([P, CHANNELS], F32, tag="vector_bank")
+                    nc.tensor.matmul_mx(
+                        out=p_pass[:],
+                        lhsT=g_words[:, k * P : (k + 1) * P].bitcast(E5M2_X4),
+                        lhsT_scale=g_scales[:, k * P : (k + 1) * P],
+                        rhs=m_words[:].bitcast(E4M3_X4),
+                        rhs_scale=m_scales[:],
+                        start=True,
+                        stop=True,
                     )
-                    g_words, g_scales = grad_operand[s]
-                    for k in range(CHUNKS):
-                        nc.tensor.matmul_mx(
-                            out=p_banks[k][:],
-                            lhsT=g_words[:, k * P : (k + 1) * P].bitcast(E5M2_X4),
-                            lhsT_scale=g_scales[:, k * P : (k + 1) * P],
-                            rhs=m_words[:].bitcast(E4M3_X4),
-                            rhs_scale=m_scales[:],
-                            start=(b == 0 and s == 0),
-                            stop=(b == IMAGES - 1 and s == PASSES - 1),
-                        )
+                    if b == 0 and s == 0:
+                        nc.vector.tensor_copy(out=p_sum[:, k, :], in_=p_pass[:])
+                    else:
+                        nc.vector.tensor_tensor(out=p_sum[:, k, :], in0=p_pass[:], in1=p_sum[:, k, :], op=ALU.add)
 
         for k in range(CHUNKS):
-            nc.vector.tensor_tensor(out=factor[:, k, :], in0=p_banks[k][:], in1=factor[:, k, :], op=ALU.mult)
+            nc.vector.tensor_tensor(out=factor[:, k, :], in0=p_sum[:, k, :], in1=factor[:, k, :], op=ALU.mult)
             nc.sync.dma_start(out=out_view[:, k, :], in_=factor[:, k, :])

@@ -26,8 +26,8 @@ PASS_PIXELS = P * PACK
 PASS_ROWS = PASS_PIXELS // WIDTH
 PASSES = PIXELS // PASS_PIXELS
 PAD = 68
-SOFTMAX_LEAD = 2
-SCALAR_EVERY = 3
+WINDOW_CYCLE = 5
+SCALAR_TURNS = (1, 3)
 
 FLOPS = 2 * CHANNELS * CHANNELS * IMAGES * PIXELS + 2 * TAPS * CHANNELS * IMAGES * PIXELS
 
@@ -56,36 +56,6 @@ def tile_localcrf_kernel(tc, input_F, input_logit, compatibility, grad_out, out)
         for k in range(CHUNKS):
             nc.vector.memset(q_chan[k][:, 0:PAD], 0.0)
             nc.vector.memset(q_chan[k][:, PAD + PIXELS :], 0.0)
-
-        factor = keep.tile([P, CHUNKS, CHANNELS], F32)
-        taps = keep.tile([P, IMAGES * TILES, TAPS], F32)
-        with tc.tile_pool(name="setup", bufs=1) as setup:
-            comp_bf = setup.tile([P, CHUNKS, CHANNELS], BF16)
-            nc.sync.dma_start(out=comp_bf[:], in_=comp_view)
-            one_minus = setup.tile([P, CHUNKS, CHANNELS], F32)
-            nc.scalar.activation(out=factor[:], in_=comp_bf[:], func=FUNC.Sigmoid, scale=100.0)
-            nc.scalar.activation(out=one_minus[:], in_=comp_bf[:], func=FUNC.Sigmoid, scale=-100.0)
-            nc.vector.scalar_tensor_tensor(
-                out=factor[:], in0=factor[:], scalar=-100.0, in1=one_minus[:], op0=ALU.mult, op1=ALU.mult
-            )
-
-            f_raw = setup.tile([P, IMAGES * PIXELS], BF16)
-            nc.vector.memset(f_raw[:], 0.0)
-            for b in range(IMAGES):
-                f_rows = f_raw[:, b * PIXELS : (b + 1) * PIXELS].rearrange("p (i j) -> p i j", j=WIDTH)
-                for dj in range(KERNEL):
-                    lo = max(0, REACH - dj)
-                    hi = WIDTH - max(0, dj - REACH)
-                    nc.scalar.dma_start(out=f_rows[dj:TAPS:KERNEL, :, lo:hi], in_=input_F[b, dj:TAPS:KERNEL, :, lo:hi])
-            per_bank = 8
-            for first in range(0, IMAGES * TILES, per_bank):
-                f_px = psum_scalar.tile([P, per_bank, P], BF16, tag="scalar_bank")
-                for n in range(per_bank):
-                    nc.tensor.transpose(f_px[:, n, :], f_raw[:, (first + n) * P : (first + n + 1) * P], ident_bf[:])
-                nc.scalar.copy(out=taps[:, first : first + per_bank, :], in_=f_px[:, :, 0:TAPS])
-
-        products = stack.enter_context(tc.tile_pool(name="products", bufs=4))
-        operands = stack.enter_context(tc.tile_pool(name="operands", bufs=2))
 
         def softmax_pass(b, s):
             x_slab = slabs.tile([P, CHUNKS, PASS_PIXELS], BF16)
@@ -136,10 +106,39 @@ def tile_localcrf_kernel(tc, input_F, input_logit, compatibility, grad_out, out)
             )
             return g_words, g_scales
 
-        p_sum = keep.tile([P, CHUNKS, CHANNELS], F32)
+        softmax_pass(0, 0)
 
-        for s in range(SOFTMAX_LEAD):
-            softmax_pass(0, s)
+        factor = keep.tile([P, CHUNKS, CHANNELS], F32)
+        taps = keep.tile([P, IMAGES * TILES, TAPS], F32)
+        with tc.tile_pool(name="setup", bufs=1) as setup:
+            comp_bf = setup.tile([P, CHUNKS, CHANNELS], BF16)
+            nc.scalar.dma_start(out=comp_bf[:], in_=comp_view)
+            one_minus = setup.tile([P, CHUNKS, CHANNELS], F32)
+            nc.scalar.activation(out=factor[:], in_=comp_bf[:], func=FUNC.Sigmoid, scale=100.0)
+            nc.scalar.activation(out=one_minus[:], in_=comp_bf[:], func=FUNC.Sigmoid, scale=-100.0)
+            nc.vector.scalar_tensor_tensor(
+                out=factor[:], in0=factor[:], scalar=-100.0, in1=one_minus[:], op0=ALU.mult, op1=ALU.mult
+            )
+
+            f_raw = setup.tile([P, IMAGES * PIXELS], BF16)
+            nc.vector.memset(f_raw[:], 0.0)
+            for b in range(IMAGES):
+                f_rows = f_raw[:, b * PIXELS : (b + 1) * PIXELS].rearrange("p (i j) -> p i j", j=WIDTH)
+                for dj in range(KERNEL):
+                    lo = max(0, REACH - dj)
+                    hi = WIDTH - max(0, dj - REACH)
+                    nc.scalar.dma_start(out=f_rows[dj:TAPS:KERNEL, :, lo:hi], in_=input_F[b, dj:TAPS:KERNEL, :, lo:hi])
+            per_bank = 8
+            for first in range(0, IMAGES * TILES, per_bank):
+                f_px = psum_scalar.tile([P, per_bank, P], BF16, tag="scalar_bank")
+                for n in range(per_bank):
+                    nc.tensor.transpose(f_px[:, n, :], f_raw[:, (first + n) * P : (first + n + 1) * P], ident_bf[:])
+                nc.scalar.copy(out=taps[:, first : first + per_bank, :], in_=f_px[:, :, 0:TAPS])
+
+        products = stack.enter_context(tc.tile_pool(name="products", bufs=4))
+        operands = stack.enter_context(tc.tile_pool(name="operands", bufs=2))
+
+        p_sum = keep.tile([P, CHUNKS, CHANNELS], F32)
 
         last_row_of_pass = [min(TILE_ROWS * (PACK * s + PACK - 1) + REACH, HEIGHT - 1) for s in range(PASSES)]
         window_count = 0
@@ -150,8 +149,8 @@ def tile_localcrf_kernel(tc, input_F, input_logit, compatibility, grad_out, out)
             begun_gpsimd = set()
             grad_operand = {}
             for r in range(-1, HEIGHT):
-                if r % PASS_ROWS == 0:
-                    ahead = b * PASSES + r // PASS_ROWS + SOFTMAX_LEAD
+                if (r + 1) % PASS_ROWS == 0 and r < HEIGHT - 1:
+                    ahead = b * PASSES + (r + 1) // PASS_ROWS + 1
                     if ahead < IMAGES * PASSES:
                         softmax_pass(ahead // PASSES, ahead % PASSES)
                 if r % PASS_ROWS == PASS_ROWS // 2:
@@ -164,7 +163,7 @@ def tile_localcrf_kernel(tc, input_F, input_logit, compatibility, grad_out, out)
                         sum_vector[s] = sums.tile([P, PACK, CHANNELS], F32, name="sum_vector")
                         sum_gpsimd[s] = sums.tile([P, PACK, CHANNELS], F32, name="sum_gpsimd")
                 for dj in range(KERNEL):
-                    to_scalar = window_count % SCALAR_EVERY == SCALAR_EVERY - 1
+                    to_scalar = window_count % WINDOW_CYCLE in SCALAR_TURNS
                     window_count += 1
                     start = PAD + r * WIDTH + dj - REACH
                     if to_scalar:

@@ -26,8 +26,11 @@ PASS_PIXELS = P * PACK
 PASS_ROWS = PASS_PIXELS // WIDTH
 PASSES = PIXELS // PASS_PIXELS
 PAD = 68
-WINDOW_CYCLE = 5
-SCALAR_TURNS = (1, 3)
+SCALAR_WINDOWS_ODD_ROW = (0, 1, 3, 5)
+SCALAR_WINDOWS_EVEN_ROW = ()
+RING = 2 * PACK
+MERGE_AFTER = 2
+GROUP = 2
 
 FLOPS = 2 * CHANNELS * CHANNELS * IMAGES * PIXELS + 2 * TAPS * CHANNELS * IMAGES * PIXELS
 
@@ -57,69 +60,71 @@ def tile_localcrf_kernel(tc, input_F, input_logit, compatibility, grad_out, out)
             nc.vector.memset(q_chan[k][:, 0:PAD], 0.0)
             nc.vector.memset(q_chan[k][:, PAD + PIXELS :], 0.0)
 
-        def softmax_pass(b, s):
-            x_slab = slabs.tile([P, CHUNKS, PASS_PIXELS], BF16)
-            nc.sync.dma_start(out=x_slab[:], in_=logit_view[b][:, :, s * PASS_PIXELS : (s + 1) * PASS_PIXELS])
-            q_px = []
-            for t in range(PACK):
-                x_px = psum_scalar.tile([P, CHANNELS], BF16, tag="scalar_bank")
-                for k in range(CHUNKS):
-                    nc.tensor.transpose(x_px[:, k * P : (k + 1) * P], x_slab[:, k, t * P : (t + 1) * P], ident_bf[:])
-                top = soft.tile([P, 1], F32)
-                nc.vector.reduce_max(out=top[:], in_=x_px[:], axis=AXIS.X)
-                minus_top = soft.tile([P, 1], F32)
-                nc.vector.tensor_scalar_mul(out=minus_top[:], in0=top[:], scalar1=-1.0)
-                q_px.append(soft.tile([P, CHANNELS], F32, name="q_px"))
-                total = soft.tile([P, 1], F32)
-                nc.scalar.activation(
-                    out=q_px[t][:], in_=x_px[:], func=FUNC.Exp, bias=minus_top[:], scale=1.0, accum_out=total[:]
-                )
-                inverse = soft.tile([P, 1], F32)
-                nc.vector.reciprocal(out=inverse[:], in_=total[:])
-                nc.scalar.activation(out=q_px[t][:], in_=q_px[t][:], func=FUNC.Copy, scale=inverse[:])
-            start = PAD + s * PASS_PIXELS
-            for k in range(CHUNKS):
-                q_back = psum_scalar.tile([P, PASS_PIXELS], F32, tag="scalar_bank")
-                for t in range(PACK):
-                    nc.tensor.transpose(q_back[:, t * P : (t + 1) * P], q_px[t][:, k * P : (k + 1) * P], ident_f32[:])
-                nc.scalar.copy(out=q_chan[k][:, start : start + PASS_PIXELS], in_=q_back[:])
+        x_slab = {}
+        q_px = {}
+        total = {}
+        g_slab = {}
+        g_grouped = {}
+        grad_operand = {}
 
-        def grad_pass(b, s):
-            g_slab = slabs.tile([P, CHUNKS, PASS_PIXELS], BF16)
-            nc.sync.dma_start(out=g_slab[:], in_=grad_view[b][:, :, s * PASS_PIXELS : (s + 1) * PASS_PIXELS])
-            g_grouped = operands.tile([P, CHANNELS, PACK], BF16, align_bytes=64)
+        def pixels_of(g):
+            return slice((g % PASSES) * PASS_PIXELS, (g % PASSES + 1) * PASS_PIXELS)
+
+        def load_logits(g):
+            x_slab[g] = slabs.tile([P, CHUNKS, PASS_PIXELS], BF16, name="x_slab")
+            nc.sync.dma_start(out=x_slab[g][:], in_=logit_view[g // PASSES][:, :, pixels_of(g)])
+            total[g] = soft.tile([P, PACK], F32, name="total")
+
+        def exponentials(g, t):
+            x_px = psum_scalar.tile([P, CHANNELS], BF16, tag="scalar_bank")
+            for k in range(CHUNKS):
+                nc.tensor.transpose(x_px[:, k * P : (k + 1) * P], x_slab[g][:, k, t * P : (t + 1) * P], ident_bf[:])
+            minus_top = soft.tile([P, 1], F32)
+            nc.vector.reduce_max(out=minus_top[:], in_=x_px[:], axis=AXIS.X, negate=True)
+            q_px[g, t] = soft.tile([P, CHANNELS], F32, name="q_px")
+            nc.scalar.activation(
+                out=q_px[g, t][:], in_=x_px[:], func=FUNC.Exp, bias=minus_top[:], scale=1.0,
+                accum_out=total[g][:, t : t + 1],
+            )
+
+        def normalise(g):
+            inverse = soft.tile([P, PACK], F32)
+            nc.vector.reciprocal(out=inverse[:], in_=total[g][:])
+            for t in range(PACK):
+                nc.scalar.activation(out=q_px[g, t][:], in_=q_px[g, t][:], func=FUNC.Copy, scale=inverse[:, t : t + 1])
+
+        def to_channels(g, k):
+            q_back = psum_scalar.tile([P, PASS_PIXELS], F32, tag="scalar_bank")
+            for t in range(PACK):
+                nc.tensor.transpose(q_back[:, t * P : (t + 1) * P], q_px[g, t][:, k * P : (k + 1) * P], ident_f32[:])
+            start = PAD + (g % PASSES) * PASS_PIXELS
+            nc.scalar.copy(out=q_chan[k][:, start : start + PASS_PIXELS], in_=q_back[:])
+
+        def load_grad(g):
+            g_slab[g] = slabs.tile([P, CHUNKS, PASS_PIXELS], BF16, name="g_slab")
+            nc.sync.dma_start(out=g_slab[g][:], in_=grad_view[g // PASSES][:, :, pixels_of(g)])
+            g_grouped[g] = operands.tile([P, CHANNELS, PACK], BF16, name="g_grouped", align_bytes=64)
+
+        def gather_grad(g, h):
             half = CHANNELS // 2
-            for h in range(2):
-                g_px = psum_scalar.tile([P, PACK, half], BF16, tag="scalar_bank")
-                for t in range(PACK):
-                    for k in range(half // P):
-                        nc.tensor.transpose(
-                            g_px[:, t, k * P : (k + 1) * P],
-                            g_slab[:, h * (half // P) + k, t * P : (t + 1) * P],
-                            ident_bf[:],
-                        )
-                nc.scalar.copy(out=g_grouped[:, h * half : (h + 1) * half, :], in_=g_px[:].rearrange("p t o -> p o t"))
+            g_px = psum_scalar.tile([P, PACK, half], BF16, tag="scalar_bank")
+            for t in range(PACK):
+                for k in range(half // P):
+                    nc.tensor.transpose(
+                        g_px[:, t, k * P : (k + 1) * P], g_slab[g][:, h * (half // P) + k, t * P : (t + 1) * P], ident_bf[:]
+                    )
+            nc.scalar.copy(out=g_grouped[g][:, h * half : (h + 1) * half, :], in_=g_px[:].rearrange("p t o -> p o t"))
+
+        def quantise_grad(g):
             g_words = operands.tile([P, CHANNELS], U32, align_bytes=64)
             g_scales = operands.tile([P, CHANNELS], U8, align_bytes=64)
             nc.vector.quantize_mx(
-                out=g_words[:].bitcast(E5M2_X4), scales=g_scales[:], in_=g_grouped[:].rearrange("p o t -> p (o t)")
+                out=g_words[:].bitcast(E5M2_X4), scales=g_scales[:], in_=g_grouped[g][:].rearrange("p o t -> p (o t)")
             )
-            return g_words, g_scales
+            grad_operand[g] = (g_words, g_scales)
 
-        softmax_pass(0, 0)
-
-        factor = keep.tile([P, CHUNKS, CHANNELS], F32)
         taps = keep.tile([P, IMAGES * TILES, TAPS], F32)
         with tc.tile_pool(name="setup", bufs=1) as setup:
-            comp_bf = setup.tile([P, CHUNKS, CHANNELS], BF16)
-            nc.scalar.dma_start(out=comp_bf[:], in_=comp_view)
-            one_minus = setup.tile([P, CHUNKS, CHANNELS], F32)
-            nc.scalar.activation(out=factor[:], in_=comp_bf[:], func=FUNC.Sigmoid, scale=100.0)
-            nc.scalar.activation(out=one_minus[:], in_=comp_bf[:], func=FUNC.Sigmoid, scale=-100.0)
-            nc.vector.scalar_tensor_tensor(
-                out=factor[:], in0=factor[:], scalar=-100.0, in1=one_minus[:], op0=ALU.mult, op1=ALU.mult
-            )
-
             f_raw = setup.tile([P, IMAGES * PIXELS], BF16)
             nc.vector.memset(f_raw[:], 0.0)
             for b in range(IMAGES):
@@ -128,113 +133,179 @@ def tile_localcrf_kernel(tc, input_F, input_logit, compatibility, grad_out, out)
                     lo = max(0, REACH - dj)
                     hi = WIDTH - max(0, dj - REACH)
                     nc.scalar.dma_start(out=f_rows[dj:TAPS:KERNEL, :, lo:hi], in_=input_F[b, dj:TAPS:KERNEL, :, lo:hi])
+            load_logits(0)
+            for t in range(PACK):
+                exponentials(0, t)
+            normalise(0)
             per_bank = 8
             for first in range(0, IMAGES * TILES, per_bank):
-                f_px = psum_scalar.tile([P, per_bank, P], BF16, tag="scalar_bank")
+                f_px = psum_vector.tile([P, per_bank, P], BF16, tag="vector_bank")
                 for n in range(per_bank):
                     nc.tensor.transpose(f_px[:, n, :], f_raw[:, (first + n) * P : (first + n + 1) * P], ident_bf[:])
-                nc.scalar.copy(out=taps[:, first : first + per_bank, :], in_=f_px[:, :, 0:TAPS])
+                nc.vector.tensor_copy(out=taps[:, first : first + per_bank, :], in_=f_px[:, :, 0:TAPS])
+            for k in range(CHUNKS):
+                to_channels(0, k)
 
         products = stack.enter_context(tc.tile_pool(name="products", bufs=4))
         operands = stack.enter_context(tc.tile_pool(name="operands", bufs=2))
 
+        factor = keep.tile([P, CHUNKS, CHANNELS], F32)
+
+        helper = {}
+
+        def load_compatibility():
+            helper["z"] = operands.tile([P, CHUNKS, CHANNELS], BF16, name="comp_bf", tag="m_rows")
+            nc.sync.dma_start(out=helper["z"][:], in_=comp_view)
+
+        def sigmoids():
+            helper["1-s"] = products.tile([P, CHUNKS, CHANNELS], F32, name="one_minus", tag="product")
+            nc.scalar.activation(out=factor[:], in_=helper["z"][:], func=FUNC.Sigmoid, scale=100.0)
+            nc.scalar.activation(out=helper["1-s"][:], in_=helper["z"][:], func=FUNC.Sigmoid, scale=-100.0)
+
+        def finish_factor():
+            nc.vector.scalar_tensor_tensor(
+                out=factor[:], in0=factor[:], scalar=-100.0, in1=helper["1-s"][:], op0=ALU.mult, op1=ALU.mult
+            )
+
         p_sum = keep.tile([P, CHUNKS, CHANNELS], F32)
 
-        last_row_of_pass = [min(TILE_ROWS * (PACK * s + PACK - 1) + REACH, HEIGHT - 1) for s in range(PASSES)]
-        window_count = 0
-        for b in range(IMAGES):
-            sum_vector = {}
-            sum_gpsimd = {}
-            begun_vector = set()
-            begun_gpsimd = set()
-            grad_operand = {}
-            for r in range(-1, HEIGHT):
-                if (r + 1) % PASS_ROWS == 0 and r < HEIGHT - 1:
-                    ahead = b * PASSES + (r + 1) // PASS_ROWS + 1
-                    if ahead < IMAGES * PASSES:
-                        softmax_pass(ahead // PASSES, ahead % PASSES)
-                if r % PASS_ROWS == PASS_ROWS // 2:
-                    grad_operand[r // PASS_ROWS] = grad_pass(b, r // PASS_ROWS)
+        sum_gpsimd = keep.tile([P, RING, CHANNELS], F32)
 
-                first_tile = max(0, (r - REACH + 1) // TILE_ROWS)
-                last_tile = min(TILES - 1, (r + REACH) // TILE_ROWS)
-                for s in range(first_tile // PACK, last_tile // PACK + 1):
-                    if s not in sum_vector:
-                        sum_vector[s] = sums.tile([P, PACK, CHANNELS], F32, name="sum_vector")
-                        sum_gpsimd[s] = sums.tile([P, PACK, CHANNELS], F32, name="sum_gpsimd")
-                for dj in range(KERNEL):
-                    to_scalar = window_count % WINDOW_CYCLE in SCALAR_TURNS
-                    window_count += 1
-                    start = PAD + r * WIDTH + dj - REACH
-                    if to_scalar:
-                        window = psum_scalar.tile([P, CHANNELS], F32, tag="scalar_bank")
-                    else:
-                        window = psum_vector.tile([P, CHANNELS], F32, tag="vector_bank")
-                    for k in range(CHUNKS):
-                        nc.tensor.transpose(window[:, k * P : (k + 1) * P], q_chan[k][:, start : start + P], ident_f32[:])
+        sum_vector = {}
+        begun = {}
+        m_rows = {}
+        m_grouped = {}
+        m_operand = {}
 
-                    if to_scalar:
-                        last_begun = max([i for i in range(first_tile, last_tile + 1) if i in begun_gpsimd], default=-1)
-                        if last_begun >= first_tile:
-                            product = products.tile([P, PACK, CHANNELS], F32)
-                        for i in range(first_tile, last_tile + 1):
-                            tap = (r - TILE_ROWS * i + REACH) * KERNEL + dj
-                            if i <= last_begun:
-                                target = product[:, i - first_tile, :]
-                            else:
-                                target = sum_gpsimd[i // PACK][:, i % PACK, :]
-                                begun_gpsimd.add(i)
-                            nc.scalar.activation(
-                                out=target, in_=window[:], func=FUNC.Copy, scale=taps[:, b * TILES + i, tap : tap + 1]
-                            )
-                        for s in range(first_tile // PACK, last_begun // PACK + 1):
-                            lo = max(first_tile, s * PACK)
-                            hi = min(last_begun, s * PACK + PACK - 1)
-                            running = sum_gpsimd[s][:, lo - s * PACK : hi - s * PACK + 1, :]
-                            nc.gpsimd.tensor_tensor(
-                                out=running, in0=running, in1=product[:, lo - first_tile : hi - first_tile + 1, :], op=ALU.add
-                            )
-                    else:
-                        for i in range(first_tile, last_tile + 1):
-                            tap = (r - TILE_ROWS * i + REACH) * KERNEL + dj
-                            weight = taps[:, b * TILES + i, tap : tap + 1]
-                            running = sum_vector[i // PACK][:, i % PACK, :]
-                            if i in begun_vector:
-                                nc.vector.scalar_tensor_tensor(
-                                    out=running, in0=window[:], scalar=weight, in1=running, op0=ALU.mult, op1=ALU.add
-                                )
-                            else:
-                                nc.vector.tensor_scalar_mul(out=running, in0=window[:], scalar1=weight)
-                                begun_vector.add(i)
-
-                if r not in last_row_of_pass:
-                    continue
-                s = last_row_of_pass.index(r)
-                m_rows = operands.tile([P, PACK, CHANNELS], BF16)
-                nc.vector.tensor_tensor(out=m_rows[:], in0=sum_vector[s][:], in1=sum_gpsimd[s][:], op=ALU.add)
-                m_grouped = operands.tile([P, CHANNELS, PACK], BF16, align_bytes=64)
-                nc.scalar.copy(out=m_grouped[:], in_=m_rows[:].rearrange("p t c -> p c t"))
-                m_words = operands.tile([P, CHANNELS], U32, align_bytes=64)
-                m_scales = operands.tile([P, CHANNELS], U8, align_bytes=64)
-                nc.vector.quantize_mx(
-                    out=m_words[:].bitcast(E4M3_X4), scales=m_scales[:], in_=m_grouped[:].rearrange("p c t -> p (c t)")
-                )
-                g_words, g_scales = grad_operand[s]
+        def window_row(b, r):
+            first_tile = b * TILES + max(0, (r - REACH + 1) // TILE_ROWS)
+            last_tile = b * TILES + min(TILES - 1, (r + REACH) // TILE_ROWS)
+            for g in range(first_tile // PACK, last_tile // PACK + 1):
+                if g not in sum_vector:
+                    sum_vector[g] = sums.tile([P, PACK, CHANNELS], F32, name="sum_vector")
+            scalar_windows = SCALAR_WINDOWS_ODD_ROW if r % 2 == 1 else SCALAR_WINDOWS_EVEN_ROW
+            for dj in range(KERNEL):
+                start = PAD + r * WIDTH + dj - REACH
+                if dj in scalar_windows:
+                    window = psum_scalar.tile([P, CHANNELS], F32, tag="scalar_bank")
+                else:
+                    window = psum_vector.tile([P, CHANNELS], F32, tag="vector_bank")
                 for k in range(CHUNKS):
-                    p_pass = psum_vector.tile([P, CHANNELS], F32, tag="vector_bank")
+                    nc.tensor.transpose(window[:, k * P : (k + 1) * P], q_chan[k][:, start : start + P], ident_f32[:])
+
+                if dj in scalar_windows:
+                    last_begun = max([i for i in range(first_tile, last_tile + 1) if begun.get(i, 0) == 2], default=-1)
+                    if last_begun >= first_tile:
+                        product = products.tile([P, PACK, CHANNELS], F32)
+                    for i in reversed(range(first_tile, last_tile + 1)):
+                        tap = (r - TILE_ROWS * (i - b * TILES) + REACH) * KERNEL + dj
+                        if i <= last_begun:
+                            target = product[:, i - first_tile, :]
+                        elif begun.get(i, 0) == 0:
+                            target = sum_vector[i // PACK][:, i % PACK, :]
+                            begun[i] = 1
+                        else:
+                            target = sum_gpsimd[:, i % RING, :]
+                            begun[i] = 2
+                        nc.scalar.activation(out=target, in_=window[:], func=FUNC.Copy, scale=taps[:, i, tap : tap + 1])
+                    for turn in range(first_tile // RING, last_begun // RING + 1):
+                        lo = max(first_tile, turn * RING)
+                        hi = min(last_begun, turn * RING + RING - 1)
+                        running = sum_gpsimd[:, lo % RING : hi % RING + 1, :]
+                        nc.gpsimd.tensor_tensor(
+                            out=running, in0=running, in1=product[:, lo - first_tile : hi - first_tile + 1, :], op=ALU.add
+                        )
+                else:
+                    for i in range(first_tile, last_tile + 1):
+                        assert begun[i] == 2
+                        tap = (r - TILE_ROWS * (i - b * TILES) + REACH) * KERNEL + dj
+                        running = sum_vector[i // PACK][:, i % PACK, :]
+                        nc.vector.scalar_tensor_tensor(
+                            out=running, in0=window[:], scalar=taps[:, i, tap : tap + 1], in1=running,
+                            op0=ALU.mult, op1=ALU.add,
+                        )
+
+        def merge(g):
+            m_rows[g] = operands.tile([P, PACK, CHANNELS], BF16, name="m_rows")
+            place = (g * PACK) % RING
+            nc.vector.tensor_tensor(
+                out=m_rows[g][:], in0=sum_vector[g][:], in1=sum_gpsimd[:, place : place + PACK, :], op=ALU.add
+            )
+
+        def regroup(g):
+            m_grouped[g] = operands.tile([P, CHANNELS, PACK], BF16, name="m_grouped", align_bytes=64)
+            nc.scalar.copy(out=m_grouped[g][:], in_=m_rows[g][:].rearrange("p t c -> p c t"))
+
+        def quantise_m(g):
+            m_words = operands.tile([P, CHANNELS], U32, align_bytes=64)
+            m_scales = operands.tile([P, CHANNELS], U8, align_bytes=64)
+            nc.vector.quantize_mx(
+                out=m_words[:].bitcast(E4M3_X4), scales=m_scales[:], in_=m_grouped[g][:].rearrange("p c t -> p (c t)")
+            )
+            m_operand[g] = (m_words, m_scales)
+
+        def multiply(last):
+            for k in range(CHUNKS):
+                p_group = psum_vector.tile([P, CHANNELS], F32, tag="vector_bank")
+                for g in range(last - GROUP + 1, last + 1):
+                    g_words, g_scales = grad_operand[g]
+                    m_words, m_scales = m_operand[g]
                     nc.tensor.matmul_mx(
-                        out=p_pass[:],
+                        out=p_group[:],
                         lhsT=g_words[:, k * P : (k + 1) * P].bitcast(E5M2_X4),
                         lhsT_scale=g_scales[:, k * P : (k + 1) * P],
                         rhs=m_words[:].bitcast(E4M3_X4),
                         rhs_scale=m_scales[:],
-                        start=True,
-                        stop=True,
+                        start=(g == last - GROUP + 1),
+                        stop=(g == last),
                     )
-                    if b == 0 and s == 0:
-                        nc.vector.tensor_copy(out=p_sum[:, k, :], in_=p_pass[:])
-                    else:
-                        nc.vector.tensor_tensor(out=p_sum[:, k, :], in0=p_pass[:], in1=p_sum[:, k, :], op=ALU.add)
+                if last == GROUP - 1:
+                    nc.vector.tensor_copy(out=p_sum[:, k, :], in_=p_group[:])
+                else:
+                    nc.vector.tensor_tensor(out=p_sum[:, k, :], in0=p_group[:], in1=p_sum[:, k, :], op=ALU.add)
+
+        rows = [(b, r) for b in range(IMAGES) for r in range(-1, HEIGHT)]
+        first_step = [rows.index((g // PASSES, (g % PASSES) * PASS_ROWS)) for g in range(IMAGES * PASSES)]
+        last_step = [
+            rows.index((g // PASSES, min(TILE_ROWS * (PACK * (g % PASSES) + PACK - 1) + REACH, HEIGHT - 1)))
+            for g in range(IMAGES * PASSES)
+        ]
+        for step in range(len(rows) + MERGE_AFTER + 5):
+            for g in range(IMAGES * PASSES):
+                before_first = first_step[g] - step
+                if before_first == 8:
+                    load_logits(g)
+                if before_first in (7, 6):
+                    exponentials(g, 2 * (7 - before_first))
+                    exponentials(g, 2 * (7 - before_first) + 1)
+                if before_first == 5:
+                    normalise(g)
+                if before_first in (4, 3):
+                    to_channels(g, 2 * (4 - before_first))
+                    to_channels(g, 2 * (4 - before_first) + 1)
+                after_last = step - last_step[g]
+                if after_last == -4:
+                    load_grad(g)
+                if after_last in (-3, -2):
+                    gather_grad(g, after_last + 3)
+                if after_last == -1:
+                    quantise_grad(g)
+                if after_last == MERGE_AFTER + 1:
+                    merge(g)
+                if after_last == MERGE_AFTER + 2:
+                    regroup(g)
+                if after_last == MERGE_AFTER + 3:
+                    quantise_m(g)
+                if after_last == MERGE_AFTER + 4 and g % GROUP == GROUP - 1:
+                    multiply(g)
+            if step == first_step[IMAGES * PASSES - 1] - 1:
+                load_compatibility()
+            if step == first_step[IMAGES * PASSES - 1]:
+                sigmoids()
+            if step == first_step[IMAGES * PASSES - 1] + 1:
+                finish_factor()
+            if step < len(rows):
+                window_row(rows[step][0], rows[step][1])
 
         for k in range(CHUNKS):
             nc.vector.tensor_tensor(out=factor[:, k, :], in0=p_sum[:, k, :], in1=factor[:, k, :], op=ALU.mult)

@@ -26,8 +26,8 @@ PASS_PIXELS = P * PACK
 PASS_ROWS = PASS_PIXELS // WIDTH
 PASSES = PIXELS // PASS_PIXELS
 PAD = 68
-SCALAR_WINDOWS_ODD_ROW = (0, 1, 3, 5)
-SCALAR_WINDOWS_EVEN_ROW = ()
+SCALAR_WINDOWS_ODD_ROW = (0, 1)
+SCALAR_WINDOWS_EVEN_ROW = (1, 3, 5)
 RING = 2 * PACK
 MERGE_AFTER = 2
 GROUP = 2
@@ -127,13 +127,13 @@ def tile_localcrf_kernel(tc, input_F, input_logit, compatibility, grad_out, out)
         with tc.tile_pool(name="setup", bufs=1) as setup:
             f_raw = setup.tile([P, IMAGES * PIXELS], BF16)
             nc.vector.memset(f_raw[:], 0.0)
+            load_logits(0)
             for b in range(IMAGES):
                 f_rows = f_raw[:, b * PIXELS : (b + 1) * PIXELS].rearrange("p (i j) -> p i j", j=WIDTH)
                 for dj in range(KERNEL):
                     lo = max(0, REACH - dj)
                     hi = WIDTH - max(0, dj - REACH)
-                    nc.scalar.dma_start(out=f_rows[dj:TAPS:KERNEL, :, lo:hi], in_=input_F[b, dj:TAPS:KERNEL, :, lo:hi])
-            load_logits(0)
+                    nc.sync.dma_start(out=f_rows[dj:TAPS:KERNEL, :, lo:hi], in_=input_F[b, dj:TAPS:KERNEL, :, lo:hi])
             for t in range(PACK):
                 exponentials(0, t)
             normalise(0)

@@ -43,6 +43,7 @@ def tile_localcrf_kernel(tc, input_F, input_logit, compatibility, grad_out, out)
     out_view = out.rearrange("(k o) c a b -> o k (c a b)", o=P)
 
     with ExitStack() as stack:
+        stack.enter_context(tc.manual_schedule())
         keep = stack.enter_context(tc.tile_pool(name="keep", bufs=1))
         slabs = stack.enter_context(tc.tile_pool(name="slabs", bufs=2))
         soft = stack.enter_context(tc.tile_pool(name="soft", bufs=6))

@@ -130,11 +130,23 @@ def tile_localcrf_kernel(tc, input_F, input_logit, compatibility, grad_out, out)
             nc.vector.memset(f_raw[:], 0.0)
             load_logits(0)
             for b in range(IMAGES):
-                f_rows = f_raw[:, b * PIXELS : (b + 1) * PIXELS].rearrange("p (i j) -> p i j", j=WIDTH)
-                for dj in range(KERNEL):
-                    lo = max(0, REACH - dj)
-                    hi = WIDTH - max(0, dj - REACH)
-                    nc.sync.dma_start(out=f_rows[dj:TAPS:KERNEL, :, lo:hi], in_=input_F[b, dj:TAPS:KERNEL, :, lo:hi])
+                nc.sync.dma_start(
+                    out=f_raw[0:TAPS, b * PIXELS : (b + 1) * PIXELS], in_=input_F[b].rearrange("p i j -> p (i j)")
+                )
+            ident_cols = ident_f32[:].rearrange("p (h j) -> p h j", j=WIDTH)
+            outside = setup.tile([P, KERNEL], F32)
+            nc.vector.memset(outside[:], 0.0)
+            for dj in range(KERNEL):
+                if dj < REACH:
+                    nc.vector.tensor_reduce(
+                        out=outside[:, dj : dj + 1], in_=ident_cols[:, :, 0 : REACH - dj], axis=AXIS.XY, op=ALU.add
+                    )
+                if dj > REACH:
+                    nc.vector.tensor_reduce(
+                        out=outside[:, dj : dj + 1], in_=ident_cols[:, :, WIDTH - (dj - REACH) : WIDTH], axis=AXIS.XY, op=ALU.add
+                    )
+            inside = setup.tile([P, KERNEL], F32)
+            nc.vector.tensor_scalar(out=inside[:], in0=outside[:], scalar1=-1.0, scalar2=1.0, op0=ALU.mult, op1=ALU.add)
             for t in range(PACK):
                 exponentials(0, t)
             normalise(0)
@@ -143,7 +155,12 @@ def tile_localcrf_kernel(tc, input_F, input_logit, compatibility, grad_out, out)
                 f_px = psum_vector.tile([P, per_bank, P], BF16, tag="vector_bank")
                 for n in range(per_bank):
                     nc.tensor.transpose(f_px[:, n, :], f_raw[:, (first + n) * P : (first + n + 1) * P], ident_bf[:])
-                nc.vector.tensor_copy(out=taps[:, first : first + per_bank, :], in_=f_px[:, :, 0:TAPS])
+                nc.vector.tensor_tensor(
+                    out=taps[:, first : first + per_bank, :].rearrange("p n (a d) -> p n a d", d=KERNEL),
+                    in0=f_px[:, :, 0:TAPS].rearrange("p n (a d) -> p n a d", d=KERNEL),
+                    in1=inside[:].unsqueeze(1).unsqueeze(1).to_broadcast([P, per_bank, KERNEL, KERNEL]),
+                    op=ALU.mult,
+                )
             for k in range(CHUNKS):
                 to_channels(0, k)
 

@@ -25,12 +25,15 @@ PACK = 4
 PASS_PIXELS = P * PACK
 PASS_ROWS = PASS_PIXELS // WIDTH
 PASSES = PIXELS // PASS_PIXELS
+HALF = CHANNELS // 2
 PAD = 68
-SCALAR_WINDOWS_ODD_ROW = (0, 1)
-SCALAR_WINDOWS_EVEN_ROW = (1, 3, 5)
-RING = 2 * PACK
-MERGE_AFTER = 2
-GROUP = 2
+AHEAD = 2
+GROUP = 4
+SCALAR_TAKES_TWO_OF_THREE = (1, 4)
+FULL = 2
+PATIENCE = 4
+ADDS = 3
+PRODUCTS = 12
 
 FLOPS = 2 * CHANNELS * CHANNELS * IMAGES * PIXELS + 2 * TAPS * CHANNELS * IMAGES * PIXELS
 
@@ -47,9 +50,10 @@ def tile_localcrf_kernel(tc, input_F, input_logit, compatibility, grad_out, out)
         keep = stack.enter_context(tc.tile_pool(name="keep", bufs=1))
         slabs = stack.enter_context(tc.tile_pool(name="slabs", bufs=2))
         soft = stack.enter_context(tc.tile_pool(name="soft", bufs=6))
-        sums = stack.enter_context(tc.tile_pool(name="sums", bufs=2))
-        psum_vector = stack.enter_context(tc.psum_pool(name="psum_vector", bufs=4))
-        psum_scalar = stack.enter_context(tc.psum_pool(name="psum_scalar", bufs=4))
+        sums = stack.enter_context(tc.tile_pool(name="sums", bufs=4))
+        psum_window = stack.enter_context(tc.psum_pool(name="psum_window", bufs=4))
+        psum_total = stack.enter_context(tc.psum_pool(name="psum_total", bufs=1))
+        psum_side = stack.enter_context(tc.psum_pool(name="psum_side", bufs=1))
 
         ident_bf = keep.tile([P, P], BF16)
         make_identity(nc, ident_bf[:])
@@ -62,9 +66,13 @@ def tile_localcrf_kernel(tc, input_F, input_logit, compatibility, grad_out, out)
             nc.vector.memset(q_chan[k][:, PAD + PIXELS :], 0.0)
 
         x_slab = {}
+        x_px = {}
+        minus_top = {}
         q_px = {}
+        q_back = {}
         total = {}
         g_slab = {}
+        g_px = {}
         g_grouped = {}
         grad_operand = {}
 
@@ -76,15 +84,19 @@ def tile_localcrf_kernel(tc, input_F, input_logit, compatibility, grad_out, out)
             nc.sync.dma_start(out=x_slab[g][:], in_=logit_view[g // PASSES][:, :, pixels_of(g)])
             total[g] = soft.tile([P, PACK], F32, name="total")
 
-        def exponentials(g, t):
-            x_px = psum_scalar.tile([P, CHANNELS], BF16, tag="scalar_bank")
+        def turn_logits(g, t, pool, tag):
+            x_px[g, t] = pool.tile([P, CHANNELS], BF16, name="x_px", tag=tag)
             for k in range(CHUNKS):
-                nc.tensor.transpose(x_px[:, k * P : (k + 1) * P], x_slab[g][:, k, t * P : (t + 1) * P], ident_bf[:])
-            minus_top = soft.tile([P, 1], F32)
-            nc.vector.reduce_max(out=minus_top[:], in_=x_px[:], axis=AXIS.X, negate=True)
+                nc.tensor.transpose(x_px[g, t][:, k * P : (k + 1) * P], x_slab[g][:, k, t * P : (t + 1) * P], ident_bf[:])
+
+        def find_top(g, t):
+            minus_top[g, t] = soft.tile([P, 1], F32, name="minus_top")
+            nc.vector.reduce_max(out=minus_top[g, t][:], in_=x_px[g, t][:], axis=AXIS.X, negate=True)
+
+        def exponentials(g, t):
             q_px[g, t] = soft.tile([P, CHANNELS], F32, name="q_px")
             nc.scalar.activation(
-                out=q_px[g, t][:], in_=x_px[:], func=FUNC.Exp, bias=minus_top[:], scale=1.0,
+                out=q_px[g, t][:], in_=x_px[g, t][:], func=FUNC.Exp, bias=minus_top[g, t][:], scale=1.0,
                 accum_out=total[g][:, t : t + 1],
             )
 
@@ -92,33 +104,42 @@ def tile_localcrf_kernel(tc, input_F, input_logit, compatibility, grad_out, out)
             inverse = soft.tile([P, PACK], F32)
             nc.vector.reciprocal(out=inverse[:], in_=total[g][:])
             for t in range(PACK):
-                nc.scalar.activation(out=q_px[g, t][:], in_=q_px[g, t][:], func=FUNC.Copy, scale=inverse[:, t : t + 1])
+                nc.gpsimd.tensor_scalar(
+                    out=q_px[g, t][:], in0=q_px[g, t][:], scalar1=inverse[:, t : t + 1], scalar2=0.0,
+                    op0=ALU.mult, op1=ALU.add,
+                )
 
-        def to_channels(g, k):
-            q_back = psum_scalar.tile([P, PASS_PIXELS], F32, tag="scalar_bank")
+        def turn_q(g, k, pool, tag):
+            q_back[g, k] = pool.tile([P, PASS_PIXELS], F32, name="q_back", tag=tag)
             for t in range(PACK):
-                nc.tensor.transpose(q_back[:, t * P : (t + 1) * P], q_px[g, t][:, k * P : (k + 1) * P], ident_f32[:])
+                nc.tensor.transpose(q_back[g, k][:, t * P : (t + 1) * P], q_px[g, t][:, k * P : (k + 1) * P], ident_f32[:])
+
+        def keep_q(g, k):
             start = PAD + (g % PASSES) * PASS_PIXELS
-            nc.scalar.copy(out=q_chan[k][:, start : start + PASS_PIXELS], in_=q_back[:])
+            nc.scalar.copy(out=q_chan[k][:, start : start + PASS_PIXELS], in_=q_back[g, k][:])
 
         def load_grad(g):
             g_slab[g] = slabs.tile([P, CHUNKS, PASS_PIXELS], BF16, name="g_slab")
             nc.sync.dma_start(out=g_slab[g][:], in_=grad_view[g // PASSES][:, :, pixels_of(g)])
             g_grouped[g] = operands.tile([P, CHANNELS, PACK], BF16, name="g_grouped", align_bytes=64)
 
-        def gather_grad(g, h):
-            half = CHANNELS // 2
-            g_px = psum_scalar.tile([P, PACK, half], BF16, tag="scalar_bank")
+        def turn_grad(g, h, tag):
+            g_px[g, h] = psum_side.tile([P, PACK, HALF], BF16, name="g_px", tag=tag)
             for t in range(PACK):
-                for k in range(half // P):
+                for k in range(HALF // P):
                     nc.tensor.transpose(
-                        g_px[:, t, k * P : (k + 1) * P], g_slab[g][:, h * (half // P) + k, t * P : (t + 1) * P], ident_bf[:]
+                        g_px[g, h][:, t, k * P : (k + 1) * P], g_slab[g][:, h * (HALF // P) + k, t * P : (t + 1) * P], ident_bf[:]
                     )
-            nc.scalar.copy(out=g_grouped[g][:, h * half : (h + 1) * half, :], in_=g_px[:].rearrange("p t o -> p o t"))
+
+        def group_grad(g, h, k):
+            first = h * HALF + k * P
+            nc.scalar.copy(
+                out=g_grouped[g][:, first : first + P, :], in_=g_px[g, h][:, :, k * P : (k + 1) * P].rearrange("p t o -> p o t")
+            )
 
         def quantise_grad(g):
-            g_words = operands.tile([P, CHANNELS], U32, align_bytes=64)
-            g_scales = operands.tile([P, CHANNELS], U8, align_bytes=64)
+            g_words = codes.tile([P, CHANNELS], U32, align_bytes=64)
+            g_scales = codes.tile([P, CHANNELS], U8, align_bytes=64)
             nc.vector.quantize_mx(
                 out=g_words[:].bitcast(E5M2_X4), scales=g_scales[:], in_=g_grouped[g][:].rearrange("p o t -> p (o t)")
             )
@@ -148,11 +169,13 @@ def tile_localcrf_kernel(tc, input_F, input_logit, compatibility, grad_out, out)
             inside = setup.tile([P, KERNEL], F32)
             nc.vector.tensor_scalar(out=inside[:], in0=outside[:], scalar1=-1.0, scalar2=1.0, op0=ALU.mult, op1=ALU.add)
             for t in range(PACK):
+                turn_logits(0, t, psum_window, "window")
+                find_top(0, t)
                 exponentials(0, t)
             normalise(0)
             per_bank = 8
             for first in range(0, IMAGES * TILES, per_bank):
-                f_px = psum_vector.tile([P, per_bank, P], BF16, tag="vector_bank")
+                f_px = psum_window.tile([P, per_bank, P], BF16, tag="window")
                 for n in range(per_bank):
                     nc.tensor.transpose(f_px[:, n, :], f_raw[:, (first + n) * P : (first + n + 1) * P], ident_bf[:])
                 nc.vector.tensor_tensor(
@@ -162,169 +185,340 @@ def tile_localcrf_kernel(tc, input_F, input_logit, compatibility, grad_out, out)
                     op=ALU.mult,
                 )
             for k in range(CHUNKS):
-                to_channels(0, k)
+                turn_q(0, k, psum_window, "window")
+                keep_q(0, k)
 
-        products = stack.enter_context(tc.tile_pool(name="products", bufs=4))
+        products = stack.enter_context(tc.tile_pool(name="products", bufs=PRODUCTS))
+        turned = stack.enter_context(tc.tile_pool(name="turned", bufs=8))
         operands = stack.enter_context(tc.tile_pool(name="operands", bufs=2))
+        codes = stack.enter_context(tc.tile_pool(name="codes", bufs=GROUP + 3))
 
         factor = keep.tile([P, CHUNKS, CHANNELS], F32)
-
-        helper = {}
-
-        def load_compatibility():
-            helper["z"] = operands.tile([P, CHUNKS, CHANNELS], BF16, name="comp_bf", tag="m_rows")
-            nc.sync.dma_start(out=helper["z"][:], in_=comp_view)
-
-        def sigmoids():
-            helper["1-s"] = products.tile([P, CHUNKS, CHANNELS], F32, name="one_minus", tag="product")
-            nc.scalar.activation(out=factor[:], in_=helper["z"][:], func=FUNC.Sigmoid, scale=100.0)
-            nc.scalar.activation(out=helper["1-s"][:], in_=helper["z"][:], func=FUNC.Sigmoid, scale=-100.0)
-
-        def finish_factor():
-            nc.vector.scalar_tensor_tensor(
-                out=factor[:], in0=factor[:], scalar=-100.0, in1=helper["1-s"][:], op0=ALU.mult, op1=ALU.mult
-            )
+        comp_bf = keep.tile([P, CHUNKS, CHANNELS], BF16)
+        one_minus = {}
 
         p_sum = keep.tile([P, CHUNKS, CHANNELS], F32)
 
-        sum_gpsimd = keep.tile([P, RING, CHANNELS], F32)
+        rows = [(b, r) for b in range(IMAGES) for r in range(-1, HEIGHT)]
+        slots = len(rows) * KERNEL
+        last_pass = IMAGES * PASSES - 1
 
-        sum_vector = {}
-        begun = {}
-        m_rows = {}
-        m_grouped = {}
-        m_operand = {}
-
-        def window_row(b, r):
+        def tiles_of(step):
+            b, r = rows[step]
             first_tile = b * TILES + max(0, (r - REACH + 1) // TILE_ROWS)
             last_tile = b * TILES + min(TILES - 1, (r + REACH) // TILE_ROWS)
-            for g in range(first_tile // PACK, last_tile // PACK + 1):
-                if g not in sum_vector:
-                    sum_vector[g] = sums.tile([P, PACK, CHANNELS], F32, name="sum_vector")
-            scalar_windows = SCALAR_WINDOWS_ODD_ROW if r % 2 == 1 else SCALAR_WINDOWS_EVEN_ROW
-            for dj in range(KERNEL):
-                start = PAD + r * WIDTH + dj - REACH
-                if dj in scalar_windows:
-                    window = psum_scalar.tile([P, CHANNELS], F32, tag="scalar_bank")
+            return [(i, r - TILE_ROWS * (i - b * TILES) + REACH) for i in range(first_tile, last_tile + 1)]
+
+        def shares(slot):
+            if not 0 <= slot < slots:
+                return [], []
+            dj = slot % KERNEL
+            served = [(i, di * KERNEL + dj) for i, di in tiles_of(slot // KERNEL)]
+            scalars = len(served) // 2
+            if len(served) % 2 == 1 and dj in SCALAR_TAKES_TWO_OF_THREE:
+                scalars += 1
+            return served[:scalars], served[scalars:]
+
+        vector_left = {}
+        parts_left = {}
+        for slot in range(slots):
+            for i, tap in shares(slot)[0]:
+                parts_left[i] = parts_left.get(i, 0) + 1
+            for i, tap in shares(slot)[1]:
+                if i not in vector_left:
+                    parts_left[i] = parts_left.get(i, 0) + 1
+                vector_left[i] = vector_left.get(i, 0) + 1
+
+        now = [-AHEAD]
+        timed = {}
+        queue = {"scalar": [], "vector": [], "urgent": []}
+        parts = []
+        chains = []
+        free_banks = ["side_a", "side_b"]
+        finale = []
+
+        def at(slot, job):
+            timed.setdefault(max(slot, -AHEAD), []).extend([job])
+
+        def after(engine, delay, job):
+            queue[engine].extend([(now[0] + delay, job)])
+
+        def chain(earliest, deadline, start):
+            chains.extend([(earliest, deadline, start)])
+
+        def release(bank):
+            free_banks.extend([bank])
+
+        def take(engine, room):
+            ripe = [entry for entry in queue[engine] if entry[0] <= now[0]]
+            if room <= 0 and ripe and ripe[0][0] + PATIENCE <= now[0]:
+                room = 1
+            for entry in ripe[: max(room, 0)]:
+                queue[engine].remove(entry)
+                entry[1]()
+
+        def start_chain():
+            ripe = [entry for entry in chains if entry[0] <= now[0]]
+            if ripe and free_banks:
+                entry = min(ripe, key=lambda e: e[1])
+                bank = free_banks[0]
+                free_banks.remove(bank)
+                chains.remove(entry)
+                entry[2](bank)
+
+        window = {}
+        sum_vector = {}
+        m_total = {}
+        total_bank = {}
+        free_totals = ["total_a", "total_b"]
+        m_turned = {}
+        m_px = {}
+        m_grouped = {}
+        m_operand = {}
+        p_group = {}
+        done = {}
+        kept = {0: CHUNKS}
+
+        def count(key, goal):
+            done[key] = done.get(key, 0) + 1
+            return done[key] == goal
+
+        def make_window(slot):
+            b, r = rows[slot // KERNEL]
+            start = PAD + r * WIDTH + slot % KERNEL - REACH
+            for g in range(b * PASSES, (b + 1) * PASSES):
+                first = PAD + (g % PASSES) * PASS_PIXELS
+                if start < first + PASS_PIXELS and first < start + P:
+                    assert kept.get(g, 0) == CHUNKS
+            window[slot] = psum_window.tile([P, CHANNELS], F32, name="window", tag="window")
+            for k in range(CHUNKS):
+                nc.tensor.transpose(window[slot][:, k * P : (k + 1) * P], q_chan[k][:, start : start + P], ident_f32[:])
+
+        def add_parts():
+            room = ADDS
+            for entry in list(parts):
+                ready, i, part = entry
+                if room == 0 or ready > now[0]:
+                    continue
+                if i not in m_total:
+                    if not free_totals:
+                        continue
+                    total_bank[i] = free_totals[0]
+                    free_totals.remove(total_bank[i])
+                    m_total[i] = psum_total.tile([P, CHUNKS, P], F32, name="m_total", tag=total_bank[i])
+                    first = True
                 else:
-                    window = psum_vector.tile([P, CHANNELS], F32, tag="vector_bank")
+                    first = False
+                parts.remove(entry)
+                room -= 1
+                parts_left[i] -= 1
                 for k in range(CHUNKS):
-                    nc.tensor.transpose(window[:, k * P : (k + 1) * P], q_chan[k][:, start : start + P], ident_f32[:])
+                    nc.tensor.matmul(
+                        m_total[i][:, k, :], lhsT=part[:, k * P : (k + 1) * P], rhs=ident_f32[:], is_transpose=True,
+                        start=(first and k == 0), stop=(parts_left[i] == 0 and k == CHUNKS - 1),
+                    )
+                if parts_left[i] == 0:
+                    after("urgent", 2, lambda i=i: round_m(i))
 
-                if dj in scalar_windows:
-                    last_begun = max([i for i in range(first_tile, last_tile + 1) if begun.get(i, 0) == 2], default=-1)
-                    if last_begun >= first_tile:
-                        product = products.tile([P, PACK, CHANNELS], F32)
-                    for i in reversed(range(first_tile, last_tile + 1)):
-                        tap = (r - TILE_ROWS * (i - b * TILES) + REACH) * KERNEL + dj
-                        if i <= last_begun:
-                            target = product[:, i - first_tile, :]
-                        elif begun.get(i, 0) == 0:
-                            target = sum_vector[i // PACK][:, i % PACK, :]
-                            begun[i] = 1
-                        else:
-                            target = sum_gpsimd[:, i % RING, :]
-                            begun[i] = 2
-                        nc.scalar.activation(out=target, in_=window[:], func=FUNC.Copy, scale=taps[:, i, tap : tap + 1])
-                    for turn in range(first_tile // RING, last_begun // RING + 1):
-                        lo = max(first_tile, turn * RING)
-                        hi = min(last_begun, turn * RING + RING - 1)
-                        running = sum_gpsimd[:, lo % RING : hi % RING + 1, :]
-                        nc.gpsimd.tensor_tensor(
-                            out=running, in0=running, in1=product[:, lo - first_tile : hi - first_tile + 1, :], op=ALU.add
-                        )
-                else:
-                    for i in range(first_tile, last_tile + 1):
-                        assert begun[i] == 2
-                        tap = (r - TILE_ROWS * (i - b * TILES) + REACH) * KERNEL + dj
-                        running = sum_vector[i // PACK][:, i % PACK, :]
-                        nc.vector.scalar_tensor_tensor(
-                            out=running, in0=window[:], scalar=taps[:, i, tap : tap + 1], in1=running,
-                            op0=ALU.mult, op1=ALU.add,
-                        )
+        def round_m(i):
+            m_turned[i] = turned.tile([P, CHUNKS, P], BF16, name="m_turned")
+            nc.scalar.copy(out=m_turned[i][:], in_=m_total[i][:])
+            free_totals.extend([total_bank[i]])
+            g = i // PACK
+            if count(("rounded", g), PACK):
+                m_grouped[g] = operands.tile([P, CHANNELS, PACK], BF16, name="m_grouped", align_bytes=64)
+                for h in range(2):
+                    chain(now[0] + 1, now[0] + 10 + h, lambda bank, h=h: m_chain(g, h, bank))
 
-        def merge(g):
-            m_rows[g] = operands.tile([P, PACK, CHANNELS], BF16, name="m_rows")
-            place = (g * PACK) % RING
-            nc.vector.tensor_tensor(
-                out=m_rows[g][:], in0=sum_vector[g][:], in1=sum_gpsimd[:, place : place + PACK, :], op=ALU.add
-            )
+        def m_chain(g, h, bank):
+            m_px[g, h] = psum_side.tile([P, PACK, HALF], BF16, name="m_px", tag=bank)
+            for t in range(PACK):
+                for k in range(HALF // P):
+                    nc.tensor.transpose(
+                        m_px[g, h][:, t, k * P : (k + 1) * P], m_turned[g * PACK + t][:, h * (HALF // P) + k, :], ident_bf[:]
+                    )
 
-        def regroup(g):
-            m_grouped[g] = operands.tile([P, CHANNELS, PACK], BF16, name="m_grouped", align_bytes=64)
-            nc.scalar.copy(out=m_grouped[g][:], in_=m_rows[g][:].rearrange("p t c -> p c t"))
+            def group(k):
+                first = h * HALF + k * P
+                nc.scalar.copy(
+                    out=m_grouped[g][:, first : first + P, :], in_=m_px[g, h][:, :, k * P : (k + 1) * P].rearrange("p t c -> p c t")
+                )
+                if k == 1:
+                    release(bank)
+                    if count(("m grouped", g), 2):
+                        after("vector", 1, lambda: quantise_m(g))
+
+            after("scalar", 1, lambda: group(0))
+            after("scalar", 1, lambda: group(1))
 
         def quantise_m(g):
-            m_words = operands.tile([P, CHANNELS], U32, align_bytes=64)
-            m_scales = operands.tile([P, CHANNELS], U8, align_bytes=64)
+            m_words = codes.tile([P, CHANNELS], U32, align_bytes=64)
+            m_scales = codes.tile([P, CHANNELS], U8, align_bytes=64)
             nc.vector.quantize_mx(
                 out=m_words[:].bitcast(E4M3_X4), scales=m_scales[:], in_=m_grouped[g][:].rearrange("p c t -> p (c t)")
             )
             m_operand[g] = (m_words, m_scales)
+            if g % GROUP == GROUP - 1 and g != last_pass:
+                for k in range(CHUNKS):
+                    chain(now[0] + 2, now[0] + 60 + k, lambda bank, k=k: early_group(g, k, bank))
 
-        def multiply(last):
-            for k in range(CHUNKS):
-                p_group = psum_vector.tile([P, CHANNELS], F32, tag="vector_bank")
-                for g in range(last - GROUP + 1, last + 1):
-                    g_words, g_scales = grad_operand[g]
-                    m_words, m_scales = m_operand[g]
-                    nc.tensor.matmul_mx(
-                        out=p_group[:],
-                        lhsT=g_words[:, k * P : (k + 1) * P].bitcast(E5M2_X4),
-                        lhsT_scale=g_scales[:, k * P : (k + 1) * P],
-                        rhs=m_words[:].bitcast(E4M3_X4),
-                        rhs_scale=m_scales[:],
-                        start=(g == last - GROUP + 1),
-                        stop=(g == last),
-                    )
+        def grad_chain(g, h, bank):
+            turn_grad(g, h, bank)
+
+            def group(k):
+                group_grad(g, h, k)
+                if k == 1:
+                    release(bank)
+                    if count(("grad grouped", g), 2):
+                        after("vector", 1, lambda: quantise_grad(g))
+
+            after("scalar", 1, lambda: group(0))
+            after("scalar", 1, lambda: group(1))
+
+        def softmax_chain(g, t, bank):
+            turn_logits(g, t, psum_side, bank)
+
+            def top():
+                find_top(g, t)
+                after("scalar", 2, finish)
+
+            def finish():
+                exponentials(g, t)
+                release(bank)
+                if count(("exp", g), PACK):
+                    after("vector", 1, divide)
+
+            def divide():
+                normalise(g)
+                for k in range(CHUNKS):
+                    chain(now[0] + 4, needed(g) - 10 + k, lambda bank, k=k: q_chain(g, k, bank))
+                if g == last_pass:
+                    for k in range(CHUNKS):
+                        after("scalar", 8, lambda k=k: sigmoid(k, 1.0))
+                        after("scalar", 8, lambda k=k: sigmoid(k, -1.0))
+
+            after("vector", 1, top)
+
+        def begin_softmax(g):
+            for t in range(PACK):
+                chain(needed(g) - 100, needed(g) - 40 + t, lambda bank, t=t: softmax_chain(g, t, bank))
+
+        def q_chain(g, k, bank):
+            turn_q(g, k, psum_side, bank)
+
+            def finish():
+                keep_q(g, k)
+                kept[g] = kept.get(g, 0) + 1
+                release(bank)
+                if kept[g] == CHUNKS and g < last_pass:
+                    begin_softmax(g + 1)
+
+            after("scalar", 1, finish)
+
+        def sigmoid(k, sign):
+            if sign > 0:
+                nc.scalar.activation(out=factor[:, k, :], in_=comp_bf[:, k, :], func=FUNC.Sigmoid, scale=100.0)
+            else:
+                one_minus[k] = sums.tile([P, CHANNELS], F32, name="one_minus")
+                nc.scalar.activation(out=one_minus[k][:], in_=comp_bf[:, k, :], func=FUNC.Sigmoid, scale=-100.0)
+                after("vector", 1, lambda: finish_factor(k))
+
+        def finish_factor(k):
+            nc.vector.scalar_tensor_tensor(
+                out=factor[:, k, :], in0=factor[:, k, :], scalar=-100.0, in1=one_minus[k][:], op0=ALU.mult, op1=ALU.mult
+            )
+
+        def multiply(bank, k, passes, start, stop):
+            for g in passes:
+                g_words, g_scales = grad_operand[g]
+                m_words, m_scales = m_operand[g]
+                nc.tensor.matmul_mx(
+                    out=bank[:],
+                    lhsT=g_words[:, k * P : (k + 1) * P].bitcast(E5M2_X4),
+                    lhsT_scale=g_scales[:, k * P : (k + 1) * P],
+                    rhs=m_words[:].bitcast(E4M3_X4),
+                    rhs_scale=m_scales[:],
+                    start=(start and g == passes[0]),
+                    stop=(stop and g == passes[-1]),
+                )
+
+        def early_group(last, k, bank):
+            p_early = psum_side.tile([P, CHANNELS], F32, tag=bank)
+            multiply(p_early, k, list(range(last - GROUP + 1, last + 1)), True, True)
+
+            def gather():
                 if last == GROUP - 1:
-                    nc.vector.tensor_copy(out=p_sum[:, k, :], in_=p_group[:])
+                    nc.vector.tensor_copy(out=p_sum[:, k, :], in_=p_early[:])
                 else:
-                    nc.vector.tensor_tensor(out=p_sum[:, k, :], in0=p_group[:], in1=p_sum[:, k, :], op=ALU.add)
+                    nc.vector.tensor_tensor(out=p_sum[:, k, :], in0=p_early[:], in1=p_sum[:, k, :], op=ALU.add)
+                release(bank)
 
-        rows = [(b, r) for b in range(IMAGES) for r in range(-1, HEIGHT)]
-        first_step = [rows.index((g // PASSES, (g % PASSES) * PASS_ROWS)) for g in range(IMAGES * PASSES)]
-        last_step = [
-            rows.index((g // PASSES, min(TILE_ROWS * (PACK * (g % PASSES) + PACK - 1) + REACH, HEIGHT - 1)))
-            for g in range(IMAGES * PASSES)
-        ]
-        for step in range(len(rows) + MERGE_AFTER + 5):
-            for g in range(IMAGES * PASSES):
-                before_first = first_step[g] - step
-                if before_first == 8:
-                    load_logits(g)
-                if before_first in (7, 6):
-                    exponentials(g, 2 * (7 - before_first))
-                    exponentials(g, 2 * (7 - before_first) + 1)
-                if before_first == 5:
-                    normalise(g)
-                if before_first in (4, 3):
-                    to_channels(g, 2 * (4 - before_first))
-                    to_channels(g, 2 * (4 - before_first) + 1)
-                after_last = step - last_step[g]
-                if after_last == -4:
-                    load_grad(g)
-                if after_last in (-3, -2):
-                    gather_grad(g, after_last + 3)
-                if after_last == -1:
-                    quantise_grad(g)
-                if after_last == MERGE_AFTER + 1:
-                    merge(g)
-                if after_last == MERGE_AFTER + 2:
-                    regroup(g)
-                if after_last == MERGE_AFTER + 3:
-                    quantise_m(g)
-                if after_last == MERGE_AFTER + 4 and g % GROUP == GROUP - 1:
-                    multiply(g)
-            if step == first_step[IMAGES * PASSES - 1] - 1:
-                load_compatibility()
-            if step == first_step[IMAGES * PASSES - 1]:
-                sigmoids()
-            if step == first_step[IMAGES * PASSES - 1] + 1:
-                finish_factor()
-            if step < len(rows):
-                window_row(rows[step][0], rows[step][1])
+            after("vector", 1, gather)
 
-        for k in range(CHUNKS):
+        def open_last_group(k):
+            p_group[k] = psum_window.tile([P, CHANNELS], F32, name="p_group", tag="window")
+            multiply(p_group[k], k, list(range(last_pass - GROUP + 1, last_pass)), True, False)
+
+        def close_last_group(k):
+            multiply(p_group[k], k, [last_pass], False, True)
+            nc.vector.tensor_tensor(out=p_sum[:, k, :], in0=p_group[k][:], in1=p_sum[:, k, :], op=ALU.add)
             nc.vector.tensor_tensor(out=factor[:, k, :], in0=p_sum[:, k, :], in1=factor[:, k, :], op=ALU.mult)
             nc.sync.dma_start(out=out_view[:, k, :], in_=factor[:, k, :])
+
+        def use_window(slot):
+            scalars, vectors = shares(slot)
+            for i, tap in scalars:
+                product = products.tile([P, CHANNELS], F32)
+                nc.scalar.activation(out=product[:], in_=window[slot][:], func=FUNC.Copy, scale=taps[:, i, tap : tap + 1])
+                parts.extend([(slot + 1, i, product)])
+            for i, tap in vectors:
+                if i not in sum_vector:
+                    sum_vector[i] = sums.tile([P, CHANNELS], F32, name="sum_vector")
+                    nc.vector.tensor_scalar_mul(out=sum_vector[i][:], in0=window[slot][:], scalar1=taps[:, i, tap : tap + 1])
+                else:
+                    nc.vector.scalar_tensor_tensor(
+                        out=sum_vector[i][:], in0=window[slot][:], scalar=taps[:, i, tap : tap + 1], in1=sum_vector[i][:],
+                        op0=ALU.mult, op1=ALU.add,
+                    )
+                vector_left[i] -= 1
+                if vector_left[i] == 0:
+                    parts.extend([(slot + 3, i, sum_vector[i])])
+
+        def needed(g):
+            first_step = rows.index((g // PASSES, (g % PASSES) * PASS_ROWS))
+            return KERNEL * (first_step - 2) - AHEAD
+
+        for g in range(IMAGES * PASSES):
+            last_step = rows.index((g // PASSES, min(TILE_ROWS * (PACK * (g % PASSES) + PACK - 1) + REACH, HEIGHT - 1)))
+            if g > 0:
+                at(needed(g) - 115, lambda g=g: load_logits(g))
+            at(KERNEL * last_step - 75, lambda g=g: load_grad(g))
+            for h in range(2):
+                chain(KERNEL * last_step - 60, KERNEL * last_step + h, lambda bank, g=g, h=h: grad_chain(g, h, bank))
+        begin_softmax(1)
+        at(needed(last_pass) - 115, lambda: nc.sync.dma_start(out=comp_bf[:], in_=comp_view))
+        for k in range(CHUNKS):
+            finale.extend([(lambda: last_pass - 1 in m_operand and last_pass - 1 in grad_operand, lambda k=k: open_last_group(k))])
+        for k in range(CHUNKS):
+            finale.extend([(lambda: last_pass in m_operand and last_pass in grad_operand, lambda k=k: close_last_group(k))])
+
+        for slot in range(-AHEAD, slots + 60):
+            now[0] = slot
+            if slot + AHEAD < slots:
+                make_window(slot + AHEAD)
+            for job in timed.get(slot, []):
+                job()
+            add_parts()
+            assert len(parts) <= PRODUCTS - 4
+            start_chain()
+            if slot >= slots and finale and finale[0][0]():
+                job = finale[0]
+                finale.remove(job)
+                job[1]()
+            scalars, vectors = shares(slot)
+            take("urgent", FULL)
+            take("scalar", FULL - len(scalars))
+            take("vector", FULL - len(vectors))
+            if 0 <= slot < slots:
+                use_window(slot)
+        assert not (parts or chains or finale or queue["scalar"] or queue["vector"] or queue["urgent"])

@@ -27,15 +27,25 @@ PASS_ROWS = PASS_PIXELS // WIDTH
 PASSES = PIXELS // PASS_PIXELS
 HALF = CHANNELS // 2
 PAD = 68
-AHEAD = 2
+AHEAD = 1
 GROUP = 4
-SCALAR_TAKES_TWO_OF_THREE = (1, 4)
-FULL = 2
-PATIENCE = 4
-ADDS = 3
-PRODUCTS = 12
+SCALAR_TAKES_TWO = (3,)
+FULL = 3
+PATIENCE = 0
+ADDS = 6
+PRODUCTS = 8
+STRAIGHT = 3
+GPSIMD_TAKES = (2, 3, 2, 3, 2, 3, 2)
+Q_TILES = 12
+LEAD = 40
 
 FLOPS = 2 * CHANNELS * CHANNELS * IMAGES * PIXELS + 2 * TAPS * CHANNELS * IMAGES * PIXELS
+
+
+def column(di, dj):
+    if di % 2 == 0:
+        return (di // 2) * KERNEL + dj
+    return (KERNEL // 2 + 1) * KERNEL + (KERNEL // 2) * dj + di // 2
 
 
 def tile_localcrf_kernel(tc, input_F, input_logit, compatibility, grad_out, out):
@@ -49,16 +59,18 @@ def tile_localcrf_kernel(tc, input_F, input_logit, compatibility, grad_out, out)
         stack.enter_context(tc.manual_schedule())
         keep = stack.enter_context(tc.tile_pool(name="keep", bufs=1))
         slabs = stack.enter_context(tc.tile_pool(name="slabs", bufs=2))
-        soft = stack.enter_context(tc.tile_pool(name="soft", bufs=6))
+        soft = stack.enter_context(tc.tile_pool(name="soft", bufs=Q_TILES))
         sums = stack.enter_context(tc.tile_pool(name="sums", bufs=4))
-        psum_window = stack.enter_context(tc.psum_pool(name="psum_window", bufs=4))
+        psum_window = stack.enter_context(tc.psum_pool(name="psum_window", bufs=3))
         psum_total = stack.enter_context(tc.psum_pool(name="psum_total", bufs=1))
         psum_side = stack.enter_context(tc.psum_pool(name="psum_side", bufs=1))
 
         ident_bf = keep.tile([P, P], BF16)
         make_identity(nc, ident_bf[:])
-        ident_f32 = keep.tile([P, P], F32)
-        make_identity(nc, ident_f32[:])
+        twice = keep.tile([P, 2 * P], F32)
+        make_identity(nc, twice[:, 0:P])
+        nc.vector.tensor_copy(out=twice[:, P : 2 * P], in_=twice[:, 0:P])
+        ident_f32 = twice[:, 0:P]
 
         q_chan = [keep.tile([P, PAD + PIXELS + PAD], F32, name="q_chan%d" % k) for k in range(CHUNKS)]
         for k in range(CHUNKS):
@@ -112,7 +124,7 @@ def tile_localcrf_kernel(tc, input_F, input_logit, compatibility, grad_out, out)
         def turn_q(g, k, pool, tag):
             q_back[g, k] = pool.tile([P, PASS_PIXELS], F32, name="q_back", tag=tag)
             for t in range(PACK):
-                nc.tensor.transpose(q_back[g, k][:, t * P : (t + 1) * P], q_px[g, t][:, k * P : (k + 1) * P], ident_f32[:])
+                nc.tensor.transpose(q_back[g, k][:, t * P : (t + 1) * P], q_px[g, t][:, k * P : (k + 1) * P], ident_f32)
 
         def keep_q(g, k):
             start = PAD + (g % PASSES) * PASS_PIXELS
@@ -146,60 +158,82 @@ def tile_localcrf_kernel(tc, input_F, input_logit, compatibility, grad_out, out)
             grad_operand[g] = (g_words, g_scales)
 
         taps = keep.tile([P, IMAGES * TILES, TAPS], F32)
+        factor = keep.tile([P, CHUNKS, CHANNELS], F32)
+        p_sum = keep.tile([P, CHUNKS, CHANNELS], F32)
         with tc.tile_pool(name="setup", bufs=1) as setup:
             f_raw = setup.tile([P, IMAGES * PIXELS], BF16)
             nc.vector.memset(f_raw[:], 0.0)
+            comp_bf = setup.tile([P, CHUNKS, CHANNELS], BF16)
             load_logits(0)
+            nc.sync.dma_start(out=comp_bf[:], in_=comp_view)
             for b in range(IMAGES):
-                nc.sync.dma_start(
-                    out=f_raw[0:TAPS, b * PIXELS : (b + 1) * PIXELS], in_=input_F[b].rearrange("p i j -> p (i j)")
-                )
-            ident_cols = ident_f32[:].rearrange("p (h j) -> p h j", j=WIDTH)
-            outside = setup.tile([P, KERNEL], F32)
+                for di in range(0, KERNEL, 2):
+                    nc.sync.dma_start(
+                        out=f_raw[column(di, 0) : column(di, 0) + KERNEL, b * PIXELS : (b + 1) * PIXELS],
+                        in_=input_F[b, di * KERNEL : (di + 1) * KERNEL].rearrange("p i j -> p (i j)"),
+                    )
+                odd_rows = input_F[b, KERNEL:TAPS].rearrange("(a q) i j -> a (q i j)", q=2 * KERNEL)
+                for dj in range(KERNEL):
+                    shift = dj - REACH
+                    early = shift % 2 if shift > 0 else 0
+                    target = max(shift, 0) - early
+                    source = dj * PIXELS + max(-shift, 0) - early
+                    length = PIXELS - abs(shift) + early
+                    nc.sync.dma_start(
+                        out=f_raw[column(1, dj) : column(1, dj) + KERNEL // 2, b * PIXELS + target : b * PIXELS + target + length],
+                        in_=odd_rows[:, source : source + length],
+                    )
+            ident_cols = ident_f32.rearrange("p (h j) -> p h j", j=WIDTH)
+            outside = setup.tile([P, 2, KERNEL], F32)
             nc.vector.memset(outside[:], 0.0)
             for dj in range(KERNEL):
-                if dj < REACH:
+                reach = abs(dj - REACH)
+                if reach > 0:
+                    left, right = ident_cols[:, :, 0:reach], ident_cols[:, :, WIDTH - reach : WIDTH]
                     nc.vector.tensor_reduce(
-                        out=outside[:, dj : dj + 1], in_=ident_cols[:, :, 0 : REACH - dj], axis=AXIS.XY, op=ALU.add
+                        out=outside[:, 0, dj : dj + 1], in_=(left if dj < REACH else right), axis=AXIS.XY, op=ALU.add
                     )
-                if dj > REACH:
                     nc.vector.tensor_reduce(
-                        out=outside[:, dj : dj + 1], in_=ident_cols[:, :, WIDTH - (dj - REACH) : WIDTH], axis=AXIS.XY, op=ALU.add
+                        out=outside[:, 1, dj : dj + 1], in_=(right if dj < REACH else left), axis=AXIS.XY, op=ALU.add
                     )
-            inside = setup.tile([P, KERNEL], F32)
+            inside = setup.tile([P, 2, KERNEL], F32)
             nc.vector.tensor_scalar(out=inside[:], in0=outside[:], scalar1=-1.0, scalar2=1.0, op0=ALU.mult, op1=ALU.add)
+            mask = setup.tile([P, TAPS], F32)
+            nc.vector.tensor_copy(
+                out=mask[:, 0 : column(1, 0)].rearrange("p (a d) -> p a d", d=KERNEL),
+                in_=inside[:, 0, :].unsqueeze(1).to_broadcast([P, KERNEL // 2 + 1, KERNEL]),
+            )
+            nc.vector.tensor_copy(
+                out=mask[:, column(1, 0) : TAPS].rearrange("p (d a) -> p d a", a=KERNEL // 2),
+                in_=inside[:, 1, :].unsqueeze(2).to_broadcast([P, KERNEL, KERNEL // 2]),
+            )
             for t in range(PACK):
                 turn_logits(0, t, psum_window, "window")
                 find_top(0, t)
                 exponentials(0, t)
             normalise(0)
+            nc.scalar.activation(out=factor[:], in_=comp_bf[:], func=FUNC.Sigmoid, scale=100.0)
+            nc.scalar.activation(out=p_sum[:], in_=comp_bf[:], func=FUNC.Sigmoid, scale=-100.0)
             per_bank = 8
             for first in range(0, IMAGES * TILES, per_bank):
                 f_px = psum_window.tile([P, per_bank, P], BF16, tag="window")
                 for n in range(per_bank):
                     nc.tensor.transpose(f_px[:, n, :], f_raw[:, (first + n) * P : (first + n + 1) * P], ident_bf[:])
                 nc.vector.tensor_tensor(
-                    out=taps[:, first : first + per_bank, :].rearrange("p n (a d) -> p n a d", d=KERNEL),
-                    in0=f_px[:, :, 0:TAPS].rearrange("p n (a d) -> p n a d", d=KERNEL),
-                    in1=inside[:].unsqueeze(1).unsqueeze(1).to_broadcast([P, per_bank, KERNEL, KERNEL]),
-                    op=ALU.mult,
+                    out=taps[:, first : first + per_bank, :], in0=f_px[:, :, 0:TAPS],
+                    in1=mask[:].unsqueeze(1).to_broadcast([P, per_bank, TAPS]), op=ALU.mult,
                 )
             for k in range(CHUNKS):
                 turn_q(0, k, psum_window, "window")
                 keep_q(0, k)
+            nc.vector.scalar_tensor_tensor(out=factor[:], in0=factor[:], scalar=-100.0, in1=p_sum[:], op0=ALU.mult, op1=ALU.mult)
 
         products = stack.enter_context(tc.tile_pool(name="products", bufs=PRODUCTS))
-        turned = stack.enter_context(tc.tile_pool(name="turned", bufs=8))
+        turned = stack.enter_context(tc.tile_pool(name="turned", bufs=6))
         operands = stack.enter_context(tc.tile_pool(name="operands", bufs=2))
-        codes = stack.enter_context(tc.tile_pool(name="codes", bufs=GROUP + 3))
+        codes = stack.enter_context(tc.tile_pool(name="codes", bufs=GROUP + 2))
 
-        factor = keep.tile([P, CHUNKS, CHANNELS], F32)
-        comp_bf = keep.tile([P, CHUNKS, CHANNELS], BF16)
-        one_minus = {}
-
-        p_sum = keep.tile([P, CHUNKS, CHANNELS], F32)
-
-        rows = [(b, r) for b in range(IMAGES) for r in range(-1, HEIGHT)]
+        rows = [(b, r) for b in range(IMAGES) for r in range(-1, HEIGHT, TILE_ROWS)]
         slots = len(rows) * KERNEL
         last_pass = IMAGES * PASSES - 1
 
@@ -213,11 +247,21 @@ def tile_localcrf_kernel(tc, input_F, input_logit, compatibility, grad_out, out)
             if not 0 <= slot < slots:
                 return [], []
             dj = slot % KERNEL
-            served = [(i, di * KERNEL + dj) for i, di in tiles_of(slot // KERNEL)]
-            scalars = len(served) // 2
-            if len(served) % 2 == 1 and dj in SCALAR_TAKES_TWO_OF_THREE:
-                scalars += 1
+            served = [(i, column(di, dj)) for i, di in tiles_of(slot // KERNEL)]
+            scalars = 2 if len(served) == PACK and dj in SCALAR_TAKES_TWO else 1
             return served[:scalars], served[scalars:]
+
+        def straight(slot):
+            if not 0 <= slot < slots:
+                return []
+            b, r = rows[slot // KERNEL]
+            i = (r + 1) // TILE_ROWS - 1
+            dj = slot % KERNEL
+            return [
+                (b * TILES + i, b * TILES + i + (di - REACH) // 2, column(di, dj), (dj - REACH) % P)
+                for di in range(1, KERNEL, 2)
+                if i >= 0 and 0 <= i + (di - REACH) // 2 < TILES
+            ]
 
         vector_left = {}
         parts_left = {}
@@ -228,6 +272,8 @@ def tile_localcrf_kernel(tc, input_F, input_logit, compatibility, grad_out, out)
                 if i not in vector_left:
                     parts_left[i] = parts_left.get(i, 0) + 1
                 vector_left[i] = vector_left.get(i, 0) + 1
+            for i, u, tap, shift in straight(slot):
+                parts_left[i] = parts_left.get(i, 0) + 1
 
         now = [-AHEAD]
         timed = {}
@@ -270,7 +316,7 @@ def tile_localcrf_kernel(tc, input_F, input_logit, compatibility, grad_out, out)
         sum_vector = {}
         m_total = {}
         total_bank = {}
-        free_totals = ["total_a", "total_b"]
+        free_totals = ["total_a", "total_b", "total_c"]
         m_turned = {}
         m_px = {}
         m_grouped = {}
@@ -292,12 +338,12 @@ def tile_localcrf_kernel(tc, input_F, input_logit, compatibility, grad_out, out)
                     assert kept.get(g, 0) == CHUNKS
             window[slot] = psum_window.tile([P, CHANNELS], F32, name="window", tag="window")
             for k in range(CHUNKS):
-                nc.tensor.transpose(window[slot][:, k * P : (k + 1) * P], q_chan[k][:, start : start + P], ident_f32[:])
+                nc.tensor.transpose(window[slot][:, k * P : (k + 1) * P], q_chan[k][:, start : start + P], ident_f32)
 
         def add_parts():
             room = ADDS
             for entry in list(parts):
-                ready, i, part = entry
+                ready, i, part, shift = entry
                 if room == 0 or ready > now[0]:
                     continue
                 if i not in m_total:
@@ -314,7 +360,7 @@ def tile_localcrf_kernel(tc, input_F, input_logit, compatibility, grad_out, out)
                 parts_left[i] -= 1
                 for k in range(CHUNKS):
                     nc.tensor.matmul(
-                        m_total[i][:, k, :], lhsT=part[:, k * P : (k + 1) * P], rhs=ident_f32[:], is_transpose=True,
+                        m_total[i][:, k, :], lhsT=part[:, k * P : (k + 1) * P], rhs=twice[:, shift : shift + P], is_transpose=True,
                         start=(first and k == 0), stop=(parts_left[i] == 0 and k == CHUNKS - 1),
                     )
                 if parts_left[i] == 0:
@@ -332,6 +378,7 @@ def tile_localcrf_kernel(tc, input_F, input_logit, compatibility, grad_out, out)
 
         def m_chain(g, h, bank):
             m_px[g, h] = psum_side.tile([P, PACK, HALF], BF16, name="m_px", tag=bank)
+            count(("m turned", g), 2)
             for t in range(PACK):
                 for k in range(HALF // P):
                     nc.tensor.transpose(
@@ -346,7 +393,7 @@ def tile_localcrf_kernel(tc, input_F, input_logit, compatibility, grad_out, out)
                 if k == 1:
                     release(bank)
                     if count(("m grouped", g), 2):
-                        after("vector", 1, lambda: quantise_m(g))
+                        after("vector", 3, lambda: quantise_m(g))
 
             after("scalar", 1, lambda: group(0))
             after("scalar", 1, lambda: group(1))
@@ -360,7 +407,7 @@ def tile_localcrf_kernel(tc, input_F, input_logit, compatibility, grad_out, out)
             m_operand[g] = (m_words, m_scales)
             if g % GROUP == GROUP - 1 and g != last_pass:
                 for k in range(CHUNKS):
-                    chain(now[0] + 2, now[0] + 60 + k, lambda bank, k=k: early_group(g, k, bank))
+                    chain(now[0] + 2, now[0] + 30 + k, lambda bank, k=k: early_group(g, k, bank))
 
         def grad_chain(g, h, bank):
             turn_grad(g, h, bank)
@@ -370,7 +417,7 @@ def tile_localcrf_kernel(tc, input_F, input_logit, compatibility, grad_out, out)
                 if k == 1:
                     release(bank)
                     if count(("grad grouped", g), 2):
-                        after("vector", 1, lambda: quantise_grad(g))
+                        after("vector", 3, lambda: quantise_grad(g))
 
             after("scalar", 1, lambda: group(0))
             after("scalar", 1, lambda: group(1))
@@ -391,17 +438,9 @@ def tile_localcrf_kernel(tc, input_F, input_logit, compatibility, grad_out, out)
             def divide():
                 normalise(g)
                 for k in range(CHUNKS):
-                    chain(now[0] + 4, needed(g) - 10 + k, lambda bank, k=k: q_chain(g, k, bank))
-                if g == last_pass:
-                    for k in range(CHUNKS):
-                        after("scalar", 8, lambda k=k: sigmoid(k, 1.0))
-                        after("scalar", 8, lambda k=k: sigmoid(k, -1.0))
+                    chain(now[0] + 2, needed(g) - 4 + k, lambda bank, k=k: q_chain(g, k, bank))
 
-            after("vector", 1, top)
-
-        def begin_softmax(g):
-            for t in range(PACK):
-                chain(needed(g) - 100, needed(g) - 40 + t, lambda bank, t=t: softmax_chain(g, t, bank))
+            after("vector", 2, top)
 
         def q_chain(g, k, bank):
             turn_q(g, k, psum_side, bank)
@@ -410,23 +449,8 @@ def tile_localcrf_kernel(tc, input_F, input_logit, compatibility, grad_out, out)
                 keep_q(g, k)
                 kept[g] = kept.get(g, 0) + 1
                 release(bank)
-                if kept[g] == CHUNKS and g < last_pass:
-                    begin_softmax(g + 1)
 
             after("scalar", 1, finish)
-
-        def sigmoid(k, sign):
-            if sign > 0:
-                nc.scalar.activation(out=factor[:, k, :], in_=comp_bf[:, k, :], func=FUNC.Sigmoid, scale=100.0)
-            else:
-                one_minus[k] = sums.tile([P, CHANNELS], F32, name="one_minus")
-                nc.scalar.activation(out=one_minus[k][:], in_=comp_bf[:, k, :], func=FUNC.Sigmoid, scale=-100.0)
-                after("vector", 1, lambda: finish_factor(k))
-
-        def finish_factor(k):
-            nc.vector.scalar_tensor_tensor(
-                out=factor[:, k, :], in0=factor[:, k, :], scalar=-100.0, in1=one_minus[k][:], op0=ALU.mult, op1=ALU.mult
-            )
 
         def multiply(bank, k, passes, start, stop):
             for g in passes:
@@ -453,10 +477,14 @@ def tile_localcrf_kernel(tc, input_F, input_logit, compatibility, grad_out, out)
                     nc.vector.tensor_tensor(out=p_sum[:, k, :], in0=p_early[:], in1=p_sum[:, k, :], op=ALU.add)
                 release(bank)
 
-            after("vector", 1, gather)
+            after("vector", 3, gather)
 
         def open_last_group(k):
-            p_group[k] = psum_window.tile([P, CHANNELS], F32, name="p_group", tag="window")
+            if k < CHUNKS - 1:
+                p_group[k] = psum_window.tile([P, CHANNELS], F32, name="p_group", tag="window")
+            else:
+                p_group[k] = psum_total.tile([P, CHANNELS], F32, name="p_group", tag=free_totals[0])
+                free_totals.remove(free_totals[0])
             multiply(p_group[k], k, list(range(last_pass - GROUP + 1, last_pass)), True, False)
 
         def close_last_group(k):
@@ -467,10 +495,6 @@ def tile_localcrf_kernel(tc, input_F, input_logit, compatibility, grad_out, out)
 
         def use_window(slot):
             scalars, vectors = shares(slot)
-            for i, tap in scalars:
-                product = products.tile([P, CHANNELS], F32)
-                nc.scalar.activation(out=product[:], in_=window[slot][:], func=FUNC.Copy, scale=taps[:, i, tap : tap + 1])
-                parts.extend([(slot + 1, i, product)])
             for i, tap in vectors:
                 if i not in sum_vector:
                     sum_vector[i] = sums.tile([P, CHANNELS], F32, name="sum_vector")
@@ -482,23 +506,44 @@ def tile_localcrf_kernel(tc, input_F, input_logit, compatibility, grad_out, out)
                     )
                 vector_left[i] -= 1
                 if vector_left[i] == 0:
-                    parts.extend([(slot + 3, i, sum_vector[i])])
+                    parts.extend([(slot + 2, i, sum_vector[i], 0)])
+            for i, tap in scalars:
+                product = products.tile([P, CHANNELS], F32)
+                nc.scalar.activation(out=product[:], in_=window[slot][:], func=FUNC.Copy, scale=taps[:, i, tap : tap + 1])
+                parts.extend([(slot + 2, i, product, 0)])
+            for n, (i, u, tap, shift) in enumerate(straight(slot)):
+                source = q_px[u // PACK, u % PACK]
+                if n < GPSIMD_TAKES[slot % KERNEL]:
+                    product_g = products.tile([P, CHANNELS], F32)
+                    nc.gpsimd.tensor_scalar(
+                        out=product_g[:], in0=source[:], scalar1=taps[:, i, tap : tap + 1], scalar2=0.0, op0=ALU.mult, op1=ALU.add
+                    )
+                    parts.extend([(slot + 2, i, product_g, shift)])
+                else:
+                    product = products.tile([P, CHANNELS], F32)
+                    nc.scalar.activation(out=product[:], in_=source[:], func=FUNC.Copy, scale=taps[:, i, tap : tap + 1])
+                    parts.extend([(slot + 1, i, product, shift)])
 
         def needed(g):
-            first_step = rows.index((g // PASSES, (g % PASSES) * PASS_ROWS))
-            return KERNEL * (first_step - 2) - AHEAD
+            return KERNEL * rows.index((g // PASSES, (g % PASSES) * PASS_ROWS - 1)) - AHEAD
 
+        last_reader = {}
+        for slot in range(slots):
+            for i, u, tap, shift in straight(slot):
+                last_reader[u] = slot
         for g in range(IMAGES * PASSES):
             last_step = rows.index((g // PASSES, min(TILE_ROWS * (PACK * (g % PASSES) + PACK - 1) + REACH, HEIGHT - 1)))
             if g > 0:
-                at(needed(g) - 115, lambda g=g: load_logits(g))
-            at(KERNEL * last_step - 75, lambda g=g: load_grad(g))
+                at(needed(g) - LEAD - 8, lambda g=g: load_logits(g))
+                for t in range(PACK):
+                    earliest = max(needed(g) - LEAD, last_reader.get(g * PACK + t - Q_TILES, 0) + 1)
+                    chain(earliest, needed(g) - 16 + t, lambda bank, g=g, t=t: softmax_chain(g, t, bank))
+            at(KERNEL * last_step - 40, lambda g=g: load_grad(g))
             for h in range(2):
-                chain(KERNEL * last_step - 60, KERNEL * last_step + h, lambda bank, g=g, h=h: grad_chain(g, h, bank))
-        begin_softmax(1)
-        at(needed(last_pass) - 115, lambda: nc.sync.dma_start(out=comp_bf[:], in_=comp_view))
-        for k in range(CHUNKS):
-            finale.extend([(lambda: last_pass - 1 in m_operand and last_pass - 1 in grad_operand, lambda k=k: open_last_group(k))])
+                chain(KERNEL * last_step - 30, KERNEL * last_step + h, lambda bank, g=g, h=h: grad_chain(g, h, bank))
+        finale.extend([(lambda: not parts, lambda: open_last_group(0))])
+        for k in range(1, CHUNKS):
+            finale.extend([(lambda: done.get(("m turned", last_pass), 0) == 2, lambda k=k: open_last_group(k))])
         for k in range(CHUNKS):
             finale.extend([(lambda: last_pass in m_operand and last_pass in grad_operand, lambda k=k: close_last_group(k))])
 
@@ -509,7 +554,7 @@ def tile_localcrf_kernel(tc, input_F, input_logit, compatibility, grad_out, out)
             for job in timed.get(slot, []):
                 job()
             add_parts()
-            assert len(parts) <= PRODUCTS - 4
+            assert len(parts) <= 2 * PRODUCTS - 8
             start_chain()
             if slot >= slots and finale and finale[0][0]():
                 job = finale[0]
@@ -517,7 +562,7 @@ def tile_localcrf_kernel(tc, input_F, input_logit, compatibility, grad_out, out)
                 job[1]()
             scalars, vectors = shares(slot)
             take("urgent", FULL)
-            take("scalar", FULL - len(scalars))
+            take("scalar", FULL - len(scalars) - max(len(straight(slot)) - GPSIMD_TAKES[slot % KERNEL], 0))
             take("vector", FULL - len(vectors))
             if 0 <= slot < slots:
                 use_window(slot)

@@ -35,7 +35,7 @@ PATIENCE = 0
 ADDS = 6
 PRODUCTS = 8
 STRAIGHT = 3
-GPSIMD_TAKES = (2, 3, 2, 3, 2, 3, 2)
+GPSIMD_TAKES = (2, 2, 2, 2, 2, 1, 2)
 Q_TILES = 12
 LEAD = 40
 

@@ -16,54 +16,45 @@ AXIS = mybir.AxisListType
 P = 128
 IMAGES, CHANNELS, HEIGHT, WIDTH, KERNEL = 2, 512, 64, 64, 7
 REACH = KERNEL // 2
-TAPS = KERNEL * KERNEL
-PIXELS = HEIGHT * WIDTH
 CHUNKS = CHANNELS // P
-TILE_ROWS = P // WIDTH
-TILES = PIXELS // P
 PACK = 4
-PASS_PIXELS = P * PACK
-PASS_ROWS = PASS_PIXELS // WIDTH
-PASSES = PIXELS // PASS_PIXELS
+PASSES = HEIGHT // PACK
 HALF = CHANNELS // 2
-PAD = 68
-AHEAD = 1
+PAIRS = (KERNEL + 1) // 2
+PAD = 4
+SLOTS = 7
 GROUP = 4
-SCALAR_TAKES_TWO = (3,)
-FULL = 3
-PATIENCE = 0
+VECTOR_COLUMNS = (2, 3, 4)
+VECTOR_LEAVES = ((6, 4),)
+SCALAR_ROOM = 3
+GPSIMD_ROOM = 2
 ADDS = 6
+EARLY = 3
+Q_TILES = 11
+SUMS = 9
 PRODUCTS = 8
-STRAIGHT = 3
-GPSIMD_TAKES = (2, 2, 2, 2, 2, 1, 2)
-Q_TILES = 12
-LEAD = 40
+RING = 3
 
-FLOPS = 2 * CHANNELS * CHANNELS * IMAGES * PIXELS + 2 * TAPS * CHANNELS * IMAGES * PIXELS
-
-
-def column(di, dj):
-    if di % 2 == 0:
-        return (di // 2) * KERNEL + dj
-    return (KERNEL // 2 + 1) * KERNEL + (KERNEL // 2) * dj + di // 2
+FLOPS = 2 * CHANNELS * CHANNELS * IMAGES * HEIGHT * WIDTH + 2 * KERNEL * KERNEL * CHANNELS * IMAGES * HEIGHT * WIDTH
 
 
 def tile_localcrf_kernel(tc, input_F, input_logit, compatibility, grad_out, out):
     nc = tc.nc
-    logit_view = input_logit.rearrange("b (k c) i j -> b c k (i j)", c=P)
-    grad_view = grad_out.rearrange("b (k o) i j -> b o k (i j)", o=P)
     comp_view = compatibility.rearrange("(k o) c a b -> o k (c a b)", o=P)
     out_view = out.rearrange("(k o) c a b -> o k (c a b)", o=P)
 
     with ExitStack() as stack:
         stack.enter_context(tc.manual_schedule())
         keep = stack.enter_context(tc.tile_pool(name="keep", bufs=1))
-        slabs = stack.enter_context(tc.tile_pool(name="slabs", bufs=2))
+        slabs = stack.enter_context(tc.tile_pool(name="slabs", bufs=3))
         soft = stack.enter_context(tc.tile_pool(name="soft", bufs=Q_TILES))
-        sums = stack.enter_context(tc.tile_pool(name="sums", bufs=4))
-        psum_window = stack.enter_context(tc.psum_pool(name="psum_window", bufs=3))
-        psum_total = stack.enter_context(tc.psum_pool(name="psum_total", bufs=1))
-        psum_side = stack.enter_context(tc.psum_pool(name="psum_side", bufs=1))
+        stats = stack.enter_context(tc.tile_pool(name="stats", bufs=6))
+        sums = stack.enter_context(tc.tile_pool(name="sums", bufs=SUMS))
+        products = stack.enter_context(tc.tile_pool(name="products", bufs=PRODUCTS))
+        turned = stack.enter_context(tc.tile_pool(name="turned", bufs=2))
+        operands = stack.enter_context(tc.tile_pool(name="operands", bufs=2))
+        codes = stack.enter_context(tc.tile_pool(name="codes", bufs=GROUP + 2))
+        psum = stack.enter_context(tc.psum_pool(name="psum", bufs=1))
 
         ident_bf = keep.tile([P, P], BF16)
         make_identity(nc, ident_bf[:])
@@ -71,274 +62,182 @@ def tile_localcrf_kernel(tc, input_F, input_logit, compatibility, grad_out, out)
         make_identity(nc, twice[:, 0:P])
         nc.vector.tensor_copy(out=twice[:, P : 2 * P], in_=twice[:, 0:P])
         ident_f32 = twice[:, 0:P]
+        warm = keep.tile([P, 1], F32)
+        nc.scalar.activation(out=warm[:], in_=twice[:, 0:1], func=FUNC.Exp)
 
-        q_chan = [keep.tile([P, PAD + PIXELS + PAD], F32, name="q_chan%d" % k) for k in range(CHUNKS)]
-        for k in range(CHUNKS):
-            nc.vector.memset(q_chan[k][:, 0:PAD], 0.0)
-            nc.vector.memset(q_chan[k][:, PAD + PIXELS :], 0.0)
+        q_ring = [keep.tile([P, CHUNKS, PAD + P + PAD], F32, name="q_ring%d" % n) for n in range(RING)]
+        for n in range(RING):
+            nc.vector.memset(q_ring[n][:], 0.0)
+
+        tables = [("target", dj) for dj in VECTOR_COLUMNS]
+        for dj in range(KERNEL):
+            if dj not in VECTOR_COLUMNS or [tap for tap in VECTOR_LEAVES if tap[1] == dj]:
+                tables.extend([("source", dj)])
+        taps = keep.tile([P, len(tables), PAIRS, P], F32)
+
+        def weight(kind, di, dj, i):
+            n = tables.index((kind, dj))
+            return taps[:, n, di // 2, WIDTH * (di % 2) + i : WIDTH * (di % 2) + i + 1]
+
+        factor = keep.tile([P, CHUNKS, CHANNELS], F32)
+        p_sum = keep.tile([P, CHUNKS, CHANNELS], F32)
+        f_raw = keep.tile([P, KERNEL * PAIRS, P], BF16)
+        f_wide = keep.tile([P, KERNEL * PAIRS, PAD + P + PAD], F32)
+        comp_bf = keep.tile([P, CHUNKS, CHANNELS], BF16)
+        nc.vector.memset(f_raw[:], 0.0)
+        nc.vector.memset(f_wide[:, :, 0:PAD], 0.0)
+        nc.vector.memset(f_wide[:, :, PAD + P :], 0.0)
 
         x_slab = {}
         x_px = {}
         minus_top = {}
+        total = {}
+        inverse = {}
         q_px = {}
         q_back = {}
-        total = {}
         g_slab = {}
-        g_px = {}
+        g_words = {}
         g_grouped = {}
         grad_operand = {}
 
-        def pixels_of(g):
-            return slice((g % PASSES) * PASS_PIXELS, (g % PASSES + 1) * PASS_PIXELS)
+        def load(slab, source, g):
+            for b in range(IMAGES):
+                for k in range(CHUNKS):
+                    nc.sync.dma_start(out=slab[:, k, :, b, :], in_=source[b, k * P : (k + 1) * P, g * PACK : (g + 1) * PACK, :])
 
         def load_logits(g):
-            x_slab[g] = slabs.tile([P, CHUNKS, PASS_PIXELS], BF16, name="x_slab")
-            nc.sync.dma_start(out=x_slab[g][:], in_=logit_view[g // PASSES][:, :, pixels_of(g)])
-            total[g] = soft.tile([P, PACK], F32, name="total")
+            x_slab[g] = slabs.tile([P, CHUNKS, PACK, IMAGES, WIDTH], BF16, name="x_slab")
+            load(x_slab[g], input_logit, g)
 
-        def turn_logits(g, t, pool, tag):
-            x_px[g, t] = pool.tile([P, CHANNELS], BF16, name="x_px", tag=tag)
+        def turn_logits(r):
+            x_px[r] = psum.tile([P, CHANNELS], BF16, name="x_px", tag="side_a")
             for k in range(CHUNKS):
-                nc.tensor.transpose(x_px[g, t][:, k * P : (k + 1) * P], x_slab[g][:, k, t * P : (t + 1) * P], ident_bf[:])
-
-        def find_top(g, t):
-            minus_top[g, t] = soft.tile([P, 1], F32, name="minus_top")
-            nc.vector.reduce_max(out=minus_top[g, t][:], in_=x_px[g, t][:], axis=AXIS.X, negate=True)
-
-        def exponentials(g, t):
-            q_px[g, t] = soft.tile([P, CHANNELS], F32, name="q_px")
-            nc.scalar.activation(
-                out=q_px[g, t][:], in_=x_px[g, t][:], func=FUNC.Exp, bias=minus_top[g, t][:], scale=1.0,
-                accum_out=total[g][:, t : t + 1],
-            )
-
-        def normalise(g):
-            inverse = soft.tile([P, PACK], F32)
-            nc.vector.reciprocal(out=inverse[:], in_=total[g][:])
-            for t in range(PACK):
-                nc.gpsimd.tensor_scalar(
-                    out=q_px[g, t][:], in0=q_px[g, t][:], scalar1=inverse[:, t : t + 1], scalar2=0.0,
-                    op0=ALU.mult, op1=ALU.add,
+                nc.tensor.transpose(
+                    x_px[r][:, k * P : (k + 1) * P], x_slab[r // PACK][:, k, r % PACK, :, :].rearrange("p b j -> p (b j)"), ident_bf[:]
                 )
 
-        def turn_q(g, k, pool, tag):
-            q_back[g, k] = pool.tile([P, PASS_PIXELS], F32, name="q_back", tag=tag)
-            for t in range(PACK):
-                nc.tensor.transpose(q_back[g, k][:, t * P : (t + 1) * P], q_px[g, t][:, k * P : (k + 1) * P], ident_f32)
+        def find_top(r):
+            minus_top[r] = stats.tile([P, 1], F32, name="minus_top")
+            nc.vector.reduce_max(out=minus_top[r][:], in_=x_px[r][:], axis=AXIS.X, negate=True)
 
-        def keep_q(g, k):
-            start = PAD + (g % PASSES) * PASS_PIXELS
-            nc.scalar.copy(out=q_chan[k][:, start : start + PASS_PIXELS], in_=q_back[g, k][:])
+        def exponentials(r):
+            q_px[r] = soft.tile([P, CHANNELS], F32, name="q_px")
+            total[r] = stats.tile([P, 1], F32, name="total")
+            nc.scalar.activation(
+                out=q_px[r][:], in_=x_px[r][:], func=FUNC.Exp, bias=minus_top[r][:], scale=1.0, accum_out=total[r][:]
+            )
+
+        def invert(r):
+            inverse[r] = stats.tile([P, 1], F32, name="inverse")
+            nc.vector.reciprocal(out=inverse[r][:], in_=total[r][:])
+
+        def normalise(r):
+            nc.gpsimd.tensor_scalar(out=q_px[r][:], in0=q_px[r][:], scalar1=inverse[r][:], scalar2=0.0, op0=ALU.mult, op1=ALU.add)
+
+        def turn_q(r):
+            q_back[r] = psum.tile([P, CHUNKS, P], F32, name="q_back", tag="side_b")
+            for k in range(CHUNKS):
+                nc.tensor.transpose(q_back[r][:, k, :], q_px[r][:, k * P : (k + 1) * P], ident_f32)
+
+        def keep_q(r):
+            nc.scalar.copy(out=q_ring[r % RING][:, :, PAD : PAD + P], in_=q_back[r][:])
 
         def load_grad(g):
-            g_slab[g] = slabs.tile([P, CHUNKS, PASS_PIXELS], BF16, name="g_slab")
-            nc.sync.dma_start(out=g_slab[g][:], in_=grad_view[g // PASSES][:, :, pixels_of(g)])
+            g_slab[g] = slabs.tile([P, CHUNKS, PACK, IMAGES, WIDTH], BF16, name="g_slab")
+            load(g_slab[g], grad_out, g)
             g_grouped[g] = operands.tile([P, CHANNELS, PACK], BF16, name="g_grouped", align_bytes=64)
 
-        def turn_grad(g, h, tag):
-            g_px[g, h] = psum_side.tile([P, PACK, HALF], BF16, name="g_px", tag=tag)
-            for t in range(PACK):
+        def turn_words(bank, rows_of):
+            for u in range(2):
                 for k in range(HALF // P):
-                    nc.tensor.transpose(
-                        g_px[g, h][:, t, k * P : (k + 1) * P], g_slab[g][:, h * (HALF // P) + k, t * P : (t + 1) * P], ident_bf[:]
-                    )
+                    nc.tensor.transpose(bank[:, u, k * P : (k + 1) * P], rows_of(k, u).bitcast(F32), ident_f32)
 
-        def group_grad(g, h, k):
-            first = h * HALF + k * P
-            nc.scalar.copy(
-                out=g_grouped[g][:, first : first + P, :], in_=g_px[g, h][:, :, k * P : (k + 1) * P].rearrange("p t o -> p o t")
+        def group_words(grouped, h, bank):
+            nc.scalar.copy(out=grouped[:].bitcast(F32)[:, h * HALF : (h + 1) * HALF, :], in_=bank[:].rearrange("p u c -> p c u"))
+
+        def turn_grad(g, h):
+            g_words[g, h] = psum.tile([P, 2, HALF], F32, name="g_words", tag="side_c")
+            turn_words(
+                g_words[g, h],
+                lambda k, u: g_slab[g][:, h * (HALF // P) + k, 2 * u : 2 * u + 2, :, :].rearrange("p s b j -> p (s b j)"),
             )
 
         def quantise_grad(g):
-            g_words = codes.tile([P, CHANNELS], U32, align_bytes=64)
+            g_codes = codes.tile([P, CHANNELS], U32, align_bytes=64)
             g_scales = codes.tile([P, CHANNELS], U8, align_bytes=64)
             nc.vector.quantize_mx(
-                out=g_words[:].bitcast(E5M2_X4), scales=g_scales[:], in_=g_grouped[g][:].rearrange("p o t -> p (o t)")
+                out=g_codes[:].bitcast(E5M2_X4), scales=g_scales[:], in_=g_grouped[g][:].rearrange("p o t -> p (o t)")
             )
-            grad_operand[g] = (g_words, g_scales)
+            grad_operand[g] = (g_codes, g_scales)
 
-        taps = keep.tile([P, IMAGES * TILES, TAPS], F32)
-        factor = keep.tile([P, CHUNKS, CHANNELS], F32)
-        p_sum = keep.tile([P, CHUNKS, CHANNELS], F32)
-        with tc.tile_pool(name="setup", bufs=1) as setup:
-            f_raw = setup.tile([P, IMAGES * PIXELS], BF16)
-            nc.vector.memset(f_raw[:], 0.0)
-            comp_bf = setup.tile([P, CHUNKS, CHANNELS], BF16)
-            load_logits(0)
-            nc.sync.dma_start(out=comp_bf[:], in_=comp_view)
-            for b in range(IMAGES):
-                for di in range(0, KERNEL, 2):
-                    nc.sync.dma_start(
-                        out=f_raw[column(di, 0) : column(di, 0) + KERNEL, b * PIXELS : (b + 1) * PIXELS],
-                        in_=input_F[b, di * KERNEL : (di + 1) * KERNEL].rearrange("p i j -> p (i j)"),
-                    )
-                odd_rows = input_F[b, KERNEL:TAPS].rearrange("(a q) i j -> a (q i j)", q=2 * KERNEL)
-                for dj in range(KERNEL):
-                    shift = dj - REACH
-                    early = shift % 2 if shift > 0 else 0
-                    target = max(shift, 0) - early
-                    source = dj * PIXELS + max(-shift, 0) - early
-                    length = PIXELS - abs(shift) + early
-                    nc.sync.dma_start(
-                        out=f_raw[column(1, dj) : column(1, dj) + KERNEL // 2, b * PIXELS + target : b * PIXELS + target + length],
-                        in_=odd_rows[:, source : source + length],
-                    )
-            ident_cols = ident_f32.rearrange("p (h j) -> p h j", j=WIDTH)
-            outside = setup.tile([P, 2, KERNEL], F32)
-            nc.vector.memset(outside[:], 0.0)
-            for dj in range(KERNEL):
-                reach = abs(dj - REACH)
-                if reach > 0:
-                    left, right = ident_cols[:, :, 0:reach], ident_cols[:, :, WIDTH - reach : WIDTH]
-                    nc.vector.tensor_reduce(
-                        out=outside[:, 0, dj : dj + 1], in_=(left if dj < REACH else right), axis=AXIS.XY, op=ALU.add
-                    )
-                    nc.vector.tensor_reduce(
-                        out=outside[:, 1, dj : dj + 1], in_=(right if dj < REACH else left), axis=AXIS.XY, op=ALU.add
-                    )
-            inside = setup.tile([P, 2, KERNEL], F32)
-            nc.vector.tensor_scalar(out=inside[:], in0=outside[:], scalar1=-1.0, scalar2=1.0, op0=ALU.mult, op1=ALU.add)
-            mask = setup.tile([P, TAPS], F32)
-            nc.vector.tensor_copy(
-                out=mask[:, 0 : column(1, 0)].rearrange("p (a d) -> p a d", d=KERNEL),
-                in_=inside[:, 0, :].unsqueeze(1).to_broadcast([P, KERNEL // 2 + 1, KERNEL]),
-            )
-            nc.vector.tensor_copy(
-                out=mask[:, column(1, 0) : TAPS].rearrange("p (d a) -> p d a", a=KERNEL // 2),
-                in_=inside[:, 1, :].unsqueeze(2).to_broadcast([P, KERNEL, KERNEL // 2]),
-            )
-            for t in range(PACK):
-                turn_logits(0, t, psum_window, "window")
-                find_top(0, t)
-                exponentials(0, t)
-            normalise(0)
-            nc.scalar.activation(out=factor[:], in_=comp_bf[:], func=FUNC.Sigmoid, scale=100.0)
-            nc.scalar.activation(out=p_sum[:], in_=comp_bf[:], func=FUNC.Sigmoid, scale=-100.0)
-            per_bank = 8
-            for first in range(0, IMAGES * TILES, per_bank):
-                f_px = psum_window.tile([P, per_bank, P], BF16, tag="window")
-                for n in range(per_bank):
-                    nc.tensor.transpose(f_px[:, n, :], f_raw[:, (first + n) * P : (first + n + 1) * P], ident_bf[:])
-                nc.vector.tensor_tensor(
-                    out=taps[:, first : first + per_bank, :], in0=f_px[:, :, 0:TAPS],
-                    in1=mask[:].unsqueeze(1).to_broadcast([P, per_bank, TAPS]), op=ALU.mult,
-                )
-            for k in range(CHUNKS):
-                turn_q(0, k, psum_window, "window")
-                keep_q(0, k)
-            nc.vector.scalar_tensor_tensor(out=factor[:], in0=factor[:], scalar=-100.0, in1=p_sum[:], op0=ALU.mult, op1=ALU.mult)
+        now = [0]
+        timed = {}
 
-        products = stack.enter_context(tc.tile_pool(name="products", bufs=PRODUCTS))
-        turned = stack.enter_context(tc.tile_pool(name="turned", bufs=6))
-        operands = stack.enter_context(tc.tile_pool(name="operands", bufs=2))
-        codes = stack.enter_context(tc.tile_pool(name="codes", bufs=GROUP + 2))
+        def at(slot, engine, job):
+            assert slot > now[0] or not timed
+            timed.setdefault(slot, []).extend([(engine, job)])
 
-        rows = [(b, r) for b in range(IMAGES) for r in range(-1, HEIGHT, TILE_ROWS)]
-        slots = len(rows) * KERNEL
-        last_pass = IMAGES * PASSES - 1
+        def after(delay, engine, job):
+            at(now[0] + delay, engine, job)
 
-        def tiles_of(step):
-            b, r = rows[step]
-            first_tile = b * TILES + max(0, (r - REACH + 1) // TILE_ROWS)
-            last_tile = b * TILES + min(TILES - 1, (r + REACH) // TILE_ROWS)
-            return [(i, r - TILE_ROWS * (i - b * TILES) + REACH) for i in range(first_tile, last_tile + 1)]
+        side_c_free = [-1000]
 
-        def shares(slot):
-            if not 0 <= slot < slots:
-                return [], []
-            dj = slot % KERNEL
-            served = [(i, column(di, dj)) for i, di in tiles_of(slot // KERNEL)]
-            scalars = 2 if len(served) == PACK and dj in SCALAR_TAKES_TWO else 1
-            return served[:scalars], served[scalars:]
+        def reserve(earliest, hold, job):
+            slot = max(earliest, side_c_free[0], now[0] + 1)
+            side_c_free[0] = slot + hold
+            at(slot, "tensor", job)
 
-        def straight(slot):
-            if not 0 <= slot < slots:
-                return []
-            b, r = rows[slot // KERNEL]
-            i = (r + 1) // TILE_ROWS - 1
-            dj = slot % KERNEL
+        def vector_slots(r):
+            ops = [
+                (w, di, dj, r + REACH - di)
+                for w, dj in enumerate(VECTOR_COLUMNS)
+                for di in range(KERNEL - 1, -1, -1)
+                if 0 <= r + REACH - di < HEIGHT and (di, dj) not in VECTOR_LEAVES
+            ]
+            return [ops[len(ops) * t // SLOTS : len(ops) * (t + 1) // SLOTS] for t in range(SLOTS)]
+
+        def products_of(i):
             return [
-                (b * TILES + i, b * TILES + i + (di - REACH) // 2, column(di, dj), (dj - REACH) % P)
-                for di in range(1, KERNEL, 2)
-                if i >= 0 and 0 <= i + (di - REACH) // 2 < TILES
+                (di, dj)
+                for dj in range(KERNEL)
+                for di in range(KERNEL)
+                if 0 <= i + di - REACH < HEIGHT and (dj not in VECTOR_COLUMNS or (di, dj) in VECTOR_LEAVES)
             ]
 
         vector_left = {}
+        for r in range(HEIGHT):
+            for ops in vector_slots(r):
+                for w, di, dj, i in ops:
+                    vector_left[i] = vector_left.get(i, 0) + 1
         parts_left = {}
-        for slot in range(slots):
-            for i, tap in shares(slot)[0]:
-                parts_left[i] = parts_left.get(i, 0) + 1
-            for i, tap in shares(slot)[1]:
-                if i not in vector_left:
-                    parts_left[i] = parts_left.get(i, 0) + 1
-                vector_left[i] = vector_left.get(i, 0) + 1
-            for i, u, tap, shift in straight(slot):
-                parts_left[i] = parts_left.get(i, 0) + 1
+        for i in range(HEIGHT):
+            parts_left[i] = len(products_of(i)) + 1
 
-        now = [-AHEAD]
-        timed = {}
-        queue = {"scalar": [], "vector": [], "urgent": []}
+        todo = []
         parts = []
-        chains = []
-        free_banks = ["side_a", "side_b"]
         finale = []
-
-        def at(slot, job):
-            timed.setdefault(max(slot, -AHEAD), []).extend([job])
-
-        def after(engine, delay, job):
-            queue[engine].extend([(now[0] + delay, job)])
-
-        def chain(earliest, deadline, start):
-            chains.extend([(earliest, deadline, start)])
-
-        def release(bank):
-            free_banks.extend([bank])
-
-        def take(engine, room):
-            ripe = [entry for entry in queue[engine] if entry[0] <= now[0]]
-            if room <= 0 and ripe and ripe[0][0] + PATIENCE <= now[0]:
-                room = 1
-            for entry in ripe[: max(room, 0)]:
-                queue[engine].remove(entry)
-                entry[1]()
-
-        def start_chain():
-            ripe = [entry for entry in chains if entry[0] <= now[0]]
-            if ripe and free_banks:
-                entry = min(ripe, key=lambda e: e[1])
-                bank = free_banks[0]
-                free_banks.remove(bank)
-                chains.remove(entry)
-                entry[2](bank)
-
         window = {}
         sum_vector = {}
         m_total = {}
         total_bank = {}
-        free_totals = ["total_a", "total_b", "total_c"]
+        free_totals = ["total_a", "total_b"]
         m_turned = {}
-        m_px = {}
+        m_words = {}
         m_grouped = {}
         m_operand = {}
         p_group = {}
         done = {}
-        kept = {0: CHUNKS}
+        last_pass = PASSES - 1
 
         def count(key, goal):
             done[key] = done.get(key, 0) + 1
             return done[key] == goal
 
-        def make_window(slot):
-            b, r = rows[slot // KERNEL]
-            start = PAD + r * WIDTH + slot % KERNEL - REACH
-            for g in range(b * PASSES, (b + 1) * PASSES):
-                first = PAD + (g % PASSES) * PASS_PIXELS
-                if start < first + PASS_PIXELS and first < start + P:
-                    assert kept.get(g, 0) == CHUNKS
-            window[slot] = psum_window.tile([P, CHANNELS], F32, name="window", tag="window")
+        def make_window(r, w):
+            start = PAD + VECTOR_COLUMNS[w] - REACH
+            window[r, w] = psum.tile([P, CHANNELS], F32, name="window", tag="window%d" % w)
             for k in range(CHUNKS):
-                nc.tensor.transpose(window[slot][:, k * P : (k + 1) * P], q_chan[k][:, start : start + P], ident_f32)
+                nc.tensor.transpose(window[r, w][:, k * P : (k + 1) * P], q_ring[r % RING][:, k, start : start + P], ident_f32)
 
         def add_parts():
             room = ADDS
@@ -351,7 +250,7 @@ def tile_localcrf_kernel(tc, input_F, input_logit, compatibility, grad_out, out)
                         continue
                     total_bank[i] = free_totals[0]
                     free_totals.remove(total_bank[i])
-                    m_total[i] = psum_total.tile([P, CHUNKS, P], F32, name="m_total", tag=total_bank[i])
+                    m_total[i] = psum.tile([P, CHUNKS, P], F32, name="m_total", tag=total_bank[i])
                     first = True
                 else:
                     first = False
@@ -364,110 +263,69 @@ def tile_localcrf_kernel(tc, input_F, input_logit, compatibility, grad_out, out)
                         start=(first and k == 0), stop=(parts_left[i] == 0 and k == CHUNKS - 1),
                     )
                 if parts_left[i] == 0:
-                    after("urgent", 2, lambda i=i: round_m(i))
+                    after(2, "scalar", lambda i=i: round_m(i))
 
         def round_m(i):
-            m_turned[i] = turned.tile([P, CHUNKS, P], BF16, name="m_turned")
-            nc.scalar.copy(out=m_turned[i][:], in_=m_total[i][:])
-            free_totals.extend([total_bank[i]])
             g = i // PACK
+            if g not in m_turned:
+                m_turned[g] = turned.tile([P, CHUNKS, PACK, P], BF16, name="m_turned")
+            nc.scalar.copy(out=m_turned[g][:, :, i % PACK, :], in_=m_total[i][:])
+            free_totals.extend([total_bank[i]])
             if count(("rounded", g), PACK):
                 m_grouped[g] = operands.tile([P, CHANNELS, PACK], BF16, name="m_grouped", align_bytes=64)
                 for h in range(2):
-                    chain(now[0] + 1, now[0] + 10 + h, lambda bank, h=h: m_chain(g, h, bank))
+                    reserve(now[0] + 1, 4, lambda h=h: turn_m(g, h))
 
-        def m_chain(g, h, bank):
-            m_px[g, h] = psum_side.tile([P, PACK, HALF], BF16, name="m_px", tag=bank)
+        def turn_m(g, h):
+            m_words[g, h] = psum.tile([P, 2, HALF], F32, name="m_words", tag="side_c")
             count(("m turned", g), 2)
-            for t in range(PACK):
-                for k in range(HALF // P):
-                    nc.tensor.transpose(
-                        m_px[g, h][:, t, k * P : (k + 1) * P], m_turned[g * PACK + t][:, h * (HALF // P) + k, :], ident_bf[:]
-                    )
+            turn_words(
+                m_words[g, h], lambda k, u: m_turned[g][:, h * (HALF // P) + k, 2 * u : 2 * u + 2, :].rearrange("p s n -> p (s n)")
+            )
+            after(2, "scalar", lambda: group_m(g, h))
 
-            def group(k):
-                first = h * HALF + k * P
-                nc.scalar.copy(
-                    out=m_grouped[g][:, first : first + P, :], in_=m_px[g, h][:, :, k * P : (k + 1) * P].rearrange("p t c -> p c t")
-                )
-                if k == 1:
-                    release(bank)
-                    if count(("m grouped", g), 2):
-                        after("vector", 3, lambda: quantise_m(g))
-
-            after("scalar", 1, lambda: group(0))
-            after("scalar", 1, lambda: group(1))
+        def group_m(g, h):
+            group_words(m_grouped[g], h, m_words[g, h])
+            if h == 1:
+                after(2, "vector", lambda: quantise_m(g))
 
         def quantise_m(g):
-            m_words = codes.tile([P, CHANNELS], U32, align_bytes=64)
+            m_codes = codes.tile([P, CHANNELS], U32, align_bytes=64)
             m_scales = codes.tile([P, CHANNELS], U8, align_bytes=64)
             nc.vector.quantize_mx(
-                out=m_words[:].bitcast(E4M3_X4), scales=m_scales[:], in_=m_grouped[g][:].rearrange("p c t -> p (c t)")
+                out=m_codes[:].bitcast(E4M3_X4), scales=m_scales[:], in_=m_grouped[g][:].rearrange("p c t -> p (c t)")
             )
-            m_operand[g] = (m_words, m_scales)
+            m_operand[g] = (m_codes, m_scales)
             if g % GROUP == GROUP - 1 and g != last_pass:
                 for k in range(CHUNKS):
-                    chain(now[0] + 2, now[0] + 30 + k, lambda bank, k=k: early_group(g, k, bank))
+                    reserve(now[0] + 2, 4, lambda k=k: early_group(g, k))
 
-        def grad_chain(g, h, bank):
-            turn_grad(g, h, bank)
+        def grad_chain(g, h):
+            turn_grad(g, h)
 
-            def group(k):
-                group_grad(g, h, k)
-                if k == 1:
-                    release(bank)
-                    if count(("grad grouped", g), 2):
-                        after("vector", 3, lambda: quantise_grad(g))
+            def group():
+                group_words(g_grouped[g], h, g_words[g, h])
+                if h == 1:
+                    after(2, "vector", lambda: quantise_grad(g))
 
-            after("scalar", 1, lambda: group(0))
-            after("scalar", 1, lambda: group(1))
-
-        def softmax_chain(g, t, bank):
-            turn_logits(g, t, psum_side, bank)
-
-            def top():
-                find_top(g, t)
-                after("scalar", 2, finish)
-
-            def finish():
-                exponentials(g, t)
-                release(bank)
-                if count(("exp", g), PACK):
-                    after("vector", 1, divide)
-
-            def divide():
-                normalise(g)
-                for k in range(CHUNKS):
-                    chain(now[0] + 2, needed(g) - 4 + k, lambda bank, k=k: q_chain(g, k, bank))
-
-            after("vector", 2, top)
-
-        def q_chain(g, k, bank):
-            turn_q(g, k, psum_side, bank)
-
-            def finish():
-                keep_q(g, k)
-                kept[g] = kept.get(g, 0) + 1
-                release(bank)
-
-            after("scalar", 1, finish)
+            after(2, "scalar", group)
 
         def multiply(bank, k, passes, start, stop):
             for g in passes:
-                g_words, g_scales = grad_operand[g]
-                m_words, m_scales = m_operand[g]
+                g_codes, g_scales = grad_operand[g]
+                m_codes, m_scales = m_operand[g]
                 nc.tensor.matmul_mx(
                     out=bank[:],
-                    lhsT=g_words[:, k * P : (k + 1) * P].bitcast(E5M2_X4),
+                    lhsT=g_codes[:, k * P : (k + 1) * P].bitcast(E5M2_X4),
                     lhsT_scale=g_scales[:, k * P : (k + 1) * P],
-                    rhs=m_words[:].bitcast(E4M3_X4),
+                    rhs=m_codes[:].bitcast(E4M3_X4),
                     rhs_scale=m_scales[:],
                     start=(start and g == passes[0]),
                     stop=(stop and g == passes[-1]),
                 )
 
-        def early_group(last, k, bank):
-            p_early = psum_side.tile([P, CHANNELS], F32, tag=bank)
+        def early_group(last, k):
+            p_early = psum.tile([P, CHANNELS], F32, name="p_early", tag="side_c")
             multiply(p_early, k, list(range(last - GROUP + 1, last + 1)), True, True)
 
             def gather():
@@ -475,95 +333,152 @@ def tile_localcrf_kernel(tc, input_F, input_logit, compatibility, grad_out, out)
                     nc.vector.tensor_copy(out=p_sum[:, k, :], in_=p_early[:])
                 else:
                     nc.vector.tensor_tensor(out=p_sum[:, k, :], in0=p_early[:], in1=p_sum[:, k, :], op=ALU.add)
-                release(bank)
 
-            after("vector", 3, gather)
+            after(2, "vector", gather)
 
         def open_last_group(k):
-            if k < CHUNKS - 1:
-                p_group[k] = psum_window.tile([P, CHANNELS], F32, name="p_group", tag="window")
-            else:
-                p_group[k] = psum_total.tile([P, CHANNELS], F32, name="p_group", tag=free_totals[0])
-                free_totals.remove(free_totals[0])
+            p_group[k] = psum.tile([P, CHANNELS], F32, name="p_group", tag=("window%d" % k if k < len(VECTOR_COLUMNS) else "side_a"))
             multiply(p_group[k], k, list(range(last_pass - GROUP + 1, last_pass)), True, False)
 
         def close_last_group(k):
             multiply(p_group[k], k, [last_pass], False, True)
             nc.vector.tensor_tensor(out=p_sum[:, k, :], in0=p_group[k][:], in1=p_sum[:, k, :], op=ALU.add)
-            nc.vector.tensor_tensor(out=factor[:, k, :], in0=p_sum[:, k, :], in1=factor[:, k, :], op=ALU.mult)
+            nc.vector.scalar_tensor_tensor(
+                out=factor[:, k, :], in0=p_sum[:, k, :], scalar=-100.0, in1=factor[:, k, :], op0=ALU.mult, op1=ALU.mult
+            )
             nc.sync.dma_start(out=out_view[:, k, :], in_=factor[:, k, :])
 
-        def use_window(slot):
-            scalars, vectors = shares(slot)
-            for i, tap in vectors:
+        def vector_taps(r, t):
+            for w, di, dj, i in vector_slots(r)[t]:
                 if i not in sum_vector:
                     sum_vector[i] = sums.tile([P, CHANNELS], F32, name="sum_vector")
-                    nc.vector.tensor_scalar_mul(out=sum_vector[i][:], in0=window[slot][:], scalar1=taps[:, i, tap : tap + 1])
+                    nc.vector.tensor_scalar_mul(out=sum_vector[i][:], in0=window[r, w][:], scalar1=weight("target", di, dj, i))
                 else:
                     nc.vector.scalar_tensor_tensor(
-                        out=sum_vector[i][:], in0=window[slot][:], scalar=taps[:, i, tap : tap + 1], in1=sum_vector[i][:],
+                        out=sum_vector[i][:], in0=window[r, w][:], scalar=weight("target", di, dj, i), in1=sum_vector[i][:],
                         op0=ALU.mult, op1=ALU.add,
                     )
                 vector_left[i] -= 1
                 if vector_left[i] == 0:
-                    parts.extend([(slot + 2, i, sum_vector[i], 0)])
-            for i, tap in scalars:
+                    parts.extend([(now[0] + 2, i, sum_vector[i], 0)])
+
+        def make_products(scalar_room, gpsimd_room):
+            for n in range(min(gpsimd_room, len(todo))):
+                i, di, dj = todo[0]
+                todo.remove(todo[0])
+                product_g = products.tile([P, CHANNELS], F32)
+                nc.gpsimd.tensor_scalar(
+                    out=product_g[:], in0=q_px[i + di - REACH][:], scalar1=weight("source", di, dj, i), scalar2=0.0,
+                    op0=ALU.mult, op1=ALU.add,
+                )
+                parts.extend([(now[0] + 2, i, product_g, (dj - REACH) % P)])
+            for n in range(min(scalar_room, len(todo))):
+                i, di, dj = todo[0]
+                todo.remove(todo[0])
                 product = products.tile([P, CHANNELS], F32)
-                nc.scalar.activation(out=product[:], in_=window[slot][:], func=FUNC.Copy, scale=taps[:, i, tap : tap + 1])
-                parts.extend([(slot + 2, i, product, 0)])
-            for n, (i, u, tap, shift) in enumerate(straight(slot)):
-                source = q_px[u // PACK, u % PACK]
-                if n < GPSIMD_TAKES[slot % KERNEL]:
-                    product_g = products.tile([P, CHANNELS], F32)
-                    nc.gpsimd.tensor_scalar(
-                        out=product_g[:], in0=source[:], scalar1=taps[:, i, tap : tap + 1], scalar2=0.0, op0=ALU.mult, op1=ALU.add
-                    )
-                    parts.extend([(slot + 2, i, product_g, shift)])
-                else:
-                    product = products.tile([P, CHANNELS], F32)
-                    nc.scalar.activation(out=product[:], in_=source[:], func=FUNC.Copy, scale=taps[:, i, tap : tap + 1])
-                    parts.extend([(slot + 1, i, product, shift)])
+                nc.scalar.activation(out=product[:], in_=q_px[i + di - REACH][:], func=FUNC.Copy, scale=weight("source", di, dj, i))
+                parts.extend([(now[0] + 1, i, product, (dj - REACH) % P)])
 
-        def needed(g):
-            return KERNEL * rows.index((g // PASSES, (g % PASSES) * PASS_ROWS - 1)) - AHEAD
+        first_slot = -20
+        now[0] = first_slot - 1
+        load_logits(0)
+        for b in range(IMAGES):
+            for di in range(KERNEL):
+                nc.sync.dma_start(
+                    out=f_raw[WIDTH * (di % 2) : WIDTH * (di % 2) + WIDTH, di // 2 : KERNEL * PAIRS : PAIRS, b * WIDTH : (b + 1) * WIDTH],
+                    in_=input_F[b, di * KERNEL : (di + 1) * KERNEL].rearrange("q i j -> i q j"),
+                )
+        load_logits(1)
+        nc.sync.dma_start(out=comp_bf[:], in_=comp_view)
+        ident_cols = ident_f32.rearrange("p (h j) -> p h j", j=WIDTH)
+        outside = keep.tile([P, 2, KERNEL], F32)
+        nc.vector.memset(outside[:], 0.0)
+        for dj in range(KERNEL):
+            reach = abs(dj - REACH)
+            if reach > 0:
+                left, right = ident_cols[:, :, 0:reach], ident_cols[:, :, WIDTH - reach : WIDTH]
+                nc.vector.tensor_reduce(out=outside[:, 0, dj : dj + 1], in_=(left if dj < REACH else right), axis=AXIS.XY, op=ALU.add)
+                nc.vector.tensor_reduce(out=outside[:, 1, dj : dj + 1], in_=(right if dj < REACH else left), axis=AXIS.XY, op=ALU.add)
+        inside = keep.tile([P, 2, KERNEL], F32)
+        nc.vector.tensor_scalar(out=inside[:], in0=outside[:], scalar1=-1.0, scalar2=1.0, op0=ALU.mult, op1=ALU.add)
 
-        last_reader = {}
-        for slot in range(slots):
-            for i, u, tap, shift in straight(slot):
-                last_reader[u] = slot
-        for g in range(IMAGES * PASSES):
-            last_step = rows.index((g // PASSES, min(TILE_ROWS * (PACK * (g % PASSES) + PACK - 1) + REACH, HEIGHT - 1)))
-            if g > 0:
-                at(needed(g) - LEAD - 8, lambda g=g: load_logits(g))
-                for t in range(PACK):
-                    earliest = max(needed(g) - LEAD, last_reader.get(g * PACK + t - Q_TILES, 0) + 1)
-                    chain(earliest, needed(g) - 16 + t, lambda bank, g=g, t=t: softmax_chain(g, t, bank))
-            at(KERNEL * last_step - 40, lambda g=g: load_grad(g))
-            for h in range(2):
-                chain(KERNEL * last_step - 30, KERNEL * last_step + h, lambda bank, g=g, h=h: grad_chain(g, h, bank))
-        finale.extend([(lambda: not parts, lambda: open_last_group(0))])
-        for k in range(1, CHUNKS):
-            finale.extend([(lambda: done.get(("m turned", last_pass), 0) == 2, lambda k=k: open_last_group(k))])
+        def widen(dj):
+            nc.gpsimd.tensor_scalar(
+                out=f_wide[:, dj * PAIRS : (dj + 1) * PAIRS, PAD : PAD + P], in0=f_raw[:, dj * PAIRS : (dj + 1) * PAIRS, :],
+                scalar1=1.0, scalar2=0.0, op0=ALU.mult, op1=ALU.add,
+            )
+
+        def make_table(n, bank):
+            kind, dj = tables[n]
+            if kind == "target":
+                f_px = psum.tile([P, PAIRS, P], BF16, name="f_px", tag=bank)
+                for a in range(PAIRS):
+                    nc.tensor.transpose(f_px[:, a, :], f_raw[:, dj * PAIRS + a, :], ident_bf[:])
+            else:
+                start = PAD - (dj - REACH)
+                f_px = psum.tile([P, PAIRS, P], F32, name="f_px", tag=bank)
+                for a in range(PAIRS):
+                    nc.tensor.transpose(f_px[:, a, :], f_wide[:, dj * PAIRS + a, start : start + P], ident_f32)
+            after(
+                1, "scalar",
+                lambda: nc.scalar.activation(
+                    out=taps[:, n, :, :], in_=f_px[:], func=FUNC.Copy, scale=inside[:, (0 if kind == "target" else 1), dj : dj + 1]
+                ),
+            )
+
+        for n in range(len(tables)):
+            kind, dj = tables[n]
+            if kind == "target":
+                at(-13 + 2 * n, "tensor", lambda n=n: make_table(n, ("total_a", "total_b")[n % 2]))
+            else:
+                at(-9 + 2 * n, "gpsimd", lambda dj=dj: widen(dj))
+                at(-5 + 2 * n, "tensor", lambda n=n: make_table(n, ("total_a", "total_b")[n % 2]))
+        at(8, "scalar", lambda: nc.scalar.activation(out=factor[:], in_=comp_bf[:], func=FUNC.Sigmoid, scale=100.0))
+        at(9, "scalar", lambda: nc.scalar.activation(out=p_sum[:], in_=comp_bf[:], func=FUNC.Sigmoid, scale=-100.0))
+        at(12, "gpsimd", lambda: nc.gpsimd.tensor_tensor(out=factor[:], in0=factor[:], in1=p_sum[:], op=ALU.mult))
+
+        for g in range(PASSES):
+            if g > 1:
+                at(max(SLOTS * PACK * g - 60, first_slot), "sync", lambda g=g: load_logits(g))
+            at(max(SLOTS * PACK * g - 20, first_slot), "sync", lambda g=g: load_grad(g))
+        for r in range(HEIGHT):
+            base = SLOTS * r
+            at(base - 18, "tensor", lambda r=r: turn_logits(r))
+            at(base - 16, "vector", lambda r=r: find_top(r))
+            at(base - 14, "scalar", lambda r=r: exponentials(r))
+            at(base - 12, "vector", lambda r=r: invert(r))
+            at(base - 11, "gpsimd", lambda r=r: normalise(r))
+            at(base - 8, "tensor", lambda r=r: turn_q(r))
+            at(base - 6, "scalar", lambda r=r: keep_q(r))
+            for w in range(len(VECTOR_COLUMNS)):
+                first_use = min([t for t in range(SLOTS) if [op for op in vector_slots(r)[t] if op[0] == w]])
+                at(base + first_use - 2, "tensor", lambda r=r, w=w: make_window(r, w))
+        for k in range(CHUNKS):
+            finale.extend([(lambda: not parts and not todo and last_pass - 1 in m_operand and last_pass - 1 in grad_operand, lambda k=k: open_last_group(k))])
         for k in range(CHUNKS):
             finale.extend([(lambda: last_pass in m_operand and last_pass in grad_operand, lambda k=k: close_last_group(k))])
 
-        for slot in range(-AHEAD, slots + 60):
+        for slot in range(first_slot, SLOTS * (HEIGHT + 12)):
             now[0] = slot
-            if slot + AHEAD < slots:
-                make_window(slot + AHEAD)
-            for job in timed.get(slot, []):
+            if (slot + EARLY) % SLOTS == 0 and 0 <= (slot + EARLY) // SLOTS - REACH < HEIGHT:
+                i = (slot + EARLY) // SLOTS - REACH
+                todo.extend([(i, di, dj) for di, dj in products_of(i)])
+            if slot % (SLOTS * PACK) == 0 and 0 <= slot // (SLOTS * PACK) < PASSES:
+                for h in range(2):
+                    reserve(slot + 1, 4, lambda g=slot // (SLOTS * PACK), h=h: grad_chain(g, h))
+            jobs = timed.get(slot, [])
+            for engine, job in jobs:
                 job()
             add_parts()
-            assert len(parts) <= 2 * PRODUCTS - 8
-            start_chain()
-            if slot >= slots and finale and finale[0][0]():
+            assert len(parts) <= 2 * PRODUCTS - 6
+            if slot >= SLOTS * HEIGHT and finale and finale[0][0]():
                 job = finale[0]
                 finale.remove(job)
                 job[1]()
-            scalars, vectors = shares(slot)
-            take("urgent", FULL)
-            take("scalar", FULL - len(scalars) - max(len(straight(slot)) - GPSIMD_TAKES[slot % KERNEL], 0))
-            take("vector", FULL - len(vectors))
-            if 0 <= slot < slots:
-                use_window(slot)
-        assert not (parts or chains or finale or queue["scalar"] or queue["vector"] or queue["urgent"])
+            make_products(
+                SCALAR_ROOM - len([job for job in jobs if job[0] == "scalar"]), GPSIMD_ROOM - len([job for job in jobs if job[0] == "gpsimd"])
+            )
+            if 0 <= slot < SLOTS * HEIGHT:
+                vector_taps(slot // SLOTS, slot % SLOTS)
+        assert not (parts or todo or finale)
+        assert max(timed) <= now[0]

@@ -32,7 +32,7 @@ ADDS = 6
 EARLY = 3
 Q_TILES = 11
 SUMS = 9
-PRODUCTS = 8
+PRODUCTS = 12
 RING = 3
 
 FLOPS = 2 * CHANNELS * CHANNELS * IMAGES * HEIGHT * WIDTH + 2 * KERNEL * KERNEL * CHANNELS * IMAGES * HEIGHT * WIDTH
@@ -241,10 +241,8 @@ def tile_localcrf_kernel(tc, input_F, input_logit, compatibility, grad_out, out)
 
         def add_parts():
             room = ADDS
-            for entry in list(parts):
+            for entry in reversed([entry for entry in parts if entry[0] <= now[0]][:ADDS]):
                 ready, i, part, shift = entry
-                if room == 0 or ready > now[0]:
-                    continue
                 if i not in m_total:
                     if not free_totals:
                         continue
@@ -371,13 +369,13 @@ def tile_localcrf_kernel(tc, input_F, input_logit, compatibility, grad_out, out)
                     out=product_g[:], in0=q_px[i + di - REACH][:], scalar1=weight("source", di, dj, i), scalar2=0.0,
                     op0=ALU.mult, op1=ALU.add,
                 )
-                parts.extend([(now[0] + 2, i, product_g, (dj - REACH) % P)])
+                parts.extend([(now[0] + 3, i, product_g, (dj - REACH) % P)])
             for n in range(min(scalar_room, len(todo))):
                 i, di, dj = todo[0]
                 todo.remove(todo[0])
                 product = products.tile([P, CHANNELS], F32)
                 nc.scalar.activation(out=product[:], in_=q_px[i + di - REACH][:], func=FUNC.Copy, scale=weight("source", di, dj, i))
-                parts.extend([(now[0] + 1, i, product, (dj - REACH) % P)])
+                parts.extend([(now[0] + 2, i, product, (dj - REACH) % P)])
 
         first_slot = -20
         now[0] = first_slot - 1
@@ -452,7 +450,7 @@ def tile_localcrf_kernel(tc, input_F, input_logit, compatibility, grad_out, out)
             at(base - 6, "scalar", lambda r=r: keep_q(r))
             for w in range(len(VECTOR_COLUMNS)):
                 first_use = min([t for t in range(SLOTS) if [op for op in vector_slots(r)[t] if op[0] == w]])
-                at(base + first_use - 2, "tensor", lambda r=r, w=w: make_window(r, w))
+                at(base + first_use - 3, "tensor", lambda r=r, w=w: make_window(r, w))
         for k in range(CHUNKS):
             finale.extend([(lambda: not parts and not todo and last_pass - 1 in m_operand and last_pass - 1 in grad_operand, lambda k=k: open_last_group(k))])
         for k in range(CHUNKS):

@@ -26,13 +26,14 @@ SLOTS = 7
 GROUP = 4
 VECTOR_COLUMNS = (2, 3, 4)
 VECTOR_LEAVES = ((6, 4),)
-SCALAR_ROOM = 3
-GPSIMD_ROOM = 2
+SCALAR_ROOM = 10
+GPSIMD_ROOM = 4
+MERGE_COLUMNS = (0,)
 ADDS = 6
 EARLY = 3
 Q_TILES = 11
 SUMS = 9
-PRODUCTS = 12
+PRODUCTS = 11
 RING = 3
 
 FLOPS = 2 * CHANNELS * CHANNELS * IMAGES * HEIGHT * WIDTH + 2 * KERNEL * KERNEL * CHANNELS * IMAGES * HEIGHT * WIDTH
@@ -51,6 +52,7 @@ def tile_localcrf_kernel(tc, input_F, input_logit, compatibility, grad_out, out)
         stats = stack.enter_context(tc.tile_pool(name="stats", bufs=6))
         sums = stack.enter_context(tc.tile_pool(name="sums", bufs=SUMS))
         products = stack.enter_context(tc.tile_pool(name="products", bufs=PRODUCTS))
+        paired_products = stack.enter_context(tc.tile_pool(name="paired_products", bufs=4))
         turned = stack.enter_context(tc.tile_pool(name="turned", bufs=2))
         operands = stack.enter_context(tc.tile_pool(name="operands", bufs=2))
         codes = stack.enter_context(tc.tile_pool(name="codes", bufs=GROUP + 2))
@@ -209,11 +211,23 @@ def tile_localcrf_kernel(tc, input_F, input_logit, compatibility, grad_out, out)
             for ops in vector_slots(r):
                 for w, di, dj, i in ops:
                     vector_left[i] = vector_left.get(i, 0) + 1
+        def merged_of(i):
+            pairs = []
+            for dj in MERGE_COLUMNS:
+                column = [tap for tap in products_of(i) if tap[1] == dj]
+                pairs.extend([(column[0], column[1])])
+            return pairs
+
         parts_left = {}
         for i in range(HEIGHT):
-            parts_left[i] = len(products_of(i)) + 1
+            parts_left[i] = len(products_of(i)) - len(merged_of(i)) + 1
 
         todo = []
+        todo_pairs = []
+        halves = {}
+        merges = []
+        credit = [0]
+        credit_scalar = [0]
         parts = []
         finale = []
         window = {}
@@ -361,21 +375,43 @@ def tile_localcrf_kernel(tc, input_F, input_logit, compatibility, grad_out, out)
                     parts.extend([(now[0] + 2, i, sum_vector[i], 0)])
 
         def make_products(scalar_room, gpsimd_room):
-            for n in range(min(gpsimd_room, len(todo))):
-                i, di, dj = todo[0]
-                todo.remove(todo[0])
-                product_g = products.tile([P, CHANNELS], F32)
-                nc.gpsimd.tensor_scalar(
-                    out=product_g[:], in0=q_px[i + di - REACH][:], scalar1=weight("source", di, dj, i), scalar2=0.0,
-                    op0=ALU.mult, op1=ALU.add,
-                )
-                parts.extend([(now[0] + 3, i, product_g, (dj - REACH) % P)])
-            for n in range(min(scalar_room, len(todo))):
-                i, di, dj = todo[0]
-                todo.remove(todo[0])
-                product = products.tile([P, CHANNELS], F32)
-                nc.scalar.activation(out=product[:], in_=q_px[i + di - REACH][:], func=FUNC.Copy, scale=weight("source", di, dj, i))
-                parts.extend([(now[0] + 2, i, product, (dj - REACH) % P)])
+            credit[0] = min(credit[0], 0) + gpsimd_room
+            while credit[0] > 0:
+                if merges and merges[0][0] <= now[0]:
+                    ready, i, dj = merges[0]
+                    merges.remove(merges[0])
+                    pair = halves[i, dj]
+                    nc.gpsimd.tensor_tensor(out=pair[0][:], in0=pair[0][:], in1=pair[1][:], op=ALU.add)
+                    parts.extend([(now[0] + 3, i, pair[0], (dj - REACH) % P)])
+                    credit[0] -= 3
+                elif todo:
+                    i, di, dj = todo[0]
+                    todo.remove(todo[0])
+                    product_g = products.tile([P, CHANNELS], F32)
+                    nc.gpsimd.tensor_scalar(
+                        out=product_g[:], in0=q_px[i + di - REACH][:], scalar1=weight("source", di, dj, i), scalar2=0.0,
+                        op0=ALU.mult, op1=ALU.add,
+                    )
+                    parts.extend([(now[0] + 3, i, product_g, (dj - REACH) % P)])
+                    credit[0] -= 2
+                else:
+                    credit[0] = 0
+            credit_scalar[0] = min(credit_scalar[0], 2) + scalar_room
+            while credit_scalar[0] >= 3:
+                credit_scalar[0] -= 3
+                if todo_pairs or todo:
+                    paired = len(todo_pairs) > 0
+                    queue = todo_pairs if paired else todo
+                    i, di, dj = queue[0]
+                    queue.remove(queue[0])
+                    product = (paired_products if paired else products).tile([P, CHANNELS], F32, name="product")
+                    nc.scalar.activation(out=product[:], in_=q_px[i + di - REACH][:], func=FUNC.Copy, scale=weight("source", di, dj, i))
+                    if paired:
+                        halves.setdefault((i, dj), []).extend([product])
+                        if len(halves[i, dj]) == 2:
+                            merges.extend([(now[0] + 2, i, dj)])
+                    else:
+                        parts.extend([(now[0] + 2, i, product, (dj - REACH) % P)])
 
         first_slot = -20
         now[0] = first_slot - 1
@@ -452,7 +488,7 @@ def tile_localcrf_kernel(tc, input_F, input_logit, compatibility, grad_out, out)
                 first_use = min([t for t in range(SLOTS) if [op for op in vector_slots(r)[t] if op[0] == w]])
                 at(base + first_use - 3, "tensor", lambda r=r, w=w: make_window(r, w))
         for k in range(CHUNKS):
-            finale.extend([(lambda: not parts and not todo and last_pass - 1 in m_operand and last_pass - 1 in grad_operand, lambda k=k: open_last_group(k))])
+            finale.extend([(lambda: not parts and not todo and not merges and last_pass - 1 in m_operand and last_pass - 1 in grad_operand, lambda k=k: open_last_group(k))])
         for k in range(CHUNKS):
             finale.extend([(lambda: last_pass in m_operand and last_pass in grad_operand, lambda k=k: close_last_group(k))])
 
@@ -460,7 +496,10 @@ def tile_localcrf_kernel(tc, input_F, input_logit, compatibility, grad_out, out)
             now[0] = slot
             if (slot + EARLY) % SLOTS == 0 and 0 <= (slot + EARLY) // SLOTS - REACH < HEIGHT:
                 i = (slot + EARLY) // SLOTS - REACH
-                todo.extend([(i, di, dj) for di, dj in products_of(i)])
+                pairs = merged_of(i)
+                for pair in pairs:
+                    todo_pairs.extend([(i, pair[0][0], pair[0][1]), (i, pair[1][0], pair[1][1])])
+                todo.extend([(i, di, dj) for di, dj in products_of(i) if not [pair for pair in pairs if (di, dj) in pair]])
             if slot % (SLOTS * PACK) == 0 and 0 <= slot // (SLOTS * PACK) < PASSES:
                 for h in range(2):
                     reserve(slot + 1, 4, lambda g=slot // (SLOTS * PACK), h=h: grad_chain(g, h))
@@ -474,9 +513,9 @@ def tile_localcrf_kernel(tc, input_F, input_logit, compatibility, grad_out, out)
                 finale.remove(job)
                 job[1]()
             make_products(
-                SCALAR_ROOM - len([job for job in jobs if job[0] == "scalar"]), GPSIMD_ROOM - len([job for job in jobs if job[0] == "gpsimd"])
+                SCALAR_ROOM - 3 * len([job for job in jobs if job[0] == "scalar"]), GPSIMD_ROOM - 2 * len([job for job in jobs if job[0] == "gpsimd"])
             )
             if 0 <= slot < SLOTS * HEIGHT:
                 vector_taps(slot // SLOTS, slot % SLOTS)
-        assert not (parts or todo or finale)
+        assert not (parts or todo or todo_pairs or merges or finale)
         assert max(timed) <= now[0]

@@ -26,14 +26,29 @@ SLOTS = 7
 GROUP = 4
 VECTOR_COLUMNS = (2, 3, 4)
 VECTOR_LEAVES = ((6, 4),)
+BAND = 6
+BAND_STARTS = (0, 20, 38, 58)
+BAND_COLUMNS = (0, 1, 2, 3, 4, 5, 6)
+AFTER = 3
+AFTER_COLUMNS = (2, 3)
+KEPT_COLUMNS = ()
+PATCH = 21
+STRIDE = PATCH - 2 * REACH
+GROUPS = ((0, 18), (18, 15), (33, 15), (48, 16))
+ZONE = 192
+CENTRE = REACH * PATCH + REACH
 SCALAR_ROOM = 10
 GPSIMD_ROOM = 4
 MERGE_COLUMNS = (0,)
 ADDS = 6
+GRAD_DELAY = 20
+BAND_BEGIN = 44
+PATCH_SLOT = 3
 EARLY = 3
 Q_TILES = 11
 SUMS = 9
-PRODUCTS = 11
+PRODUCTS = 10
+WINDOW_BANKS = 3
 RING = 3
 
 FLOPS = 2 * CHANNELS * CHANNELS * IMAGES * HEIGHT * WIDTH + 2 * KERNEL * KERNEL * CHANNELS * IMAGES * HEIGHT * WIDTH
@@ -43,19 +58,26 @@ def tile_localcrf_kernel(tc, input_F, input_logit, compatibility, grad_out, out)
     nc = tc.nc
     comp_view = compatibility.rearrange("(k o) c a b -> o k (c a b)", o=P)
     out_view = out.rearrange("(k o) c a b -> o k (c a b)", o=P)
+    out_rows = out.rearrange("o c a b -> o (c a b)")
+    out_flat = out.rearrange("o c a b -> (o c a b)")
+    zones_at = 2 * P * CHANNELS
+    zones_row = len(GROUPS) * ZONE
+    zones_flat = out_flat[zones_at : zones_at + (P + 1) * zones_row]
+    f_flat = input_F.rearrange("b q i j -> (b q i j)")
 
     with ExitStack() as stack:
         stack.enter_context(tc.manual_schedule())
         keep = stack.enter_context(tc.tile_pool(name="keep", bufs=1))
-        slabs = stack.enter_context(tc.tile_pool(name="slabs", bufs=3))
+        slabs = stack.enter_context(tc.tile_pool(name="slabs", bufs=2))
         soft = stack.enter_context(tc.tile_pool(name="soft", bufs=Q_TILES))
         stats = stack.enter_context(tc.tile_pool(name="stats", bufs=6))
-        sums = stack.enter_context(tc.tile_pool(name="sums", bufs=SUMS))
+        sums = stack.enter_context(tc.tile_pool(name="sums", bufs=1))
         products = stack.enter_context(tc.tile_pool(name="products", bufs=PRODUCTS))
         paired_products = stack.enter_context(tc.tile_pool(name="paired_products", bufs=4))
-        turned = stack.enter_context(tc.tile_pool(name="turned", bufs=2))
+        turned = stack.enter_context(tc.tile_pool(name="turned", bufs=3))
         operands = stack.enter_context(tc.tile_pool(name="operands", bufs=2))
-        codes = stack.enter_context(tc.tile_pool(name="codes", bufs=GROUP + 2))
+        codes = stack.enter_context(tc.tile_pool(name="codes", bufs=GROUP + 1))
+        grad_codes = stack.enter_context(tc.tile_pool(name="grad_codes", bufs=GROUP + 2))
         psum = stack.enter_context(tc.psum_pool(name="psum", bufs=1))
 
         ident_bf = keep.tile([P, P], BF16)
@@ -71,24 +93,41 @@ def tile_localcrf_kernel(tc, input_F, input_logit, compatibility, grad_out, out)
         for n in range(RING):
             nc.vector.memset(q_ring[n][:], 0.0)
 
+        def band_of(i):
+            found = [a for a in BAND_STARTS if a <= i < a + BAND]
+            return found[0] if found else None
+
+        def engine_of(i, di, dj):
+            r = i + di - REACH
+            if not 0 <= r < HEIGHT:
+                return None
+            if band_of(r) is not None:
+                if band_of(i) == band_of(r):
+                    return "matmul"
+                return "vector" if dj in BAND_COLUMNS else "product"
+            if [a for a in BAND_STARTS if a + BAND <= r < a + BAND + AFTER] and (dj not in AFTER_COLUMNS or band_of(i) is not None and dj not in KEPT_COLUMNS):
+                return "product"
+            return "vector" if dj in VECTOR_COLUMNS and (di, dj) not in VECTOR_LEAVES else "product"
+
         tables = [("target", dj) for dj in VECTOR_COLUMNS]
+        tables.extend([("target", dj) for dj in range(KERNEL) if dj not in VECTOR_COLUMNS and dj in BAND_COLUMNS])
+        targets = len(tables)
         for dj in range(KERNEL):
-            if dj not in VECTOR_COLUMNS or [tap for tap in VECTOR_LEAVES if tap[1] == dj]:
+            if [i for i in range(HEIGHT) for di in range(KERNEL) if engine_of(i, di, dj) == "product"]:
                 tables.extend([("source", dj)])
-        taps = keep.tile([P, len(tables), PAIRS, P], F32)
+        target_taps = keep.tile([P, targets, PAIRS, P], BF16)
+        source_taps = keep.tile([P, len(tables) - targets, PAIRS, P], F32)
+
+        def table(n):
+            return target_taps[:, n, :, :] if n < targets else source_taps[:, n - targets, :, :]
 
         def weight(kind, di, dj, i):
-            n = tables.index((kind, dj))
-            return taps[:, n, di // 2, WIDTH * (di % 2) + i : WIDTH * (di % 2) + i + 1]
+            return table(tables.index((kind, dj)))[:, di // 2, WIDTH * (di % 2) + i : WIDTH * (di % 2) + i + 1]
 
-        factor = keep.tile([P, CHUNKS, CHANNELS], F32)
         p_sum = keep.tile([P, CHUNKS, CHANNELS], F32)
-        f_raw = keep.tile([P, KERNEL * PAIRS, P], BF16)
-        f_wide = keep.tile([P, KERNEL * PAIRS, PAD + P + PAD], F32)
-        comp_bf = keep.tile([P, CHUNKS, CHANNELS], BF16)
-        nc.vector.memset(f_raw[:], 0.0)
-        nc.vector.memset(f_wide[:, :, 0:PAD], 0.0)
-        nc.vector.memset(f_wide[:, :, PAD + P :], 0.0)
+        early = {}
+        band_tiles = {}
+        factor = {}
 
         x_slab = {}
         x_px = {}
@@ -165,8 +204,8 @@ def tile_localcrf_kernel(tc, input_F, input_logit, compatibility, grad_out, out)
             )
 
         def quantise_grad(g):
-            g_codes = codes.tile([P, CHANNELS], U32, align_bytes=64)
-            g_scales = codes.tile([P, CHANNELS], U8, align_bytes=64)
+            g_codes = grad_codes.tile([P, CHANNELS], U32, align_bytes=64)
+            g_scales = grad_codes.tile([P, CHANNELS], U8, align_bytes=64)
             nc.vector.quantize_mx(
                 out=g_codes[:].bitcast(E5M2_X4), scales=g_scales[:], in_=g_grouped[g][:].rearrange("p o t -> p (o t)")
             )
@@ -183,44 +222,50 @@ def tile_localcrf_kernel(tc, input_F, input_logit, compatibility, grad_out, out)
             at(now[0] + delay, engine, job)
 
         side_c_free = [-1000]
+        side_b_free = [-1000]
 
         def reserve(earliest, hold, job):
             slot = max(earliest, side_c_free[0], now[0] + 1)
             side_c_free[0] = slot + hold
             at(slot, "tensor", job)
 
+        def columns_of(r):
+            return [
+                dj
+                for dj in list(VECTOR_COLUMNS) + [c for c in BAND_COLUMNS if c not in VECTOR_COLUMNS]
+                if [di for di in range(KERNEL) if 0 <= r + REACH - di < HEIGHT and engine_of(r + REACH - di, di, dj) == "vector"]
+            ]
+
         def vector_slots(r):
             ops = [
-                (w, di, dj, r + REACH - di)
-                for w, dj in enumerate(VECTOR_COLUMNS)
+                (di, dj, r + REACH - di)
+                for dj in columns_of(r)
                 for di in range(KERNEL - 1, -1, -1)
-                if 0 <= r + REACH - di < HEIGHT and (di, dj) not in VECTOR_LEAVES
+                if 0 <= r + REACH - di < HEIGHT and engine_of(r + REACH - di, di, dj) == "vector"
             ]
             return [ops[len(ops) * t // SLOTS : len(ops) * (t + 1) // SLOTS] for t in range(SLOTS)]
 
         def products_of(i):
-            return [
-                (di, dj)
-                for dj in range(KERNEL)
-                for di in range(KERNEL)
-                if 0 <= i + di - REACH < HEIGHT and (dj not in VECTOR_COLUMNS or (di, dj) in VECTOR_LEAVES)
-            ]
+            return [(di, dj) for dj in range(KERNEL) for di in range(KERNEL) if engine_of(i, di, dj) == "product"]
 
         vector_left = {}
         for r in range(HEIGHT):
             for ops in vector_slots(r):
-                for w, di, dj, i in ops:
+                for di, dj, i in ops:
                     vector_left[i] = vector_left.get(i, 0) + 1
+
         def merged_of(i):
             pairs = []
             for dj in MERGE_COLUMNS:
                 column = [tap for tap in products_of(i) if tap[1] == dj]
-                pairs.extend([(column[0], column[1])])
+                if len(column) > 1:
+                    pairs.extend([(column[0], column[1])])
             return pairs
 
         parts_left = {}
         for i in range(HEIGHT):
-            parts_left[i] = len(products_of(i)) - len(merged_of(i)) + 1
+            parts_left[i] = len(products_of(i)) - len(merged_of(i)) + (1 if i in vector_left else 0)
+        parts_in = dict(parts_left)
 
         todo = []
         todo_pairs = []
@@ -232,6 +277,8 @@ def tile_localcrf_kernel(tc, input_F, input_logit, compatibility, grad_out, out)
         finale = []
         window = {}
         sum_vector = {}
+        sum_slot = {}
+        free_sums = list(range(SUMS))
         m_total = {}
         total_bank = {}
         free_totals = ["total_a", "total_b"]
@@ -242,16 +289,18 @@ def tile_localcrf_kernel(tc, input_F, input_logit, compatibility, grad_out, out)
         p_group = {}
         done = {}
         last_pass = PASSES - 1
+        ready_early = [g for g in range(PASSES - GROUP, PASSES) if (g + 1) * PACK <= BAND_STARTS[-1]]
+        ready_late = [g for g in range(PASSES - GROUP, PASSES) if g not in ready_early]
 
         def count(key, goal):
             done[key] = done.get(key, 0) + 1
             return done[key] == goal
 
-        def make_window(r, w):
-            start = PAD + VECTOR_COLUMNS[w] - REACH
-            window[r, w] = psum.tile([P, CHANNELS], F32, name="window", tag="window%d" % w)
+        def make_window(r, dj, bank):
+            start = PAD + dj - REACH
+            window[r, dj] = psum.tile([P, CHANNELS], F32, name="window", tag="window%d" % bank)
             for k in range(CHUNKS):
-                nc.tensor.transpose(window[r, w][:, k * P : (k + 1) * P], q_ring[r % RING][:, k, start : start + P], ident_f32)
+                nc.tensor.transpose(window[r, dj][:, k * P : (k + 1) * P], q_ring[r % RING][:, k, start : start + P], ident_f32)
 
         def add_parts():
             room = ADDS
@@ -268,6 +317,8 @@ def tile_localcrf_kernel(tc, input_F, input_logit, compatibility, grad_out, out)
                     first = False
                 parts.remove(entry)
                 room -= 1
+                if part is sum_vector.get(i):
+                    free_sums.extend([sum_slot[i]])
                 parts_left[i] -= 1
                 for k in range(CHUNKS):
                     nc.tensor.matmul(
@@ -279,16 +330,51 @@ def tile_localcrf_kernel(tc, input_F, input_logit, compatibility, grad_out, out)
 
         def round_m(i):
             g = i // PACK
+            if band_of(i) is None:
+                nc.scalar.copy(out=turned_of(g)[:, :, i % PACK, :], in_=m_total[i][:])
+                free_totals.extend([total_bank[i]])
+                row_done(g)
+            else:
+                a = band_of(i)
+                nc.scalar.copy(out=band_tiles["sums"][:, :, i - a, :], in_=m_total[i][:])
+                free_totals.extend([total_bank[i]])
+                part_ready(a)
+
+        def reserve_patch(job):
+            slot = max(now[0] + 1, side_b_free[0])
+            while slot % SLOTS != PATCH_SLOT:
+                slot += 1
+            if max(now[0] + 1, side_c_free[0]) < slot:
+                reserve(now[0] + 1, 3, lambda: job("side_c"))
+            else:
+                side_b_free[0] = slot + 1
+                at(slot, "tensor", lambda: job("side_b"))
+
+        def part_ready(a):
+            if count(("ready", a), len([i for i in range(a, a + BAND) if parts_in[i] > 0]) + IMAGES + 1):
+                for b in range(IMAGES):
+                    for n in range(len(GROUPS)):
+                        reserve_patch(lambda bank, b=b, n=n: multiply_patch(a, b, n, bank))
+
+        def clear_kept(a):
+            empty = [i - a for i in range(a, a + BAND) if parts_in[i] == 0]
+            if empty:
+                nc.gpsimd.memset(band_tiles["sums"][:, :, empty[0] : empty[-1] + 1, :], 0.0)
+
+        def turned_of(g):
             if g not in m_turned:
                 m_turned[g] = turned.tile([P, CHUNKS, PACK, P], BF16, name="m_turned")
-            nc.scalar.copy(out=m_turned[g][:, :, i % PACK, :], in_=m_total[i][:])
-            free_totals.extend([total_bank[i]])
-            if count(("rounded", g), PACK):
-                m_grouped[g] = operands.tile([P, CHANNELS, PACK], BF16, name="m_grouped", align_bytes=64)
+            return m_turned[g]
+
+        def row_done(g):
+            rows = [i for i in range(g * PACK, (g + 1) * PACK) if band_of(i) is not None]
+            if count(("rounded", g), PACK - len(rows) + (IMAGES * len(GROUPS) if rows else 0)):
                 for h in range(2):
                     reserve(now[0] + 1, 4, lambda h=h: turn_m(g, h))
 
         def turn_m(g, h):
+            if h == 0:
+                m_grouped[g] = operands.tile([P, CHANNELS, PACK], BF16, name="m_grouped", align_bytes=64)
             m_words[g, h] = psum.tile([P, 2, HALF], F32, name="m_words", tag="side_c")
             count(("m turned", g), 2)
             turn_words(
@@ -308,9 +394,10 @@ def tile_localcrf_kernel(tc, input_F, input_logit, compatibility, grad_out, out)
                 out=m_codes[:].bitcast(E4M3_X4), scales=m_scales[:], in_=m_grouped[g][:].rearrange("p c t -> p (c t)")
             )
             m_operand[g] = (m_codes, m_scales)
-            if g % GROUP == GROUP - 1 and g != last_pass:
+            last = g - g % GROUP + GROUP - 1
+            if count(("quantised", last), GROUP) and last != last_pass:
                 for k in range(CHUNKS):
-                    reserve(now[0] + 2, 4, lambda k=k: early_group(g, k))
+                    reserve(now[0] + 2, 4, lambda k=k: early_group(last, k))
 
         def grad_chain(g, h):
             turn_grad(g, h)
@@ -349,30 +436,32 @@ def tile_localcrf_kernel(tc, input_F, input_logit, compatibility, grad_out, out)
             after(2, "vector", gather)
 
         def open_last_group(k):
-            p_group[k] = psum.tile([P, CHANNELS], F32, name="p_group", tag=("window%d" % k if k < len(VECTOR_COLUMNS) else "side_a"))
-            multiply(p_group[k], k, list(range(last_pass - GROUP + 1, last_pass)), True, False)
+            p_group[k] = psum.tile([P, CHANNELS], F32, name="p_group", tag=("window%d" % k if k < WINDOW_BANKS else "side_a"))
+            multiply(p_group[k], k, ready_early, True, False)
 
         def close_last_group(k):
-            multiply(p_group[k], k, [last_pass], False, True)
+            multiply(p_group[k], k, ready_late, False, True)
             nc.vector.tensor_tensor(out=p_sum[:, k, :], in0=p_group[k][:], in1=p_sum[:, k, :], op=ALU.add)
             nc.vector.scalar_tensor_tensor(
-                out=factor[:, k, :], in0=p_sum[:, k, :], scalar=-100.0, in1=factor[:, k, :], op0=ALU.mult, op1=ALU.mult
+                out=factor[k][:], in0=p_sum[:, k, :], scalar=-100.0, in1=factor[k][:], op0=ALU.mult, op1=ALU.mult
             )
-            nc.sync.dma_start(out=out_view[:, k, :], in_=factor[:, k, :])
+            nc.sync.dma_start(out=out_view[:, k, :], in_=factor[k][:])
 
         def vector_taps(r, t):
-            for w, di, dj, i in vector_slots(r)[t]:
+            for di, dj, i in vector_slots(r)[t]:
                 if i not in sum_vector:
-                    sum_vector[i] = sums.tile([P, CHANNELS], F32, name="sum_vector")
-                    nc.vector.tensor_scalar_mul(out=sum_vector[i][:], in0=window[r, w][:], scalar1=weight("target", di, dj, i))
+                    sum_slot[i] = free_sums[0]
+                    free_sums.remove(sum_slot[i])
+                    sum_vector[i] = sums.tile([P, CHANNELS], F32, name="sum_vector", tag="sum%d" % sum_slot[i])
+                    nc.vector.tensor_scalar_mul(out=sum_vector[i][:], in0=window[r, dj][:], scalar1=weight("target", di, dj, i))
                 else:
                     nc.vector.scalar_tensor_tensor(
-                        out=sum_vector[i][:], in0=window[r, w][:], scalar=weight("target", di, dj, i), in1=sum_vector[i][:],
+                        out=sum_vector[i][:], in0=window[r, dj][:], scalar=weight("target", di, dj, i), in1=sum_vector[i][:],
                         op0=ALU.mult, op1=ALU.add,
                     )
                 vector_left[i] -= 1
                 if vector_left[i] == 0:
-                    parts.extend([(now[0] + 2, i, sum_vector[i], 0)])
+                    parts.extend([(max(now[0] + 2, SLOTS * (i + REACH)), i, sum_vector[i], 0)])
 
         def make_products(scalar_room, gpsimd_room):
             credit[0] = min(credit[0], 0) + gpsimd_room
@@ -415,15 +504,6 @@ def tile_localcrf_kernel(tc, input_F, input_logit, compatibility, grad_out, out)
 
         first_slot = -20
         now[0] = first_slot - 1
-        load_logits(0)
-        for b in range(IMAGES):
-            for di in range(KERNEL):
-                nc.sync.dma_start(
-                    out=f_raw[WIDTH * (di % 2) : WIDTH * (di % 2) + WIDTH, di // 2 : KERNEL * PAIRS : PAIRS, b * WIDTH : (b + 1) * WIDTH],
-                    in_=input_F[b, di * KERNEL : (di + 1) * KERNEL].rearrange("q i j -> i q j"),
-                )
-        load_logits(1)
-        nc.sync.dma_start(out=comp_bf[:], in_=comp_view)
         ident_cols = ident_f32.rearrange("p (h j) -> p h j", j=WIDTH)
         outside = keep.tile([P, 2, KERNEL], F32)
         nc.vector.memset(outside[:], 0.0)
@@ -436,9 +516,149 @@ def tile_localcrf_kernel(tc, input_F, input_logit, compatibility, grad_out, out)
         inside = keep.tile([P, 2, KERNEL], F32)
         nc.vector.tensor_scalar(out=inside[:], in0=outside[:], scalar1=-1.0, scalar2=1.0, op0=ALU.mult, op1=ALU.add)
 
+        ident_patch = ident_f32[:, 0 : BAND * PATCH].rearrange("p (i j) -> p i j", j=PATCH)
+        leaves = keep.tile([P, KERNEL], F32)
+        nc.vector.memset(leaves[:], 0.0)
+        for e in range(KERNEL):
+            reach = abs(e - REACH)
+            if reach > 0:
+                edge = ident_patch[:, :, PATCH - reach : PATCH] if e > REACH else ident_patch[:, :, 0:reach]
+                nc.vector.tensor_reduce(out=leaves[:, e : e + 1], in_=edge, axis=AXIS.XY, op=ALU.add)
+        fits = keep.tile([P, KERNEL], F32)
+        nc.vector.tensor_scalar(out=fits[:], in0=leaves[:], scalar1=-1.0, scalar2=1.0, op0=ALU.mult, op1=ALU.add)
+
+        def open_head(head):
+            f_raw = head.tile([P, KERNEL * PAIRS, P], BF16)
+            f_wide = head.tile([P, KERNEL * PAIRS, PAD + P + PAD], F32)
+            early["f_raw"] = f_raw
+            early["f_wide"] = f_wide
+            nc.vector.memset(f_raw[:], 0.0)
+            nc.vector.memset(f_wide[:, :, 0:PAD], 0.0)
+            nc.vector.memset(f_wide[:, :, PAD + P :], 0.0)
+            load_logits(0)
+            for b in range(IMAGES):
+                for di in range(KERNEL):
+                    nc.sync.dma_start(
+                        out=f_raw[WIDTH * (di % 2) : WIDTH * (di % 2) + WIDTH, di // 2 : KERNEL * PAIRS : PAIRS, b * WIDTH : (b + 1) * WIDTH],
+                        in_=input_F[b, di * KERNEL : (di + 1) * KERNEL].rearrange("q i j -> i q j"),
+                    )
+            load_logits(1)
+
+        def open_bands(bands):
+            sources = bands.tile([P, IMAGES * len(GROUPS), CHANNELS], F32)
+            weights = bands.tile([P, IMAGES * len(GROUPS), P], F32)
+            zones = bands.tile([P, len(GROUPS), ZONE], F32)
+            f_band = bands.tile([P, IMAGES, BAND, WIDTH], BF16)
+            f_patch = bands.tile([P, IMAGES * len(GROUPS), P], BF16)
+            kept = bands.tile([P, CHUNKS, BAND, P], F32)
+            for key, tile in (("sources", sources), ("weights", weights), ("zones", zones), ("f_band", f_band), ("f_patch", f_patch), ("sums", kept)):
+                band_tiles[key] = tile
+            for tile in (sources, zones, f_band, f_patch):
+                nc.gpsimd.memset(tile[:], 0.0)
+
+        def make_factor():
+            comp_bf = slabs.tile([P, CHUNKS, CHANNELS], BF16, name="x_slab")
+            nc.sync.dma_start(out=comp_bf[:], in_=comp_view)
+            for k in range(CHUNKS):
+                factor[k] = paired_products.tile([P, CHANNELS], F32, name="product")
+                other = products.tile([P, CHANNELS], F32, name="product")
+                nc.scalar.activation(out=factor[k][:], in_=comp_bf[:, k, :], func=FUNC.Sigmoid, scale=100.0)
+                nc.scalar.activation(out=other[:], in_=comp_bf[:, k, :], func=FUNC.Sigmoid, scale=-100.0)
+                nc.gpsimd.tensor_tensor(out=factor[k][:], in0=factor[k][:], in1=other[:], op=ALU.mult)
+
+        def load_band_weights(a):
+            f_band = band_tiles["f_band"]
+            plane = HEIGHT * WIDTH
+            total = IMAGES * KERNEL * KERNEL * plane
+            for b in range(IMAGES):
+                for di in range(KERNEL):
+                    start = (b * KERNEL * KERNEL + di * KERNEL) * plane + (a - (di - REACH)) * WIDTH + REACH
+                    begin = min(start, total - KERNEL * (plane - 1))
+                    view = f_flat[begin : begin + KERNEL * (plane - 1)].rearrange("(d n) -> d n", n=plane - 1)
+                    view = view[:, start - begin : start - begin + BAND * WIDTH].rearrange("d (i j) -> d i j", j=WIDTH)
+                    nc.sync.dma_start(out=f_band[di * KERNEL : (di + 1) * KERNEL, b, :, :], in_=view)
+
+        def cut_band_weights(b):
+            for n in range(len(GROUPS)):
+                columns = min(PATCH, WIDTH - STRIDE * n)
+                f_patch = band_tiles["f_patch"][:, b * len(GROUPS) + n, 0 : BAND * PATCH].rearrange("p (i j) -> p i j", j=PATCH)
+                nc.gpsimd.tensor_copy(out=f_patch[:, :, 0:columns], in_=band_tiles["f_band"][:, b, :, STRIDE * n : STRIDE * n + columns])
+
+        def turn_band_weights(a, b):
+            f_turned = psum.tile([P, len(GROUPS), P], BF16, name="f_turned", tag="side_c")
+            for n in range(len(GROUPS)):
+                nc.tensor.transpose(f_turned[:, n, :], band_tiles["f_patch"][:, b * len(GROUPS) + n, :], ident_bf[:])
+
+            def spread():
+                first_word = CENTRE - REACH * PATCH - REACH
+                nc.vector.tensor_tensor(
+                    out=band_tiles["zones"][:, :, first_word : first_word + KERNEL * PATCH].rearrange("p g (d x) -> p g d x", x=PATCH)[:, :, :, 0:KERNEL],
+                    in0=f_turned[:, :, KERNEL * KERNEL - 1 :: -1].rearrange("p g (d e) -> p g d e", e=KERNEL),
+                    in1=fits[:].unsqueeze(1).unsqueeze(1).to_broadcast([P, len(GROUPS), KERNEL, KERNEL]),
+                    op=ALU.mult,
+                )
+                after(1, "sync", skew)
+
+            def skew():
+                nc.sync.dma_start(
+                    out=zones_flat[0 : P * zones_row].rearrange("(p x) -> p x", x=zones_row), in_=band_tiles["zones"][:].rearrange("p g z -> p (g z)")
+                )
+                skewed = zones_flat[CENTRE : CENTRE + P * (zones_row - 1)].rearrange("(p x) -> p x", x=zones_row - 1)
+                for n in range(len(GROUPS)):
+                    nc.sync.dma_start(
+                        out=band_tiles["weights"][:, b * len(GROUPS) + n, 0 : BAND * PATCH], in_=skewed[:, n * ZONE : n * ZONE + BAND * PATCH]
+                    )
+                part_ready(a)
+
+            after(2, "vector", spread)
+
+        def store_sources(r):
+            nc.sync.dma_start(out=out_rows[(r % 2) * P : (r % 2 + 1) * P, :], in_=q_px[r][:])
+
+        def gather_sources(a, r):
+            scratch = out_rows[(r % 2) * P : (r % 2 + 1) * P, :]
+            sources = band_tiles["sources"][(r - a) * PATCH : (r - a + 1) * PATCH, :, :]
+            for b in range(IMAGES):
+                image = scratch[b * WIDTH : (b + 1) * WIDTH, :]
+                patches = len(GROUPS)
+                first = b * patches
+                nc.sync.dma_start(
+                    out=sources[0:STRIDE, first : first + patches, :], in_=image[0 : patches * STRIDE, :].rearrange("(n j) c -> j n c", j=STRIDE)
+                )
+                rest = image[STRIDE : patches * STRIDE, :].rearrange("(n j) c -> j n c", j=STRIDE)
+                nc.sync.dma_start(out=sources[STRIDE:PATCH, first : first + patches - 1, :], in_=rest[0 : PATCH - STRIDE, :, :])
+                left = WIDTH - patches * STRIDE
+                nc.sync.dma_start(out=sources[STRIDE : STRIDE + left, first + patches - 1, :], in_=image[patches * STRIDE : WIDTH, :])
+
+        def multiply_patch(a, b, n, bank):
+            first_target, columns = GROUPS[n]
+            first = first_target - STRIDE * n
+            m_patch = psum.tile([P, CHUNKS, BAND, columns], F32, name="m_patch", tag=bank)
+            for k in range(CHUNKS):
+                nc.tensor.matmul(
+                    m_patch[:, k, :, :],
+                    lhsT=band_tiles["sources"][:, b * len(GROUPS) + n, k * P : (k + 1) * P],
+                    rhs=band_tiles["weights"][:, b * len(GROUPS) + n, 0 : BAND * PATCH].rearrange("p (i j) -> p i j", j=PATCH)[:, :, first : first + columns],
+                    start=True, stop=True,
+                )
+
+            def finish():
+                targets_at = b * WIDTH + first_target
+                for g in range(a // PACK, (a + BAND - 1) // PACK + 1):
+                    i0, i1 = max(a, g * PACK), min(a + BAND, (g + 1) * PACK)
+                    nc.vector.tensor_tensor(
+                        out=turned_of(g)[:, :, i0 % PACK : i0 % PACK + i1 - i0, targets_at : targets_at + columns],
+                        in0=m_patch[:, :, i0 - a : i1 - a, :],
+                        in1=band_tiles["sums"][:, :, i0 - a : i1 - a, targets_at : targets_at + columns],
+                        op=ALU.add,
+                    )
+                    row_done(g)
+
+            after(2, "vector", finish)
+
         def widen(dj):
             nc.gpsimd.tensor_scalar(
-                out=f_wide[:, dj * PAIRS : (dj + 1) * PAIRS, PAD : PAD + P], in0=f_raw[:, dj * PAIRS : (dj + 1) * PAIRS, :],
+                out=early["f_wide"][:, dj * PAIRS : (dj + 1) * PAIRS, PAD : PAD + P], in0=early["f_raw"][:, dj * PAIRS : (dj + 1) * PAIRS, :],
                 scalar1=1.0, scalar2=0.0, op0=ALU.mult, op1=ALU.add,
             )
 
@@ -447,34 +667,34 @@ def tile_localcrf_kernel(tc, input_F, input_logit, compatibility, grad_out, out)
             if kind == "target":
                 f_px = psum.tile([P, PAIRS, P], BF16, name="f_px", tag=bank)
                 for a in range(PAIRS):
-                    nc.tensor.transpose(f_px[:, a, :], f_raw[:, dj * PAIRS + a, :], ident_bf[:])
+                    nc.tensor.transpose(f_px[:, a, :], early["f_raw"][:, dj * PAIRS + a, :], ident_bf[:])
             else:
                 start = PAD - (dj - REACH)
                 f_px = psum.tile([P, PAIRS, P], F32, name="f_px", tag=bank)
                 for a in range(PAIRS):
-                    nc.tensor.transpose(f_px[:, a, :], f_wide[:, dj * PAIRS + a, start : start + P], ident_f32)
+                    nc.tensor.transpose(f_px[:, a, :], early["f_wide"][:, dj * PAIRS + a, start : start + P], ident_f32)
             after(
                 1, "scalar",
                 lambda: nc.scalar.activation(
-                    out=taps[:, n, :, :], in_=f_px[:], func=FUNC.Copy, scale=inside[:, (0 if kind == "target" else 1), dj : dj + 1]
+                    out=table(n), in_=f_px[:], func=FUNC.Copy, scale=inside[:, (0 if kind == "target" else 1), dj : dj + 1]
                 ),
             )
 
-        for n in range(len(tables)):
+        first = len(VECTOR_COLUMNS)
+        order = list(range(first)) + list(range(targets, len(tables))) + list(range(first, targets))
+        for q, n in enumerate(order):
             kind, dj = tables[n]
-            if kind == "target":
-                at(-13 + 2 * n, "tensor", lambda n=n: make_table(n, ("total_a", "total_b")[n % 2]))
-            else:
-                at(-9 + 2 * n, "gpsimd", lambda dj=dj: widen(dj))
-                at(-5 + 2 * n, "tensor", lambda n=n: make_table(n, ("total_a", "total_b")[n % 2]))
-        at(8, "scalar", lambda: nc.scalar.activation(out=factor[:], in_=comp_bf[:], func=FUNC.Sigmoid, scale=100.0))
-        at(9, "scalar", lambda: nc.scalar.activation(out=p_sum[:], in_=comp_bf[:], func=FUNC.Sigmoid, scale=-100.0))
-        at(12, "gpsimd", lambda: nc.gpsimd.tensor_tensor(out=factor[:], in0=factor[:], in1=p_sum[:], op=ALU.mult))
+            if q >= first and kind == "source":
+                at(-8 + q, "gpsimd", lambda dj=dj: widen(dj))
+            at(-13 + 2 * q if q < first else -4 + q, "tensor", lambda n=n, q=q: make_table(n, ("total_a", "total_b")[q % 2]))
+        head_end = -4 + len(order) + 2
 
+        windows_made = [0]
+        bank_free = {}
         for g in range(PASSES):
             if g > 1:
-                at(max(SLOTS * PACK * g - 60, first_slot), "sync", lambda g=g: load_logits(g))
-            at(max(SLOTS * PACK * g - 20, first_slot), "sync", lambda g=g: load_grad(g))
+                at(max(SLOTS * PACK * g - 50, first_slot), "sync", lambda g=g: load_logits(g))
+            at(SLOTS * PACK * g - 4, "sync", lambda g=g: load_grad(g))
         for r in range(HEIGHT):
             base = SLOTS * r
             at(base - 18, "tensor", lambda r=r: turn_logits(r))
@@ -484,15 +704,34 @@ def tile_localcrf_kernel(tc, input_F, input_logit, compatibility, grad_out, out)
             at(base - 11, "gpsimd", lambda r=r: normalise(r))
             at(base - 8, "tensor", lambda r=r: turn_q(r))
             at(base - 6, "scalar", lambda r=r: keep_q(r))
-            for w in range(len(VECTOR_COLUMNS)):
-                first_use = min([t for t in range(SLOTS) if [op for op in vector_slots(r)[t] if op[0] == w]])
-                at(base + first_use - 3, "tensor", lambda r=r, w=w: make_window(r, w))
+            for dj in columns_of(r):
+                uses = [t for t in range(SLOTS) if [tap for tap in vector_slots(r)[t] if tap[1] == dj]]
+                bank = windows_made[0] % WINDOW_BANKS
+                windows_made[0] += 1
+                at(max(base + uses[0] - 3, bank_free.get(bank, first_slot) + 1), "tensor", lambda r=r, dj=dj, bank=bank: make_window(r, dj, bank))
+                bank_free[bank] = base + uses[-1]
+        for a in BAND_STARTS:
+            base = SLOTS * a
+            at(max(base - 9, head_end + 1), "gpsimd", lambda a=a: clear_kept(a))
+            begin = max(base - 40, BAND_BEGIN)
+            at(begin, "sync", lambda a=a: load_band_weights(a))
+            for b in range(IMAGES):
+                at(begin + 8 + 2 * b, "gpsimd", lambda b=b: cut_band_weights(b))
+                at(begin + 12 + 10 * b, "tensor", lambda a=a, b=b: reserve(now[0] + 1, 4, lambda: turn_band_weights(a, b)))
+            for r in range(a, a + BAND):
+                slot = max(SLOTS * r - 9, head_end + 1)
+                at(slot, "sync", lambda r=r: store_sources(r))
+                if r > a:
+                    at(slot, "sync", lambda a=a, r=r: gather_sources(a, r - 1))
+            at(slot + 3, "sync", lambda a=a: gather_sources(a, a + BAND - 1))
+            at(slot + 3, "sync", lambda a=a: part_ready(a))
+        finale.extend([(lambda: not parts and not todo and not todo_pairs and not merges, make_factor)])
         for k in range(CHUNKS):
-            finale.extend([(lambda: not parts and not todo and not merges and last_pass - 1 in m_operand and last_pass - 1 in grad_operand, lambda k=k: open_last_group(k))])
+            finale.extend([(lambda: not [g for g in ready_early if g not in m_operand or g not in grad_operand], lambda k=k: open_last_group(k))])
         for k in range(CHUNKS):
-            finale.extend([(lambda: last_pass in m_operand and last_pass in grad_operand, lambda k=k: close_last_group(k))])
+            finale.extend([(lambda: not [g for g in ready_late if g not in m_operand or g not in grad_operand], lambda k=k: close_last_group(k))])
 
-        for slot in range(first_slot, SLOTS * (HEIGHT + 12)):
+        def write_slot(slot):
             now[0] = slot
             if (slot + EARLY) % SLOTS == 0 and 0 <= (slot + EARLY) // SLOTS - REACH < HEIGHT:
                 i = (slot + EARLY) // SLOTS - REACH
@@ -500,14 +739,14 @@ def tile_localcrf_kernel(tc, input_F, input_logit, compatibility, grad_out, out)
                 for pair in pairs:
                     todo_pairs.extend([(i, pair[0][0], pair[0][1]), (i, pair[1][0], pair[1][1])])
                 todo.extend([(i, di, dj) for di, dj in products_of(i) if not [pair for pair in pairs if (di, dj) in pair]])
-            if slot % (SLOTS * PACK) == 0 and 0 <= slot // (SLOTS * PACK) < PASSES:
+            if (slot - GRAD_DELAY) % (SLOTS * PACK) == 0 and 0 <= (slot - GRAD_DELAY) // (SLOTS * PACK) < PASSES:
                 for h in range(2):
-                    reserve(slot + 1, 4, lambda g=slot // (SLOTS * PACK), h=h: grad_chain(g, h))
+                    reserve(slot + 1, 4, lambda g=(slot - GRAD_DELAY) // (SLOTS * PACK), h=h: grad_chain(g, h))
             jobs = timed.get(slot, [])
             for engine, job in jobs:
                 job()
             add_parts()
-            assert len(parts) <= 2 * PRODUCTS - 6
+            assert len([part for part in parts if part[0] <= slot + 3]) <= 2 * PRODUCTS - 6
             if slot >= SLOTS * HEIGHT and finale and finale[0][0]():
                 job = finale[0]
                 finale.remove(job)
@@ -517,5 +756,14 @@ def tile_localcrf_kernel(tc, input_F, input_logit, compatibility, grad_out, out)
             )
             if 0 <= slot < SLOTS * HEIGHT:
                 vector_taps(slot // SLOTS, slot % SLOTS)
+
+        with tc.tile_pool(name="head", bufs=1) as head:
+            open_head(head)
+            for slot in range(first_slot, head_end):
+                write_slot(slot)
+        with tc.tile_pool(name="bands", bufs=1) as bands:
+            open_bands(bands)
+            for slot in range(head_end, SLOTS * (HEIGHT + 12)):
+                write_slot(slot)
         assert not (parts or todo or todo_pairs or merges or finale)
         assert max(timed) <= now[0]

@@ -26,15 +26,19 @@ SLOTS = 7
 GROUP = 4
 VECTOR_COLUMNS = (2, 3, 4)
 VECTOR_LEAVES = ((6, 4),)
-BAND = 6
+BAND = 8
+TARGETS = 6
 BAND_STARTS = (0, 20, 38, 58)
-BAND_COLUMNS = (0, 1, 2, 3, 4, 5, 6)
-AFTER = 3
+BAND_COLUMNS = (1, 2, 3, 4, 5)
+AFTER = 2
 AFTER_COLUMNS = (2, 3)
 KEPT_COLUMNS = ()
-PATCH = 21
+FRONT_COLUMNS = ((), (), (1, 2, 3, 4, 5), (1, 2, 3, 4, 5), (1, 2, 3, 4, 5))
+BACK_COLUMNS = ((), (), (2, 3, 4), (2, 3, 4), (2, 3, 4))
+PATCH = 16
 STRIDE = PATCH - 2 * REACH
-GROUPS = ((0, 18), (18, 15), (33, 15), (48, 16))
+GROUPS = ((0, 13), (13, 10), (23, 10), (33, 10), (43, 10), (53, 11))
+BATCH = 3
 ZONE = 192
 CENTRE = REACH * PATCH + REACH
 SCALAR_ROOM = 10
@@ -42,12 +46,15 @@ GPSIMD_ROOM = 4
 MERGE_COLUMNS = (0,)
 ADDS = 6
 GRAD_DELAY = 20
-BAND_BEGIN = 44
+BAND_LOAD = 10
+HOLD = 3
+AHEAD = 7
 PATCH_SLOT = 3
 EARLY = 3
-Q_TILES = 11
+Q_TILES = 12
 SUMS = 9
 PRODUCTS = 10
+TURNED = 3
 WINDOW_BANKS = 3
 RING = 3
 
@@ -61,7 +68,7 @@ def tile_localcrf_kernel(tc, input_F, input_logit, compatibility, grad_out, out)
     out_rows = out.rearrange("o c a b -> o (c a b)")
     out_flat = out.rearrange("o c a b -> (o c a b)")
     zones_at = 2 * P * CHANNELS
-    zones_row = len(GROUPS) * ZONE
+    zones_row = BATCH * ZONE
     zones_flat = out_flat[zones_at : zones_at + (P + 1) * zones_row]
     f_flat = input_F.rearrange("b q i j -> (b q i j)")
 
@@ -74,8 +81,8 @@ def tile_localcrf_kernel(tc, input_F, input_logit, compatibility, grad_out, out)
         sums = stack.enter_context(tc.tile_pool(name="sums", bufs=1))
         products = stack.enter_context(tc.tile_pool(name="products", bufs=PRODUCTS))
         paired_products = stack.enter_context(tc.tile_pool(name="paired_products", bufs=4))
-        turned = stack.enter_context(tc.tile_pool(name="turned", bufs=3))
-        operands = stack.enter_context(tc.tile_pool(name="operands", bufs=2))
+        turned = stack.enter_context(tc.tile_pool(name="turned", bufs=1))
+        operands = stack.enter_context(tc.tile_pool(name="operands", bufs=1))
         codes = stack.enter_context(tc.tile_pool(name="codes", bufs=GROUP + 1))
         grad_codes = stack.enter_context(tc.tile_pool(name="grad_codes", bufs=GROUP + 2))
         psum = stack.enter_context(tc.psum_pool(name="psum", bufs=1))
@@ -94,18 +101,27 @@ def tile_localcrf_kernel(tc, input_F, input_logit, compatibility, grad_out, out)
             nc.vector.memset(q_ring[n][:], 0.0)
 
         def band_of(i):
-            found = [a for a in BAND_STARTS if a <= i < a + BAND]
+            found = [a for a in BAND_STARTS if a <= i < a + TARGETS]
+            return found[0] if found else None
+
+        def sources_of(a):
+            return min(max(a - (BAND - TARGETS) // 2, 0), HEIGHT - BAND)
+
+        def source_band(r):
+            found = [a for a in BAND_STARTS if sources_of(a) <= r < sources_of(a) + BAND]
             return found[0] if found else None
 
         def engine_of(i, di, dj):
             r = i + di - REACH
             if not 0 <= r < HEIGHT:
                 return None
-            if band_of(r) is not None:
-                if band_of(i) == band_of(r):
+            a = source_band(r)
+            if a is not None:
+                if band_of(i) == a:
                     return "matmul"
-                return "vector" if dj in BAND_COLUMNS else "product"
-            if [a for a in BAND_STARTS if a + BAND <= r < a + BAND + AFTER] and (dj not in AFTER_COLUMNS or band_of(i) is not None and dj not in KEPT_COLUMNS):
+                outside = len([t for t in range(r - REACH, r + REACH + 1) if 0 <= t < HEIGHT and band_of(t) != a])
+                return "vector" if dj in (FRONT_COLUMNS if r - sources_of(a) < BAND // 2 else BACK_COLUMNS)[min(outside, 4)] else "product"
+            if [a for a in BAND_STARTS if sources_of(a) + BAND <= r < sources_of(a) + BAND + AFTER] and (dj not in AFTER_COLUMNS or band_of(i) is not None and dj not in KEPT_COLUMNS):
                 return "product"
             return "vector" if dj in VECTOR_COLUMNS and (di, dj) not in VECTOR_LEAVES else "product"
 
@@ -125,6 +141,13 @@ def tile_localcrf_kernel(tc, input_F, input_logit, compatibility, grad_out, out)
             return table(tables.index((kind, dj)))[:, di // 2, WIDTH * (di % 2) + i : WIDTH * (di % 2) + i + 1]
 
         p_sum = keep.tile([P, CHUNKS, CHANNELS], F32)
+        band_weights = keep.tile([P, IMAGES * len(GROUPS), P], F32)
+        zones = keep.tile([P, BATCH, ZONE], F32)
+        f_band = keep.tile([P, IMAGES, BAND, WIDTH], BF16)
+        f_patch = keep.tile([P, IMAGES * len(GROUPS), P], BF16)
+        nc.gpsimd.memset(f_band[:], 0.0)
+        nc.gpsimd.memset(f_patch[:], 0.0)
+        nc.gpsimd.memset(zones[:], 0.0)
         early = {}
         band_tiles = {}
         factor = {}
@@ -186,7 +209,6 @@ def tile_localcrf_kernel(tc, input_F, input_logit, compatibility, grad_out, out)
         def load_grad(g):
             g_slab[g] = slabs.tile([P, CHUNKS, PACK, IMAGES, WIDTH], BF16, name="g_slab")
             load(g_slab[g], grad_out, g)
-            g_grouped[g] = operands.tile([P, CHANNELS, PACK], BF16, name="g_grouped", align_bytes=64)
 
         def turn_words(bank, rows_of):
             for u in range(2):
@@ -196,8 +218,8 @@ def tile_localcrf_kernel(tc, input_F, input_logit, compatibility, grad_out, out)
         def group_words(grouped, h, bank):
             nc.scalar.copy(out=grouped[:].bitcast(F32)[:, h * HALF : (h + 1) * HALF, :], in_=bank[:].rearrange("p u c -> p c u"))
 
-        def turn_grad(g, h):
-            g_words[g, h] = psum.tile([P, 2, HALF], F32, name="g_words", tag="side_c")
+        def turn_grad(g, h, bank):
+            g_words[g, h] = psum.tile([P, 2, HALF], F32, name="g_words", tag=bank)
             turn_words(
                 g_words[g, h],
                 lambda k, u: g_slab[g][:, h * (HALF // P) + k, 2 * u : 2 * u + 2, :, :].rearrange("p s b j -> p (s b j)"),
@@ -221,13 +243,13 @@ def tile_localcrf_kernel(tc, input_F, input_logit, compatibility, grad_out, out)
         def after(delay, engine, job):
             at(now[0] + delay, engine, job)
 
-        side_c_free = [-1000]
         side_b_free = [-1000]
+        bank_free = {"side_c": -1000, "side_b": SLOTS * HEIGHT - SLOTS, "window0": SLOTS * HEIGHT + 1, "window1": SLOTS * HEIGHT + 1}
 
         def reserve(earliest, hold, job):
-            slot = max(earliest, side_c_free[0], now[0] + 1)
-            side_c_free[0] = slot + hold
-            at(slot, "tensor", job)
+            slot, bank = min([(max(earliest, bank_free[bank], now[0] + 1), bank) for bank in bank_free])
+            bank_free[bank] = slot + hold
+            at(slot, "tensor", lambda: job(bank))
 
         def columns_of(r):
             return [
@@ -282,6 +304,8 @@ def tile_localcrf_kernel(tc, input_F, input_logit, compatibility, grad_out, out)
         m_total = {}
         total_bank = {}
         free_totals = ["total_a", "total_b"]
+        turned_slot = {}
+        free_turned = list(range(TURNED))
         m_turned = {}
         m_words = {}
         m_grouped = {}
@@ -344,45 +368,51 @@ def tile_localcrf_kernel(tc, input_F, input_logit, compatibility, grad_out, out)
             slot = max(now[0] + 1, side_b_free[0])
             while slot % SLOTS != PATCH_SLOT:
                 slot += 1
-            if max(now[0] + 1, side_c_free[0]) < slot:
-                reserve(now[0] + 1, 3, lambda: job("side_c"))
+            if min([max(now[0] + 1, bank_free[bank]) for bank in bank_free]) < slot or slot >= SLOTS * HEIGHT - SLOTS:
+                reserve(now[0] + 1, HOLD, job)
             else:
                 side_b_free[0] = slot + 1
                 at(slot, "tensor", lambda: job("side_b"))
 
         def part_ready(a):
-            if count(("ready", a), len([i for i in range(a, a + BAND) if parts_in[i] > 0]) + IMAGES + 1):
+            if count(("ready", a), len([i for i in range(a, a + TARGETS) if parts_in[i] > 0]) + IMAGES * len(GROUPS) // BATCH + 1):
                 for b in range(IMAGES):
                     for n in range(len(GROUPS)):
                         reserve_patch(lambda bank, b=b, n=n: multiply_patch(a, b, n, bank))
 
         def clear_kept(a):
-            empty = [i - a for i in range(a, a + BAND) if parts_in[i] == 0]
+            empty = [i - a for i in range(a, a + TARGETS) if parts_in[i] == 0]
             if empty:
                 nc.gpsimd.memset(band_tiles["sums"][:, :, empty[0] : empty[-1] + 1, :], 0.0)
 
         def turned_of(g):
             if g not in m_turned:
-                m_turned[g] = turned.tile([P, CHUNKS, PACK, P], BF16, name="m_turned")
+                turned_slot[g] = free_turned[0]
+                free_turned.remove(turned_slot[g])
+                m_turned[g] = turned.tile([P, CHUNKS, PACK, P], BF16, name="m_turned", tag="turned%d" % turned_slot[g])
             return m_turned[g]
 
         def row_done(g):
             rows = [i for i in range(g * PACK, (g + 1) * PACK) if band_of(i) is not None]
             if count(("rounded", g), PACK - len(rows) + (IMAGES * len(GROUPS) if rows else 0)):
                 for h in range(2):
-                    reserve(now[0] + 1, 4, lambda h=h: turn_m(g, h))
+                    reserve(now[0] + 1, HOLD, lambda bank, h=h: turn_m(g, h, bank))
 
-        def turn_m(g, h):
-            if h == 0:
-                m_grouped[g] = operands.tile([P, CHANNELS, PACK], BF16, name="m_grouped", align_bytes=64)
-            m_words[g, h] = psum.tile([P, 2, HALF], F32, name="m_words", tag="side_c")
+        def turn_m(g, h, bank):
+            m_words[g, h] = psum.tile([P, 2, HALF], F32, name="m_words", tag=bank)
             count(("m turned", g), 2)
             turn_words(
                 m_words[g, h], lambda k, u: m_turned[g][:, h * (HALF // P) + k, 2 * u : 2 * u + 2, :].rearrange("p s n -> p (s n)")
             )
+            if h == 1:
+                free_turned.extend([turned_slot[g]])
             after(2, "scalar", lambda: group_m(g, h))
 
         def group_m(g, h):
+            if h == 0:
+                m_grouped[g] = operands.tile(
+                    [P, CHANNELS, PACK], BF16, name="m_grouped", tag=("g_grouped" if g == last_pass else "m_grouped"), align_bytes=64
+                )
             group_words(m_grouped[g], h, m_words[g, h])
             if h == 1:
                 after(2, "vector", lambda: quantise_m(g))
@@ -397,12 +427,14 @@ def tile_localcrf_kernel(tc, input_F, input_logit, compatibility, grad_out, out)
             last = g - g % GROUP + GROUP - 1
             if count(("quantised", last), GROUP) and last != last_pass:
                 for k in range(CHUNKS):
-                    reserve(now[0] + 2, 4, lambda k=k: early_group(last, k))
+                    reserve(now[0] + 2, HOLD, lambda bank, k=k: early_group(last, k, bank))
 
-        def grad_chain(g, h):
-            turn_grad(g, h)
+        def grad_chain(g, h, bank):
+            turn_grad(g, h, bank)
 
             def group():
+                if h == 0:
+                    g_grouped[g] = operands.tile([P, CHANNELS, PACK], BF16, name="g_grouped", align_bytes=64)
                 group_words(g_grouped[g], h, g_words[g, h])
                 if h == 1:
                     after(2, "vector", lambda: quantise_grad(g))
@@ -423,8 +455,8 @@ def tile_localcrf_kernel(tc, input_F, input_logit, compatibility, grad_out, out)
                     stop=(stop and g == passes[-1]),
                 )
 
-        def early_group(last, k):
-            p_early = psum.tile([P, CHANNELS], F32, name="p_early", tag="side_c")
+        def early_group(last, k, bank):
+            p_early = psum.tile([P, CHANNELS], F32, name="p_early", tag=bank)
             multiply(p_early, k, list(range(last - GROUP + 1, last + 1)), True, True)
 
             def gather():
@@ -436,7 +468,7 @@ def tile_localcrf_kernel(tc, input_F, input_logit, compatibility, grad_out, out)
             after(2, "vector", gather)
 
         def open_last_group(k):
-            p_group[k] = psum.tile([P, CHANNELS], F32, name="p_group", tag=("window%d" % k if k < WINDOW_BANKS else "side_a"))
+            p_group[k] = psum.tile([P, CHANNELS], F32, name="p_group", tag=("total_a", "total_b", "side_a", "window2")[k])
             multiply(p_group[k], k, ready_early, True, False)
 
         def close_last_group(k):
@@ -502,7 +534,7 @@ def tile_localcrf_kernel(tc, input_F, input_logit, compatibility, grad_out, out)
                     else:
                         parts.extend([(now[0] + 2, i, product, (dj - REACH) % P)])
 
-        first_slot = -20
+        first_slot = -20 - AHEAD
         now[0] = first_slot - 1
         ident_cols = ident_f32.rearrange("p (h j) -> p h j", j=WIDTH)
         outside = keep.tile([P, 2, KERNEL], F32)
@@ -546,15 +578,10 @@ def tile_localcrf_kernel(tc, input_F, input_logit, compatibility, grad_out, out)
 
         def open_bands(bands):
             sources = bands.tile([P, IMAGES * len(GROUPS), CHANNELS], F32)
-            weights = bands.tile([P, IMAGES * len(GROUPS), P], F32)
-            zones = bands.tile([P, len(GROUPS), ZONE], F32)
-            f_band = bands.tile([P, IMAGES, BAND, WIDTH], BF16)
-            f_patch = bands.tile([P, IMAGES * len(GROUPS), P], BF16)
-            kept = bands.tile([P, CHUNKS, BAND, P], F32)
-            for key, tile in (("sources", sources), ("weights", weights), ("zones", zones), ("f_band", f_band), ("f_patch", f_patch), ("sums", kept)):
-                band_tiles[key] = tile
-            for tile in (sources, zones, f_band, f_patch):
-                nc.gpsimd.memset(tile[:], 0.0)
+            kept = bands.tile([P, CHUNKS, TARGETS, P], F32)
+            band_tiles["sources"] = sources
+            band_tiles["sums"] = kept
+            nc.gpsimd.memset(sources[:], 0.0)
 
         def make_factor():
             comp_bf = slabs.tile([P, CHUNKS, CHANNELS], BF16, name="x_slab")
@@ -566,13 +593,12 @@ def tile_localcrf_kernel(tc, input_F, input_logit, compatibility, grad_out, out)
                 nc.scalar.activation(out=other[:], in_=comp_bf[:, k, :], func=FUNC.Sigmoid, scale=-100.0)
                 nc.gpsimd.tensor_tensor(out=factor[k][:], in0=factor[k][:], in1=other[:], op=ALU.mult)
 
-        def load_band_weights(a):
-            f_band = band_tiles["f_band"]
+        def load_band_weights(s):
             plane = HEIGHT * WIDTH
             total = IMAGES * KERNEL * KERNEL * plane
             for b in range(IMAGES):
                 for di in range(KERNEL):
-                    start = (b * KERNEL * KERNEL + di * KERNEL) * plane + (a - (di - REACH)) * WIDTH + REACH
+                    start = (b * KERNEL * KERNEL + di * KERNEL) * plane + (s - (di - REACH)) * WIDTH + REACH
                     begin = min(start, total - KERNEL * (plane - 1))
                     view = f_flat[begin : begin + KERNEL * (plane - 1)].rearrange("(d n) -> d n", n=plane - 1)
                     view = view[:, start - begin : start - begin + BAND * WIDTH].rearrange("d (i j) -> d i j", j=WIDTH)
@@ -581,32 +607,32 @@ def tile_localcrf_kernel(tc, input_F, input_logit, compatibility, grad_out, out)
         def cut_band_weights(b):
             for n in range(len(GROUPS)):
                 columns = min(PATCH, WIDTH - STRIDE * n)
-                f_patch = band_tiles["f_patch"][:, b * len(GROUPS) + n, 0 : BAND * PATCH].rearrange("p (i j) -> p i j", j=PATCH)
-                nc.gpsimd.tensor_copy(out=f_patch[:, :, 0:columns], in_=band_tiles["f_band"][:, b, :, STRIDE * n : STRIDE * n + columns])
+                patch = f_patch[:, b * len(GROUPS) + n, 0 : BAND * PATCH].rearrange("p (i j) -> p i j", j=PATCH)
+                nc.gpsimd.tensor_copy(out=patch[:, :, 0:columns], in_=f_band[:, b, :, STRIDE * n : STRIDE * n + columns])
 
-        def turn_band_weights(a, b):
-            f_turned = psum.tile([P, len(GROUPS), P], BF16, name="f_turned", tag="side_c")
-            for n in range(len(GROUPS)):
-                nc.tensor.transpose(f_turned[:, n, :], band_tiles["f_patch"][:, b * len(GROUPS) + n, :], ident_bf[:])
+        def turn_band_weights(a, first, bank):
+            f_turned = psum.tile([P, BATCH, P], BF16, name="f_turned", tag=bank)
+            for n in range(BATCH):
+                nc.tensor.transpose(f_turned[:, n, :], f_patch[:, first + n, :], ident_bf[:])
 
             def spread():
                 first_word = CENTRE - REACH * PATCH - REACH
                 nc.vector.tensor_tensor(
-                    out=band_tiles["zones"][:, :, first_word : first_word + KERNEL * PATCH].rearrange("p g (d x) -> p g d x", x=PATCH)[:, :, :, 0:KERNEL],
+                    out=zones[:, :, first_word : first_word + KERNEL * PATCH].rearrange("p g (d x) -> p g d x", x=PATCH)[:, :, :, 0:KERNEL],
                     in0=f_turned[:, :, KERNEL * KERNEL - 1 :: -1].rearrange("p g (d e) -> p g d e", e=KERNEL),
-                    in1=fits[:].unsqueeze(1).unsqueeze(1).to_broadcast([P, len(GROUPS), KERNEL, KERNEL]),
+                    in1=fits[:].unsqueeze(1).unsqueeze(1).to_broadcast([P, BATCH, KERNEL, KERNEL]),
                     op=ALU.mult,
                 )
                 after(1, "sync", skew)
 
             def skew():
                 nc.sync.dma_start(
-                    out=zones_flat[0 : P * zones_row].rearrange("(p x) -> p x", x=zones_row), in_=band_tiles["zones"][:].rearrange("p g z -> p (g z)")
+                    out=zones_flat[0 : P * zones_row].rearrange("(p x) -> p x", x=zones_row), in_=zones[:].rearrange("p g z -> p (g z)")
                 )
                 skewed = zones_flat[CENTRE : CENTRE + P * (zones_row - 1)].rearrange("(p x) -> p x", x=zones_row - 1)
-                for n in range(len(GROUPS)):
+                for n in range(BATCH):
                     nc.sync.dma_start(
-                        out=band_tiles["weights"][:, b * len(GROUPS) + n, 0 : BAND * PATCH], in_=skewed[:, n * ZONE : n * ZONE + BAND * PATCH]
+                        out=band_weights[:, first + n, 0 : BAND * PATCH], in_=skewed[:, n * ZONE : n * ZONE + BAND * PATCH]
                     )
                 part_ready(a)
 
@@ -615,9 +641,9 @@ def tile_localcrf_kernel(tc, input_F, input_logit, compatibility, grad_out, out)
         def store_sources(r):
             nc.sync.dma_start(out=out_rows[(r % 2) * P : (r % 2 + 1) * P, :], in_=q_px[r][:])
 
-        def gather_sources(a, r):
+        def gather_sources(s, r):
             scratch = out_rows[(r % 2) * P : (r % 2 + 1) * P, :]
-            sources = band_tiles["sources"][(r - a) * PATCH : (r - a + 1) * PATCH, :, :]
+            sources = band_tiles["sources"][(r - s) * PATCH : (r - s + 1) * PATCH, :, :]
             for b in range(IMAGES):
                 image = scratch[b * WIDTH : (b + 1) * WIDTH, :]
                 patches = len(GROUPS)
@@ -633,19 +659,20 @@ def tile_localcrf_kernel(tc, input_F, input_logit, compatibility, grad_out, out)
         def multiply_patch(a, b, n, bank):
             first_target, columns = GROUPS[n]
             first = first_target - STRIDE * n
-            m_patch = psum.tile([P, CHUNKS, BAND, columns], F32, name="m_patch", tag=bank)
+            row = a - sources_of(a)
+            m_patch = psum.tile([P, CHUNKS, TARGETS, columns], F32, name="m_patch", tag=bank)
             for k in range(CHUNKS):
                 nc.tensor.matmul(
                     m_patch[:, k, :, :],
                     lhsT=band_tiles["sources"][:, b * len(GROUPS) + n, k * P : (k + 1) * P],
-                    rhs=band_tiles["weights"][:, b * len(GROUPS) + n, 0 : BAND * PATCH].rearrange("p (i j) -> p i j", j=PATCH)[:, :, first : first + columns],
+                    rhs=band_weights[:, b * len(GROUPS) + n, 0 : BAND * PATCH].rearrange("p (i j) -> p i j", j=PATCH)[:, row : row + TARGETS, first : first + columns],
                     start=True, stop=True,
                 )
 
             def finish():
                 targets_at = b * WIDTH + first_target
-                for g in range(a // PACK, (a + BAND - 1) // PACK + 1):
-                    i0, i1 = max(a, g * PACK), min(a + BAND, (g + 1) * PACK)
+                for g in range(a // PACK, (a + TARGETS - 1) // PACK + 1):
+                    i0, i1 = max(a, g * PACK), min(a + TARGETS, (g + 1) * PACK)
                     nc.vector.tensor_tensor(
                         out=turned_of(g)[:, :, i0 % PACK : i0 % PACK + i1 - i0, targets_at : targets_at + columns],
                         in0=m_patch[:, :, i0 - a : i1 - a, :],
@@ -690,40 +717,42 @@ def tile_localcrf_kernel(tc, input_F, input_logit, compatibility, grad_out, out)
         head_end = -4 + len(order) + 2
 
         windows_made = [0]
-        bank_free = {}
+        window_free = {}
         for g in range(PASSES):
             if g > 1:
-                at(max(SLOTS * PACK * g - 50, first_slot), "sync", lambda g=g: load_logits(g))
-            at(SLOTS * PACK * g - 4, "sync", lambda g=g: load_grad(g))
+                at(SLOTS * PACK * g - 50 - AHEAD, "sync", lambda g=g: load_logits(g))
+            at(SLOTS * PACK * g - (4 if g < PASSES - 2 else 16), "sync", lambda g=g: load_grad(g))
         for r in range(HEIGHT):
             base = SLOTS * r
-            at(base - 18, "tensor", lambda r=r: turn_logits(r))
-            at(base - 16, "vector", lambda r=r: find_top(r))
-            at(base - 14, "scalar", lambda r=r: exponentials(r))
-            at(base - 12, "vector", lambda r=r: invert(r))
-            at(base - 11, "gpsimd", lambda r=r: normalise(r))
+            at(base - 18 - AHEAD, "tensor", lambda r=r: turn_logits(r))
+            at(base - 16 - AHEAD, "vector", lambda r=r: find_top(r))
+            at(base - 14 - AHEAD, "scalar", lambda r=r: exponentials(r))
+            at(base - 12 - AHEAD, "vector", lambda r=r: invert(r))
+            at(base - 11 - AHEAD, "gpsimd", lambda r=r: normalise(r))
             at(base - 8, "tensor", lambda r=r: turn_q(r))
             at(base - 6, "scalar", lambda r=r: keep_q(r))
             for dj in columns_of(r):
                 uses = [t for t in range(SLOTS) if [tap for tap in vector_slots(r)[t] if tap[1] == dj]]
                 bank = windows_made[0] % WINDOW_BANKS
                 windows_made[0] += 1
-                at(max(base + uses[0] - 3, bank_free.get(bank, first_slot) + 1), "tensor", lambda r=r, dj=dj, bank=bank: make_window(r, dj, bank))
-                bank_free[bank] = base + uses[-1]
+                at(max(base + uses[0] - 3, window_free.get(bank, first_slot) + 1), "tensor", lambda r=r, dj=dj, bank=bank: make_window(r, dj, bank))
+                window_free[bank] = base + uses[-1]
         for a in BAND_STARTS:
             base = SLOTS * a
-            at(max(base - 9, head_end + 1), "gpsimd", lambda a=a: clear_kept(a))
-            begin = max(base - 40, BAND_BEGIN)
-            at(begin, "sync", lambda a=a: load_band_weights(a))
+            at(max(base - 20, head_end + 1), "gpsimd", lambda a=a: clear_kept(a))
+            begin = max(base - 60, first_slot)
+            s = sources_of(a)
+            at(begin, "sync", lambda s=s: load_band_weights(s))
             for b in range(IMAGES):
-                at(begin + 8 + 2 * b, "gpsimd", lambda b=b: cut_band_weights(b))
-                at(begin + 12 + 10 * b, "tensor", lambda a=a, b=b: reserve(now[0] + 1, 4, lambda: turn_band_weights(a, b)))
-            for r in range(a, a + BAND):
-                slot = max(SLOTS * r - 9, head_end + 1)
+                at(begin + BAND_LOAD + 2 * b, "gpsimd", lambda b=b: cut_band_weights(b))
+            for q in range(IMAGES * len(GROUPS) // BATCH):
+                at(begin + BAND_LOAD + 5 + 8 * q, "tensor", lambda a=a, q=q: reserve(now[0] + 1, HOLD, lambda bank: turn_band_weights(a, q * BATCH, bank)))
+            for r in range(s, s + BAND):
+                slot = max(SLOTS * r - 9 - AHEAD, head_end + 1)
                 at(slot, "sync", lambda r=r: store_sources(r))
-                if r > a:
-                    at(slot, "sync", lambda a=a, r=r: gather_sources(a, r - 1))
-            at(slot + 3, "sync", lambda a=a: gather_sources(a, a + BAND - 1))
+                if r > s:
+                    at(slot, "sync", lambda s=s, r=r: gather_sources(s, r - 1))
+            at(slot + 3, "sync", lambda s=s: gather_sources(s, s + BAND - 1))
             at(slot + 3, "sync", lambda a=a: part_ready(a))
         finale.extend([(lambda: not parts and not todo and not todo_pairs and not merges, make_factor)])
         for k in range(CHUNKS):
@@ -739,9 +768,10 @@ def tile_localcrf_kernel(tc, input_F, input_logit, compatibility, grad_out, out)
                 for pair in pairs:
                     todo_pairs.extend([(i, pair[0][0], pair[0][1]), (i, pair[1][0], pair[1][1])])
                 todo.extend([(i, di, dj) for di, dj in products_of(i) if not [pair for pair in pairs if (di, dj) in pair]])
-            if (slot - GRAD_DELAY) % (SLOTS * PACK) == 0 and 0 <= (slot - GRAD_DELAY) // (SLOTS * PACK) < PASSES:
-                for h in range(2):
-                    reserve(slot + 1, 4, lambda g=(slot - GRAD_DELAY) // (SLOTS * PACK), h=h: grad_chain(g, h))
+            for g in range(PASSES):
+                if slot == SLOTS * PACK * g + (GRAD_DELAY if g < PASSES - 2 else 0):
+                    for h in range(2):
+                        reserve(slot + 1, HOLD, lambda bank, g=g, h=h: grad_chain(g, h, bank))
             jobs = timed.get(slot, [])
             for engine, job in jobs:
                 job()

@@ -29,31 +29,35 @@ VECTOR_LEAVES = ((6, 4),)
 BAND = 8
 TARGETS = 6
 BAND_STARTS = (0, 20, 38, 58)
-BAND_COLUMNS = (1, 2, 3, 4, 5)
-AFTER = 2
-AFTER_COLUMNS = (2, 3)
-KEPT_COLUMNS = ()
-FRONT_COLUMNS = ((), (), (1, 2, 3, 4, 5), (1, 2, 3, 4, 5), (1, 2, 3, 4, 5))
-BACK_COLUMNS = ((), (), (2, 3, 4), (2, 3, 4), (2, 3, 4))
 PATCH = 16
 STRIDE = PATCH - 2 * REACH
 GROUPS = ((0, 13), (13, 10), (23, 10), (33, 10), (43, 10), (53, 11))
-BATCH = 3
-ZONE = 192
-CENTRE = REACH * PATCH + REACH
+BATCH = 2
+SCRATCH = 3
+SCRATCH_ROW = P + 2
+ZONE = 160
+CENTRE = REACH * BAND + REACH
 SCALAR_ROOM = 10
 GPSIMD_ROOM = 4
 MERGE_COLUMNS = (0,)
 ADDS = 6
-GRAD_DELAY = 20
+GRAD_DELAY = 48
 BAND_LOAD = 10
+BAND_BEGIN = 60
+BAND_STEP = 7
+FIRST_BAND = 8
+LEAST = 2
+SPACING = 5
+FIRST_STEP = 8
+FIRST_PATCH = 10
 HOLD = 3
 AHEAD = 7
 PATCH_SLOT = 3
 EARLY = 3
-Q_TILES = 12
-SUMS = 9
-PRODUCTS = 10
+Q_TILES = 16
+SUMS = 11
+PAIRED = 4
+PRODUCTS = 9
 TURNED = 3
 WINDOW_BANKS = 3
 RING = 3
@@ -67,9 +71,9 @@ def tile_localcrf_kernel(tc, input_F, input_logit, compatibility, grad_out, out)
     out_view = out.rearrange("(k o) c a b -> o k (c a b)", o=P)
     out_rows = out.rearrange("o c a b -> o (c a b)")
     out_flat = out.rearrange("o c a b -> (o c a b)")
-    zones_at = 2 * P * CHANNELS
+    zones_at = SCRATCH * SCRATCH_ROW * CHANNELS
     zones_row = BATCH * ZONE
-    zones_flat = out_flat[zones_at : zones_at + (P + 1) * zones_row]
+    zones_flat = out_flat[zones_at : zones_at + P * zones_row]
     f_flat = input_F.rearrange("b q i j -> (b q i j)")
 
     with ExitStack() as stack:
@@ -80,11 +84,11 @@ def tile_localcrf_kernel(tc, input_F, input_logit, compatibility, grad_out, out)
         stats = stack.enter_context(tc.tile_pool(name="stats", bufs=6))
         sums = stack.enter_context(tc.tile_pool(name="sums", bufs=1))
         products = stack.enter_context(tc.tile_pool(name="products", bufs=PRODUCTS))
-        paired_products = stack.enter_context(tc.tile_pool(name="paired_products", bufs=4))
+        paired_products = stack.enter_context(tc.tile_pool(name="paired_products", bufs=PAIRED))
         turned = stack.enter_context(tc.tile_pool(name="turned", bufs=1))
         operands = stack.enter_context(tc.tile_pool(name="operands", bufs=1))
         codes = stack.enter_context(tc.tile_pool(name="codes", bufs=GROUP + 1))
-        grad_codes = stack.enter_context(tc.tile_pool(name="grad_codes", bufs=GROUP + 2))
+        grad_codes = stack.enter_context(tc.tile_pool(name="grad_codes", bufs=GROUP + 1))
         psum = stack.enter_context(tc.psum_pool(name="psum", bufs=1))
 
         ident_bf = keep.tile([P, P], BF16)
@@ -115,18 +119,11 @@ def tile_localcrf_kernel(tc, input_F, input_logit, compatibility, grad_out, out)
             r = i + di - REACH
             if not 0 <= r < HEIGHT:
                 return None
-            a = source_band(r)
-            if a is not None:
-                if band_of(i) == a:
-                    return "matmul"
-                outside = len([t for t in range(r - REACH, r + REACH + 1) if 0 <= t < HEIGHT and band_of(t) != a])
-                return "vector" if dj in (FRONT_COLUMNS if r - sources_of(a) < BAND // 2 else BACK_COLUMNS)[min(outside, 4)] else "product"
-            if [a for a in BAND_STARTS if sources_of(a) + BAND <= r < sources_of(a) + BAND + AFTER] and (dj not in AFTER_COLUMNS or band_of(i) is not None and dj not in KEPT_COLUMNS):
-                return "product"
+            if source_band(r) is not None and source_band(r) == band_of(i):
+                return "matmul"
             return "vector" if dj in VECTOR_COLUMNS and (di, dj) not in VECTOR_LEAVES else "product"
 
         tables = [("target", dj) for dj in VECTOR_COLUMNS]
-        tables.extend([("target", dj) for dj in range(KERNEL) if dj not in VECTOR_COLUMNS and dj in BAND_COLUMNS])
         targets = len(tables)
         for dj in range(KERNEL):
             if [i for i in range(HEIGHT) for di in range(KERNEL) if engine_of(i, di, dj) == "product"]:
@@ -142,12 +139,13 @@ def tile_localcrf_kernel(tc, input_F, input_logit, compatibility, grad_out, out)
 
         p_sum = keep.tile([P, CHUNKS, CHANNELS], F32)
         band_weights = keep.tile([P, IMAGES * len(GROUPS), P], F32)
-        zones = keep.tile([P, BATCH, ZONE], F32)
+        zones = [keep.tile([P, BATCH, ZONE], F32, name="zones%d" % n) for n in range(2)]
         f_band = keep.tile([P, IMAGES, BAND, WIDTH], BF16)
         f_patch = keep.tile([P, IMAGES * len(GROUPS), P], BF16)
         nc.gpsimd.memset(f_band[:], 0.0)
         nc.gpsimd.memset(f_patch[:], 0.0)
-        nc.gpsimd.memset(zones[:], 0.0)
+        for n in range(2):
+            nc.gpsimd.memset(zones[n][:], 0.0)
         early = {}
         band_tiles = {}
         factor = {}
@@ -175,6 +173,8 @@ def tile_localcrf_kernel(tc, input_F, input_logit, compatibility, grad_out, out)
 
         def turn_logits(r):
             x_px[r] = psum.tile([P, CHANNELS], BF16, name="x_px", tag="side_a")
+            if r % PACK == PACK - 1 and r // PACK + 2 < PASSES:
+                after(1, "sync", lambda: load_logits(r // PACK + 2))
             for k in range(CHUNKS):
                 nc.tensor.transpose(
                     x_px[r][:, k * P : (k + 1) * P], x_slab[r // PACK][:, k, r % PACK, :, :].rearrange("p b j -> p (b j)"), ident_bf[:]
@@ -243,18 +243,32 @@ def tile_localcrf_kernel(tc, input_F, input_logit, compatibility, grad_out, out)
         def after(delay, engine, job):
             at(now[0] + delay, engine, job)
 
-        side_b_free = [-1000]
-        bank_free = {"side_c": -1000, "side_b": SLOTS * HEIGHT - SLOTS, "window0": SLOTS * HEIGHT + 1, "window1": SLOTS * HEIGHT + 1}
+        busy = {"side_c": [], "side_b": [], "side_a": [], "window0": [], "window1": []}
 
         def reserve(earliest, hold, job):
-            slot, bank = min([(max(earliest, bank_free[bank], now[0] + 1), bank) for bank in bank_free])
-            bank_free[bank] = slot + hold
+            choice = []
+            for bank in busy:
+                slot = max(earliest, now[0] + 1)
+                for first, last in sorted(busy[bank]):
+                    if slot < last and first < slot + hold:
+                        slot = last
+                choice.extend([(slot, bank)])
+            slot, bank = min(choice)
+            busy[bank].extend([(slot, slot + hold)])
             at(slot, "tensor", lambda: job(bank))
+            return slot
+
+        words_free = {"m": -1000, "g": -1000}
+
+        def reserve_words(kind, job):
+            for h in range(2):
+                words_free[kind] = reserve(max(now[0] + 1, words_free[kind]), HOLD, lambda bank, h=h: job(h, bank))
+            words_free[kind] += 3
 
         def columns_of(r):
             return [
                 dj
-                for dj in list(VECTOR_COLUMNS) + [c for c in BAND_COLUMNS if c not in VECTOR_COLUMNS]
+                for dj in VECTOR_COLUMNS
                 if [di for di in range(KERNEL) if 0 <= r + REACH - di < HEIGHT and engine_of(r + REACH - di, di, dj) == "vector"]
             ]
 
@@ -265,7 +279,8 @@ def tile_localcrf_kernel(tc, input_F, input_logit, compatibility, grad_out, out)
                 for di in range(KERNEL - 1, -1, -1)
                 if 0 <= r + REACH - di < HEIGHT and engine_of(r + REACH - di, di, dj) == "vector"
             ]
-            return [ops[len(ops) * t // SLOTS : len(ops) * (t + 1) // SLOTS] for t in range(SLOTS)]
+            slots = max(LEAST, len(set([i for di, dj, i in ops])))
+            return [ops[len(ops) * t // slots : len(ops) * (t + 1) // slots] for t in range(slots)]
 
         def products_of(i):
             return [(di, dj) for dj in range(KERNEL) for di in range(KERNEL) if engine_of(i, di, dj) == "product"]
@@ -343,6 +358,12 @@ def tile_localcrf_kernel(tc, input_F, input_logit, compatibility, grad_out, out)
                 room -= 1
                 if part is sum_vector.get(i):
                     free_sums.extend([sum_slot[i]])
+                gone = [part]
+                for pair in halves.values():
+                    if pair[0] is part:
+                        gone = pair
+                for kind in unadded:
+                    unadded[kind] = [None if [tile for tile in gone if tile is product] else product for product in unadded[kind]]
                 parts_left[i] -= 1
                 for k in range(CHUNKS):
                     nc.tensor.matmul(
@@ -364,21 +385,11 @@ def tile_localcrf_kernel(tc, input_F, input_logit, compatibility, grad_out, out)
                 free_totals.extend([total_bank[i]])
                 part_ready(a)
 
-        def reserve_patch(job):
-            slot = max(now[0] + 1, side_b_free[0])
-            while slot % SLOTS != PATCH_SLOT:
-                slot += 1
-            if min([max(now[0] + 1, bank_free[bank]) for bank in bank_free]) < slot or slot >= SLOTS * HEIGHT - SLOTS:
-                reserve(now[0] + 1, HOLD, job)
-            else:
-                side_b_free[0] = slot + 1
-                at(slot, "tensor", lambda: job("side_b"))
-
         def part_ready(a):
             if count(("ready", a), len([i for i in range(a, a + TARGETS) if parts_in[i] > 0]) + IMAGES * len(GROUPS) // BATCH + 1):
                 for b in range(IMAGES):
                     for n in range(len(GROUPS)):
-                        reserve_patch(lambda bank, b=b, n=n: multiply_patch(a, b, n, bank))
+                        reserve(now[0] + (FIRST_PATCH if a == 0 else 1), HOLD, lambda bank, b=b, n=n: multiply_patch(a, b, n, bank))
 
         def clear_kept(a):
             empty = [i - a for i in range(a, a + TARGETS) if parts_in[i] == 0]
@@ -395,8 +406,7 @@ def tile_localcrf_kernel(tc, input_F, input_logit, compatibility, grad_out, out)
         def row_done(g):
             rows = [i for i in range(g * PACK, (g + 1) * PACK) if band_of(i) is not None]
             if count(("rounded", g), PACK - len(rows) + (IMAGES * len(GROUPS) if rows else 0)):
-                for h in range(2):
-                    reserve(now[0] + 1, HOLD, lambda bank, h=h: turn_m(g, h, bank))
+                reserve_words("m", lambda h, bank: turn_m(g, h, bank))
 
         def turn_m(g, h, bank):
             m_words[g, h] = psum.tile([P, 2, HALF], F32, name="m_words", tag=bank)
@@ -411,7 +421,7 @@ def tile_localcrf_kernel(tc, input_F, input_logit, compatibility, grad_out, out)
         def group_m(g, h):
             if h == 0:
                 m_grouped[g] = operands.tile(
-                    [P, CHANNELS, PACK], BF16, name="m_grouped", tag=("g_grouped" if g == last_pass else "m_grouped"), align_bytes=64
+                    [P, CHANNELS, PACK], BF16, name="m_grouped", align_bytes=64
                 )
             group_words(m_grouped[g], h, m_words[g, h])
             if h == 1:
@@ -431,6 +441,8 @@ def tile_localcrf_kernel(tc, input_F, input_logit, compatibility, grad_out, out)
 
         def grad_chain(g, h, bank):
             turn_grad(g, h, bank)
+            if h == 1 and g + 2 < PASSES:
+                after(1, "sync", lambda: load_grad(g + 2))
 
             def group():
                 if h == 0:
@@ -493,7 +505,12 @@ def tile_localcrf_kernel(tc, input_F, input_logit, compatibility, grad_out, out)
                     )
                 vector_left[i] -= 1
                 if vector_left[i] == 0:
-                    parts.extend([(max(now[0] + 2, SLOTS * (i + REACH)), i, sum_vector[i], 0)])
+                    parts.extend([(max(now[0] + 2, product_start[i] + EARLY), i, sum_vector[i], 0)])
+
+        unadded = {"scalar": [], "gpsimd": [], "pair": []}
+
+        def has_room(kind, tiles):
+            return len(unadded[kind]) < tiles or unadded[kind][-tiles] is None
 
         def make_products(scalar_room, gpsimd_room):
             credit[0] = min(credit[0], 0) + gpsimd_room
@@ -505,7 +522,7 @@ def tile_localcrf_kernel(tc, input_F, input_logit, compatibility, grad_out, out)
                     nc.gpsimd.tensor_tensor(out=pair[0][:], in0=pair[0][:], in1=pair[1][:], op=ALU.add)
                     parts.extend([(now[0] + 3, i, pair[0], (dj - REACH) % P)])
                     credit[0] -= 3
-                elif todo:
+                elif todo and has_room("gpsimd", PRODUCTS):
                     i, di, dj = todo[0]
                     todo.remove(todo[0])
                     product_g = products.tile([P, CHANNELS], F32)
@@ -513,6 +530,7 @@ def tile_localcrf_kernel(tc, input_F, input_logit, compatibility, grad_out, out)
                         out=product_g[:], in0=q_px[i + di - REACH][:], scalar1=weight("source", di, dj, i), scalar2=0.0,
                         op0=ALU.mult, op1=ALU.add,
                     )
+                    unadded["gpsimd"].extend([product_g])
                     parts.extend([(now[0] + 3, i, product_g, (dj - REACH) % P)])
                     credit[0] -= 2
                 else:
@@ -520,13 +538,14 @@ def tile_localcrf_kernel(tc, input_F, input_logit, compatibility, grad_out, out)
             credit_scalar[0] = min(credit_scalar[0], 2) + scalar_room
             while credit_scalar[0] >= 3:
                 credit_scalar[0] -= 3
-                if todo_pairs or todo:
-                    paired = len(todo_pairs) > 0
+                paired = len(todo_pairs) > 0 and has_room("pair", PAIRED)
+                if paired or (todo and has_room("scalar", PRODUCTS)):
                     queue = todo_pairs if paired else todo
                     i, di, dj = queue[0]
                     queue.remove(queue[0])
                     product = (paired_products if paired else products).tile([P, CHANNELS], F32, name="product")
                     nc.scalar.activation(out=product[:], in_=q_px[i + di - REACH][:], func=FUNC.Copy, scale=weight("source", di, dj, i))
+                    unadded["pair" if paired else "scalar"].extend([product])
                     if paired:
                         halves.setdefault((i, dj), []).extend([product])
                         if len(halves[i, dj]) == 2:
@@ -534,7 +553,59 @@ def tile_localcrf_kernel(tc, input_F, input_logit, compatibility, grad_out, out)
                     else:
                         parts.extend([(now[0] + 2, i, product, (dj - REACH) % P)])
 
-        first_slot = -20 - AHEAD
+        nominal = [0]
+        for r in range(HEIGHT):
+            nominal.extend([nominal[r] + len(vector_slots(r))])
+        turn_slot = {}
+        for r in reversed(range(HEIGHT)):
+            turn_slot[r] = nominal[r] - 18 - AHEAD
+            if r + 1 < HEIGHT:
+                turn_slot[r] = min(turn_slot[r], turn_slot[r + 1] - SPACING)
+        q_slot = {}
+        keep_slot = {}
+        vector_start = {}
+        vector_plan = {}
+        window_plan = []
+        window_free = {}
+        last_window = {}
+        clock = 0
+        for r in range(HEIGHT):
+            uses = {}
+            for t, ops in enumerate(vector_slots(r)):
+                for di, dj, i in ops:
+                    uses.setdefault(dj, []).extend([t])
+            q_slot[r] = max(clock - 8, turn_slot[r] + 9, keep_slot.get(r - 1, -1000) + 1)
+            keep_slot[r] = max(q_slot[r] + 2, last_window.get(r - RING, -1000) + 1)
+            start = clock
+            made = []
+            for n, dj in enumerate(uses):
+                bank = (len(window_plan) + n) % WINDOW_BANKS
+                slot = max(clock + uses[dj][0] - 3, keep_slot[r] + 2, window_free.get(bank, -1000) + 1)
+                start = max(start, slot + 1 - uses[dj][0])
+                window_free[bank] = start + uses[dj][-1]
+                made.extend([(slot, r, dj, bank)])
+            for n, dj in enumerate(uses):
+                window_free[made[n][3]] = start + uses[dj][-1]
+            window_plan.extend(made)
+            last_window[r] = max([slot for slot, row, dj, bank in made] + [keep_slot[r]])
+            vector_start[r] = start
+            for t in range(len(vector_slots(r))):
+                vector_plan[start + t] = (r, t)
+            clock = start + len(vector_slots(r))
+        vector_end = clock
+        product_start = {}
+        clock = -1000
+        for i in range(HEIGHT):
+            product_start[i] = max(clock, vector_start.get(i + REACH, vector_end) - EARLY)
+            clock = product_start[i] + len(set([di for di, dj in products_of(i)]))
+        for r in range(HEIGHT):
+            busy["side_a"].extend([(turn_slot[r], turn_slot[r] + 5)])
+            busy["side_b"].extend([(q_slot[r], keep_slot[r] + 1)])
+        busy["side_a"].extend([(turn_slot[HEIGHT - 1], 10000)])
+        for n in range(2):
+            busy["window%d" % n].extend([(-1000, vector_end + 1)])
+
+        first_slot = turn_slot[0] - 2
         now[0] = first_slot - 1
         ident_cols = ident_f32.rearrange("p (h j) -> p h j", j=WIDTH)
         outside = keep.tile([P, 2, KERNEL], F32)
@@ -548,14 +619,14 @@ def tile_localcrf_kernel(tc, input_F, input_logit, compatibility, grad_out, out)
         inside = keep.tile([P, 2, KERNEL], F32)
         nc.vector.tensor_scalar(out=inside[:], in0=outside[:], scalar1=-1.0, scalar2=1.0, op0=ALU.mult, op1=ALU.add)
 
-        ident_patch = ident_f32[:, 0 : BAND * PATCH].rearrange("p (i j) -> p i j", j=PATCH)
+        ident_patch = ident_f32.rearrange("p (j i) -> p j i", i=BAND)
         leaves = keep.tile([P, KERNEL], F32)
         nc.vector.memset(leaves[:], 0.0)
-        for e in range(KERNEL):
-            reach = abs(e - REACH)
+        for d in range(KERNEL):
+            reach = abs(d - REACH)
             if reach > 0:
-                edge = ident_patch[:, :, PATCH - reach : PATCH] if e > REACH else ident_patch[:, :, 0:reach]
-                nc.vector.tensor_reduce(out=leaves[:, e : e + 1], in_=edge, axis=AXIS.XY, op=ALU.add)
+                edge = ident_patch[:, :, BAND - reach : BAND] if d > REACH else ident_patch[:, :, 0:reach]
+                nc.vector.tensor_reduce(out=leaves[:, d : d + 1], in_=edge, axis=AXIS.XY, op=ALU.add)
         fits = keep.tile([P, KERNEL], F32)
         nc.vector.tensor_scalar(out=fits[:], in0=leaves[:], scalar1=-1.0, scalar2=1.0, op0=ALU.mult, op1=ALU.add)
 
@@ -568,6 +639,7 @@ def tile_localcrf_kernel(tc, input_F, input_logit, compatibility, grad_out, out)
             nc.vector.memset(f_wide[:, :, 0:PAD], 0.0)
             nc.vector.memset(f_wide[:, :, PAD + P :], 0.0)
             load_logits(0)
+            load_band_weights(0)
             for b in range(IMAGES):
                 for di in range(KERNEL):
                     nc.sync.dma_start(
@@ -582,6 +654,7 @@ def tile_localcrf_kernel(tc, input_F, input_logit, compatibility, grad_out, out)
             band_tiles["sources"] = sources
             band_tiles["sums"] = kept
             nc.gpsimd.memset(sources[:], 0.0)
+            clear_scratch()
 
         def make_factor():
             comp_bf = slabs.tile([P, CHUNKS, CHANNELS], BF16, name="x_slab")
@@ -607,8 +680,17 @@ def tile_localcrf_kernel(tc, input_F, input_logit, compatibility, grad_out, out)
         def cut_band_weights(b):
             for n in range(len(GROUPS)):
                 columns = min(PATCH, WIDTH - STRIDE * n)
-                patch = f_patch[:, b * len(GROUPS) + n, 0 : BAND * PATCH].rearrange("p (i j) -> p i j", j=PATCH)
-                nc.gpsimd.tensor_copy(out=patch[:, :, 0:columns], in_=f_band[:, b, :, STRIDE * n : STRIDE * n + columns])
+                nc.gpsimd.tensor_copy(
+                    out=f_patch[:, b * len(GROUPS) + n, 0 : columns * BAND].rearrange("p (j i) -> p j i", i=BAND),
+                    in_=f_band[:, b, :, STRIDE * n : STRIDE * n + columns].rearrange("p i j -> p j i"),
+                )
+
+        pending = []
+
+        def read_zones():
+            for read in list(pending):
+                pending.remove(read)
+                read()
 
         def turn_band_weights(a, first, bank):
             f_turned = psum.tile([P, BATCH, P], BF16, name="f_turned", tag=bank)
@@ -616,56 +698,60 @@ def tile_localcrf_kernel(tc, input_F, input_logit, compatibility, grad_out, out)
                 nc.tensor.transpose(f_turned[:, n, :], f_patch[:, first + n, :], ident_bf[:])
 
             def spread():
-                first_word = CENTRE - REACH * PATCH - REACH
+                first_word = CENTRE - REACH * BAND - REACH
                 nc.vector.tensor_tensor(
-                    out=zones[:, :, first_word : first_word + KERNEL * PATCH].rearrange("p g (d x) -> p g d x", x=PATCH)[:, :, :, 0:KERNEL],
-                    in0=f_turned[:, :, KERNEL * KERNEL - 1 :: -1].rearrange("p g (d e) -> p g d e", e=KERNEL),
+                    out=zones[first // BATCH % 2][:, :, first_word : first_word + KERNEL * BAND].rearrange("p g (e x) -> p g e x", x=BAND)[:, :, :, 0:KERNEL],
+                    in0=f_turned[:, :, KERNEL * KERNEL - 1 :: -1].rearrange("p g (d e) -> p g e d", e=KERNEL),
                     in1=fits[:].unsqueeze(1).unsqueeze(1).to_broadcast([P, BATCH, KERNEL, KERNEL]),
                     op=ALU.mult,
                 )
                 after(1, "sync", skew)
 
+
             def skew():
+                read_zones()
                 nc.sync.dma_start(
-                    out=zones_flat[0 : P * zones_row].rearrange("(p x) -> p x", x=zones_row), in_=zones[:].rearrange("p g z -> p (g z)")
+                    out=zones_flat.rearrange("(p x) -> p x", x=zones_row), in_=zones[first // BATCH % 2][:].rearrange("p g z -> p (g z)")
                 )
-                skewed = zones_flat[CENTRE : CENTRE + P * (zones_row - 1)].rearrange("(p x) -> p x", x=zones_row - 1)
+                pending.extend([unskew])
+                after(2, "sync", read_zones)
+
+            def unskew():
+                assert not [n for n in BAND_STARTS if n < a and done.get(("multiplied", n), 0) < IMAGES * len(GROUPS)]
+                view = zones_flat[CENTRE : CENTRE + P * (zones_row - 1)].rearrange("(p x) -> p x", x=zones_row - 1)
                 for n in range(BATCH):
-                    nc.sync.dma_start(
-                        out=band_weights[:, first + n, 0 : BAND * PATCH], in_=skewed[:, n * ZONE : n * ZONE + BAND * PATCH]
-                    )
+                    nc.sync.dma_start(out=band_weights[:, first + n, 0 : BAND * PATCH], in_=view[:, n * ZONE : n * ZONE + BAND * PATCH])
                 part_ready(a)
 
             after(2, "vector", spread)
 
+        def clear_scratch():
+            for n in range(SCRATCH):
+                nc.sync.dma_start(out=out_rows[n * SCRATCH_ROW + P : (n + 1) * SCRATCH_ROW, :], in_=band_tiles["sources"][0 : SCRATCH_ROW - P, 0, :])
+
         def store_sources(r):
-            nc.sync.dma_start(out=out_rows[(r % 2) * P : (r % 2 + 1) * P, :], in_=q_px[r][:])
+            first = r % SCRATCH * SCRATCH_ROW
+            nc.sync.dma_start(out=out_rows[first : first + P, :], in_=q_px[r][:])
 
         def gather_sources(s, r):
-            scratch = out_rows[(r % 2) * P : (r % 2 + 1) * P, :]
-            sources = band_tiles["sources"][(r - s) * PATCH : (r - s + 1) * PATCH, :, :]
+            sources = band_tiles["sources"][r - s : P : BAND, :, :]
+            patches = len(GROUPS)
             for b in range(IMAGES):
-                image = scratch[b * WIDTH : (b + 1) * WIDTH, :]
-                patches = len(GROUPS)
-                first = b * patches
-                nc.sync.dma_start(
-                    out=sources[0:STRIDE, first : first + patches, :], in_=image[0 : patches * STRIDE, :].rearrange("(n j) c -> j n c", j=STRIDE)
-                )
-                rest = image[STRIDE : patches * STRIDE, :].rearrange("(n j) c -> j n c", j=STRIDE)
-                nc.sync.dma_start(out=sources[STRIDE:PATCH, first : first + patches - 1, :], in_=rest[0 : PATCH - STRIDE, :, :])
-                left = WIDTH - patches * STRIDE
-                nc.sync.dma_start(out=sources[STRIDE : STRIDE + left, first + patches - 1, :], in_=image[patches * STRIDE : WIDTH, :])
+                first = r % SCRATCH * SCRATCH_ROW + b * WIDTH
+                for start, stop in ((0, STRIDE), (STRIDE, PATCH)):
+                    view = out_rows[first + start : first + start + patches * STRIDE, :].rearrange("(n j) c -> j n c", j=STRIDE)
+                    nc.sync.dma_start(out=sources[start:stop, b * patches : (b + 1) * patches, :], in_=view[0 : stop - start, :, :])
 
         def multiply_patch(a, b, n, bank):
             first_target, columns = GROUPS[n]
             first = first_target - STRIDE * n
             row = a - sources_of(a)
-            m_patch = psum.tile([P, CHUNKS, TARGETS, columns], F32, name="m_patch", tag=bank)
+            m_patch = psum.tile([P, CHUNKS, columns, TARGETS], F32, name="m_patch", tag=bank)
             for k in range(CHUNKS):
                 nc.tensor.matmul(
                     m_patch[:, k, :, :],
                     lhsT=band_tiles["sources"][:, b * len(GROUPS) + n, k * P : (k + 1) * P],
-                    rhs=band_weights[:, b * len(GROUPS) + n, 0 : BAND * PATCH].rearrange("p (i j) -> p i j", j=PATCH)[:, row : row + TARGETS, first : first + columns],
+                    rhs=band_weights[:, b * len(GROUPS) + n, 0 : BAND * PATCH].rearrange("p (j i) -> p j i", i=BAND)[:, first : first + columns, row : row + TARGETS],
                     start=True, stop=True,
                 )
 
@@ -675,18 +761,18 @@ def tile_localcrf_kernel(tc, input_F, input_logit, compatibility, grad_out, out)
                     i0, i1 = max(a, g * PACK), min(a + TARGETS, (g + 1) * PACK)
                     nc.vector.tensor_tensor(
                         out=turned_of(g)[:, :, i0 % PACK : i0 % PACK + i1 - i0, targets_at : targets_at + columns],
-                        in0=m_patch[:, :, i0 - a : i1 - a, :],
+                        in0=m_patch[:, :, :, i0 - a : i1 - a].rearrange("p k j i -> p k i j"),
                         in1=band_tiles["sums"][:, :, i0 - a : i1 - a, targets_at : targets_at + columns],
                         op=ALU.add,
                     )
                     row_done(g)
 
+            count(("multiplied", a), 0)
             after(2, "vector", finish)
 
         def widen(dj):
-            nc.gpsimd.tensor_scalar(
-                out=early["f_wide"][:, dj * PAIRS : (dj + 1) * PAIRS, PAD : PAD + P], in0=early["f_raw"][:, dj * PAIRS : (dj + 1) * PAIRS, :],
-                scalar1=1.0, scalar2=0.0, op0=ALU.mult, op1=ALU.add,
+            nc.vector.tensor_copy(
+                out=early["f_wide"][:, dj * PAIRS : (dj + 1) * PAIRS, PAD : PAD + P], in_=early["f_raw"][:, dj * PAIRS : (dj + 1) * PAIRS, :]
             )
 
         def make_table(n, bank):
@@ -712,80 +798,76 @@ def tile_localcrf_kernel(tc, input_F, input_logit, compatibility, grad_out, out)
         for q, n in enumerate(order):
             kind, dj = tables[n]
             if q >= first and kind == "source":
-                at(-8 + q, "gpsimd", lambda dj=dj: widen(dj))
+                at(-8 + q, "vector", lambda dj=dj: widen(dj))
             at(-13 + 2 * q if q < first else -4 + q, "tensor", lambda n=n, q=q: make_table(n, ("total_a", "total_b")[q % 2]))
         head_end = -4 + len(order) + 2
 
-        windows_made = [0]
-        window_free = {}
-        for g in range(PASSES):
-            if g > 1:
-                at(SLOTS * PACK * g - 50 - AHEAD, "sync", lambda g=g: load_logits(g))
-            at(SLOTS * PACK * g - (4 if g < PASSES - 2 else 16), "sync", lambda g=g: load_grad(g))
+        for g in range(2):
+            at(first_slot + 20 * g, "sync", lambda g=g: load_grad(g))
         for r in range(HEIGHT):
-            base = SLOTS * r
-            at(base - 18 - AHEAD, "tensor", lambda r=r: turn_logits(r))
-            at(base - 16 - AHEAD, "vector", lambda r=r: find_top(r))
-            at(base - 14 - AHEAD, "scalar", lambda r=r: exponentials(r))
-            at(base - 12 - AHEAD, "vector", lambda r=r: invert(r))
-            at(base - 11 - AHEAD, "gpsimd", lambda r=r: normalise(r))
-            at(base - 8, "tensor", lambda r=r: turn_q(r))
-            at(base - 6, "scalar", lambda r=r: keep_q(r))
-            for dj in columns_of(r):
-                uses = [t for t in range(SLOTS) if [tap for tap in vector_slots(r)[t] if tap[1] == dj]]
-                bank = windows_made[0] % WINDOW_BANKS
-                windows_made[0] += 1
-                at(max(base + uses[0] - 3, window_free.get(bank, first_slot) + 1), "tensor", lambda r=r, dj=dj, bank=bank: make_window(r, dj, bank))
-                window_free[bank] = base + uses[-1]
+            at(turn_slot[r], "tensor", lambda r=r: turn_logits(r))
+            at(turn_slot[r] + 2, "vector", lambda r=r: find_top(r))
+            at(turn_slot[r] + 4, "scalar", lambda r=r: exponentials(r))
+            at(turn_slot[r] + 6, "vector", lambda r=r: invert(r))
+            at(turn_slot[r] + 7, "gpsimd", lambda r=r: normalise(r))
+            at(q_slot[r], "tensor", lambda r=r: turn_q(r))
+            at(keep_slot[r], "scalar", lambda r=r: keep_q(r))
+        for slot, r, dj, bank in window_plan:
+            at(slot, "tensor", lambda r=r, dj=dj, bank=bank: make_window(r, dj, bank))
+        moves = []
         for a in BAND_STARTS:
-            base = SLOTS * a
-            at(max(base - 20, head_end + 1), "gpsimd", lambda a=a: clear_kept(a))
-            begin = max(base - 60, first_slot)
+            at(max(product_start[a] - 2, head_end + 1), "gpsimd", lambda a=a: clear_kept(a))
+            begin = vector_start[a] - BAND_BEGIN
             s = sources_of(a)
-            at(begin, "sync", lambda s=s: load_band_weights(s))
+            if a > 0:
+                at(begin, "sync", lambda s=s: load_band_weights(s))
+            loaded = begin + BAND_LOAD if a > 0 else first_slot + FIRST_BAND
             for b in range(IMAGES):
-                at(begin + BAND_LOAD + 2 * b, "gpsimd", lambda b=b: cut_band_weights(b))
+                at(loaded + 2 * b, "gpsimd", lambda b=b: cut_band_weights(b))
             for q in range(IMAGES * len(GROUPS) // BATCH):
-                at(begin + BAND_LOAD + 5 + 8 * q, "tensor", lambda a=a, q=q: reserve(now[0] + 1, HOLD, lambda bank: turn_band_weights(a, q * BATCH, bank)))
+                at(
+                    loaded + 5 + (BAND_STEP if a > 0 else FIRST_STEP) * q, "tensor",
+                    lambda a=a, q=q: reserve(now[0] + 1, HOLD, lambda bank: turn_band_weights(a, q * BATCH, bank)),
+                )
             for r in range(s, s + BAND):
-                slot = max(SLOTS * r - 9 - AHEAD, head_end + 1)
-                at(slot, "sync", lambda r=r: store_sources(r))
+                slot = max(turn_slot[r] + 9, head_end + 1)
+                moves.extend([(slot, a, lambda r=r: store_sources(r))])
                 if r > s:
-                    at(slot, "sync", lambda s=s, r=r: gather_sources(s, r - 1))
-            at(slot + 3, "sync", lambda s=s: gather_sources(s, s + BAND - 1))
-            at(slot + 3, "sync", lambda a=a: part_ready(a))
+                    moves.extend([(slot, a, lambda s=s, r=r: gather_sources(s, r - 1))])
+            moves.extend([(slot + 3, a, lambda s=s: gather_sources(s, s + BAND - 1)), (slot + 3, a, lambda a=a: part_ready(a))])
         finale.extend([(lambda: not parts and not todo and not todo_pairs and not merges, make_factor)])
         for k in range(CHUNKS):
-            finale.extend([(lambda: not [g for g in ready_early if g not in m_operand or g not in grad_operand], lambda k=k: open_last_group(k))])
+            finale.extend([(lambda: len(free_totals) == 2 and not [g for g in ready_early if g not in m_operand or g not in grad_operand], lambda k=k: open_last_group(k))])
         for k in range(CHUNKS):
             finale.extend([(lambda: not [g for g in ready_late if g not in m_operand or g not in grad_operand], lambda k=k: close_last_group(k))])
 
         def write_slot(slot):
             now[0] = slot
-            if (slot + EARLY) % SLOTS == 0 and 0 <= (slot + EARLY) // SLOTS - REACH < HEIGHT:
-                i = (slot + EARLY) // SLOTS - REACH
+            for i in [i for i in range(HEIGHT) if product_start[i] == slot]:
                 pairs = merged_of(i)
                 for pair in pairs:
                     todo_pairs.extend([(i, pair[0][0], pair[0][1]), (i, pair[1][0], pair[1][1])])
                 todo.extend([(i, di, dj) for di, dj in products_of(i) if not [pair for pair in pairs if (di, dj) in pair]])
             for g in range(PASSES):
-                if slot == SLOTS * PACK * g + (GRAD_DELAY if g < PASSES - 2 else 0):
-                    for h in range(2):
-                        reserve(slot + 1, HOLD, lambda bank, g=g, h=h: grad_chain(g, h, bank))
+                if slot == vector_start[PACK * g] + (GRAD_DELAY if g < PASSES - 2 else 14):
+                    reserve_words("g", lambda h, bank, g=g: grad_chain(g, h, bank))
             jobs = timed.get(slot, [])
             for engine, job in jobs:
                 job()
+            while moves and moves[0][0] <= slot and not [n for n in BAND_STARTS if n < moves[0][1] and done.get(("multiplied", n), 0) < IMAGES * len(GROUPS)]:
+                move = moves[0]
+                moves.remove(move)
+                move[2]()
             add_parts()
-            assert len([part for part in parts if part[0] <= slot + 3]) <= 2 * PRODUCTS - 6
-            if slot >= SLOTS * HEIGHT and finale and finale[0][0]():
+            if slot >= vector_end and finale and finale[0][0]():
                 job = finale[0]
                 finale.remove(job)
                 job[1]()
             make_products(
                 SCALAR_ROOM - 3 * len([job for job in jobs if job[0] == "scalar"]), GPSIMD_ROOM - 2 * len([job for job in jobs if job[0] == "gpsimd"])
             )
-            if 0 <= slot < SLOTS * HEIGHT:
-                vector_taps(slot // SLOTS, slot % SLOTS)
+            if slot in vector_plan:
+                vector_taps(vector_plan[slot][0], vector_plan[slot][1])
 
         with tc.tile_pool(name="head", bufs=1) as head:
             open_head(head)
@@ -793,7 +875,7 @@ def tile_localcrf_kernel(tc, input_F, input_logit, compatibility, grad_out, out)
                 write_slot(slot)
         with tc.tile_pool(name="bands", bufs=1) as bands:
             open_bands(bands)
-            for slot in range(head_end, SLOTS * (HEIGHT + 12)):
+            for slot in range(head_end, vector_end + 12 * SLOTS):
                 write_slot(slot)
         assert not (parts or todo or todo_pairs or merges or finale)
         assert max(timed) <= now[0]

@@ -26,15 +26,20 @@ SLOTS = 7
 GROUP = 4
 VECTOR_COLUMNS = (2, 3, 4)
 VECTOR_LEAVES = ((6, 4),)
+LATE = 58
+LATE_COLUMNS = (2, 3, 4)
 BAND = 8
 TARGETS = 6
 BAND_STARTS = (0, 20, 38, 58)
 PATCH = 16
 STRIDE = PATCH - 2 * REACH
 GROUPS = ((0, 13), (13, 10), (23, 10), (33, 10), (43, 10), (53, 11))
+EIGHT = 8
 BATCH = 2
 SCRATCH = 3
-SCRATCH_ROW = P + 2
+IMAGE_ROW = WIDTH + 6
+SCRATCH_ROW = 2 * IMAGE_ROW
+SLICES = 13
 ZONE = 160
 CENTRE = REACH * BAND + REACH
 SCALAR_ROOM = 10
@@ -44,14 +49,16 @@ ADDS = 6
 GRAD_DELAY = 48
 BAND_LOAD = 10
 BAND_BEGIN = 60
-BAND_STEP = 7
+BAND_STEP = 5
 FIRST_BAND = 8
 LEAST = 2
-SPACING = 5
-FIRST_STEP = 8
-FIRST_PATCH = 10
-HOLD = 3
-AHEAD = 7
+FAST = 10
+MARGIN = 8
+FIRST_STEP = 3
+FIRST_PATCH = 28
+PATCH_DELAY = 6
+HOLD = 2
+AHEAD = 3
 PATCH_SLOT = 3
 EARLY = 3
 Q_TILES = 16
@@ -72,8 +79,6 @@ def tile_localcrf_kernel(tc, input_F, input_logit, compatibility, grad_out, out)
     out_rows = out.rearrange("o c a b -> o (c a b)")
     out_flat = out.rearrange("o c a b -> (o c a b)")
     zones_at = SCRATCH * SCRATCH_ROW * CHANNELS
-    zones_row = BATCH * ZONE
-    zones_flat = out_flat[zones_at : zones_at + P * zones_row]
     f_flat = input_F.rearrange("b q i j -> (b q i j)")
 
     with ExitStack() as stack:
@@ -121,9 +126,12 @@ def tile_localcrf_kernel(tc, input_F, input_logit, compatibility, grad_out, out)
                 return None
             if source_band(r) is not None and source_band(r) == band_of(i):
                 return "matmul"
+            if LATE <= i < BAND_STARTS[-1]:
+                return "vector" if dj in LATE_COLUMNS else "product"
             return "vector" if dj in VECTOR_COLUMNS and (di, dj) not in VECTOR_LEAVES else "product"
 
         tables = [("target", dj) for dj in VECTOR_COLUMNS]
+        tables.extend([("target", dj) for dj in LATE_COLUMNS if dj not in VECTOR_COLUMNS])
         targets = len(tables)
         for dj in range(KERNEL):
             if [i for i in range(HEIGHT) for di in range(KERNEL) if engine_of(i, di, dj) == "product"]:
@@ -141,7 +149,7 @@ def tile_localcrf_kernel(tc, input_F, input_logit, compatibility, grad_out, out)
         band_weights = keep.tile([P, IMAGES * len(GROUPS), P], F32)
         zones = [keep.tile([P, BATCH, ZONE], F32, name="zones%d" % n) for n in range(2)]
         f_band = keep.tile([P, IMAGES, BAND, WIDTH], BF16)
-        f_patch = keep.tile([P, IMAGES * len(GROUPS), P], BF16)
+        f_patch = keep.tile([P, len(GROUPS), P], BF16)
         nc.gpsimd.memset(f_band[:], 0.0)
         nc.gpsimd.memset(f_patch[:], 0.0)
         for n in range(2):
@@ -268,7 +276,7 @@ def tile_localcrf_kernel(tc, input_F, input_logit, compatibility, grad_out, out)
         def columns_of(r):
             return [
                 dj
-                for dj in VECTOR_COLUMNS
+                for dj in LATE_COLUMNS
                 if [di for di in range(KERNEL) if 0 <= r + REACH - di < HEIGHT and engine_of(r + REACH - di, di, dj) == "vector"]
             ]
 
@@ -279,7 +287,7 @@ def tile_localcrf_kernel(tc, input_F, input_logit, compatibility, grad_out, out)
                 for di in range(KERNEL - 1, -1, -1)
                 if 0 <= r + REACH - di < HEIGHT and engine_of(r + REACH - di, di, dj) == "vector"
             ]
-            slots = max(LEAST, len(set([i for di, dj, i in ops])))
+            slots = max(LEAST, len(set([i for di, dj, i in ops])), -(-len(ops) // len(VECTOR_COLUMNS)), len(columns_of(r)) if len(columns_of(r)) > WINDOW_BANKS else 0)
             return [ops[len(ops) * t // slots : len(ops) * (t + 1) // slots] for t in range(slots)]
 
         def products_of(i):
@@ -342,12 +350,14 @@ def tile_localcrf_kernel(tc, input_F, input_logit, compatibility, grad_out, out)
                 nc.tensor.transpose(window[r, dj][:, k * P : (k + 1) * P], q_ring[r % RING][:, k, start : start + P], ident_f32)
 
         def add_parts():
-            room = ADDS
-            for entry in reversed([entry for entry in parts if entry[0] <= now[0]][:ADDS]):
+            waiting = [entry for entry in parts if entry[0] <= now[0]]
+            tiles = []
+            for entry in waiting:
+                if entry[1] not in m_total and entry[1] not in tiles and len(tiles) < len(free_totals):
+                    tiles.extend([entry[1]])
+            for entry in reversed([entry for entry in waiting if entry[1] in m_total or entry[1] in tiles][:ADDS]):
                 ready, i, part, shift = entry
                 if i not in m_total:
-                    if not free_totals:
-                        continue
                     total_bank[i] = free_totals[0]
                     free_totals.remove(total_bank[i])
                     m_total[i] = psum.tile([P, CHUNKS, P], F32, name="m_total", tag=total_bank[i])
@@ -355,7 +365,6 @@ def tile_localcrf_kernel(tc, input_F, input_logit, compatibility, grad_out, out)
                 else:
                     first = False
                 parts.remove(entry)
-                room -= 1
                 if part is sum_vector.get(i):
                     free_sums.extend([sum_slot[i]])
                 gone = [part]
@@ -371,30 +380,33 @@ def tile_localcrf_kernel(tc, input_F, input_logit, compatibility, grad_out, out)
                         start=(first and k == 0), stop=(parts_left[i] == 0 and k == CHUNKS - 1),
                     )
                 if parts_left[i] == 0:
-                    after(2, "scalar", lambda i=i: round_m(i))
+                    after(2, "scalar" if band_of(i) is None else "vector", lambda i=i: round_m(i))
 
         def round_m(i):
-            g = i // PACK
-            if band_of(i) is None:
-                nc.scalar.copy(out=turned_of(g)[:, :, i % PACK, :], in_=m_total[i][:])
-                free_totals.extend([total_bank[i]])
-                row_done(g)
+            a = band_of(i)
+            if (i // PACK not in m_turned and not free_turned) or (a is not None and done.get(("patched", a), 0) < IMAGES * len(GROUPS)):
+                after(1, "wait", lambda: round_m(i))
             else:
-                a = band_of(i)
-                nc.scalar.copy(out=band_tiles["sums"][:, :, i - a, :], in_=m_total[i][:])
+                row = turned_of(i // PACK)[:, :, i % PACK, :]
+                if a is None:
+                    nc.scalar.copy(out=row, in_=m_total[i][:])
+                else:
+                    nc.vector.tensor_tensor(out=row, in0=m_total[i][:], in1=band_tiles["patched"][:, :, i - a, :], op=ALU.add)
                 free_totals.extend([total_bank[i]])
-                part_ready(a)
+                row_done(i // PACK)
 
         def part_ready(a):
-            if count(("ready", a), len([i for i in range(a, a + TARGETS) if parts_in[i] > 0]) + IMAGES * len(GROUPS) // BATCH + 1):
+            if count(("ready", a), (1 if a == 0 else IMAGES * len(GROUPS) // BATCH) + 1):
                 for b in range(IMAGES):
                     for n in range(len(GROUPS)):
-                        reserve(now[0] + (FIRST_PATCH if a == 0 else 1), HOLD, lambda bank, b=b, n=n: multiply_patch(a, b, n, bank))
+                        reserve(now[0] + (FIRST_PATCH if a == 0 else PATCH_DELAY), HOLD, lambda bank, b=b, n=n: multiply_patch(a, b, n, bank))
 
-        def clear_kept(a):
-            empty = [i - a for i in range(a, a + TARGETS) if parts_in[i] == 0]
-            if empty:
-                nc.gpsimd.memset(band_tiles["sums"][:, :, empty[0] : empty[-1] + 1, :], 0.0)
+        def round_patched(i):
+            if i // PACK not in m_turned and not free_turned:
+                after(1, "wait", lambda: round_patched(i))
+            else:
+                nc.gpsimd.tensor_copy(out=turned_of(i // PACK)[:, :, i % PACK, :], in_=band_tiles["patched"][:, :, i - band_of(i), :])
+                row_done(i // PACK)
 
         def turned_of(g):
             if g not in m_turned:
@@ -404,8 +416,7 @@ def tile_localcrf_kernel(tc, input_F, input_logit, compatibility, grad_out, out)
             return m_turned[g]
 
         def row_done(g):
-            rows = [i for i in range(g * PACK, (g + 1) * PACK) if band_of(i) is not None]
-            if count(("rounded", g), PACK - len(rows) + (IMAGES * len(GROUPS) if rows else 0)):
+            if count(("rounded", g), PACK):
                 reserve_words("m", lambda h, bank: turn_m(g, h, bank))
 
         def turn_m(g, h, bank):
@@ -416,7 +427,7 @@ def tile_localcrf_kernel(tc, input_F, input_logit, compatibility, grad_out, out)
             )
             if h == 1:
                 free_turned.extend([turned_slot[g]])
-            after(2, "scalar", lambda: group_m(g, h))
+            after(HOLD - 1, "scalar", lambda: group_m(g, h))
 
         def group_m(g, h):
             if h == 0:
@@ -451,7 +462,7 @@ def tile_localcrf_kernel(tc, input_F, input_logit, compatibility, grad_out, out)
                 if h == 1:
                     after(2, "vector", lambda: quantise_grad(g))
 
-            after(2, "scalar", group)
+            after(HOLD - 1, "scalar", group)
 
         def multiply(bank, k, passes, start, stop):
             for g in passes:
@@ -477,7 +488,7 @@ def tile_localcrf_kernel(tc, input_F, input_logit, compatibility, grad_out, out)
                 else:
                     nc.vector.tensor_tensor(out=p_sum[:, k, :], in0=p_early[:], in1=p_sum[:, k, :], op=ALU.add)
 
-            after(2, "vector", gather)
+            after(HOLD - 1, "vector", gather)
 
         def open_last_group(k):
             p_group[k] = psum.tile([P, CHANNELS], F32, name="p_group", tag=("total_a", "total_b", "side_a", "window2")[k])
@@ -556,11 +567,36 @@ def tile_localcrf_kernel(tc, input_F, input_logit, compatibility, grad_out, out)
         nominal = [0]
         for r in range(HEIGHT):
             nominal.extend([nominal[r] + len(vector_slots(r))])
+
+        def pace(r):
+            return 1 if r < FAST else 2
+
         turn_slot = {}
         for r in reversed(range(HEIGHT)):
             turn_slot[r] = nominal[r] - 18 - AHEAD
             if r + 1 < HEIGHT:
-                turn_slot[r] = min(turn_slot[r], turn_slot[r + 1] - SPACING)
+                turn_slot[r] = min(turn_slot[r], turn_slot[r + 1] - 2 * pace(r) - 1)
+        first_row = {}
+        for r in range(HEIGHT):
+            for ops in vector_slots(r):
+                for di, dj, i in ops:
+                    first_row.setdefault(i, r)
+        product_start = {}
+        product_end = {}
+        last_target = BAND_STARTS[0] + TARGETS - 1
+        ahead = [last_target + 1, last_target + 2]
+        product_order = ahead + [i for i in range(HEIGHT) if i not in ahead]
+
+        def plan_products(rows):
+            while len(product_start) < HEIGHT and product_order[len(product_start)] + REACH < rows:
+                i = product_order[len(product_start)]
+                last = min(i + REACH, HEIGHT - 1)
+                begin = vector_start.get(i + REACH, clock) - EARLY
+                if i in ahead:
+                    begin = turn_slot[last] + 3 * pace(last) + 3
+                product_start[i] = max([begin] + [product_end[n] for n in product_end])
+                product_end[i] = product_start[i] + len(set([di for di, dj in products_of(i)]))
+
         q_slot = {}
         keep_slot = {}
         vector_start = {}
@@ -574,32 +610,42 @@ def tile_localcrf_kernel(tc, input_F, input_logit, compatibility, grad_out, out)
             for t, ops in enumerate(vector_slots(r)):
                 for di, dj, i in ops:
                     uses.setdefault(dj, []).extend([t])
-            q_slot[r] = max(clock - 8, turn_slot[r] + 9, keep_slot.get(r - 1, -1000) + 1)
+            old = r - Q_TILES + REACH
+            if old >= 0:
+                turn_slot[r] = max(turn_slot[r], product_end[old] + MARGIN - 2 * pace(r))
+            if r > 0:
+                turn_slot[r] = max(turn_slot[r], turn_slot[r - 1] + 2 * pace(r - 1) + 1)
+            begun = len([i for i in first_row if first_row[i] <= r])
+            if begun > SUMS:
+                clock = max(clock, sorted([product_start[i] for i in product_start if i in first_row])[begun - SUMS - 1] + EARLY + MARGIN)
+            q_slot[r] = max(clock - 8, turn_slot[r] + 3 * pace(r) + 3, keep_slot.get(r - 1, -1000) + 1)
             keep_slot[r] = max(q_slot[r] + 2, last_window.get(r - RING, -1000) + 1)
             start = clock
-            made = []
-            for n, dj in enumerate(uses):
-                bank = (len(window_plan) + n) % WINDOW_BANKS
-                slot = max(clock + uses[dj][0] - 3, keep_slot[r] + 2, window_free.get(bank, -1000) + 1)
-                start = max(start, slot + 1 - uses[dj][0])
-                window_free[bank] = start + uses[dj][-1]
-                made.extend([(slot, r, dj, bank)])
-            for n, dj in enumerate(uses):
-                window_free[made[n][3]] = start + uses[dj][-1]
+            settled = False
+            while not settled:
+                free = dict(window_free)
+                made = []
+                later = start
+                for n, dj in enumerate(uses):
+                    bank = (len(window_plan) + n) % WINDOW_BANKS
+                    slot = max(clock + uses[dj][0] - 3, keep_slot[r] + 2, free.get(bank, -1000) + 1)
+                    later = max(later, slot + 1 - uses[dj][0])
+                    free[bank] = start + uses[dj][-1]
+                    made.extend([(slot, r, dj, bank)])
+                settled = later == start
+                start = later
+            window_free = free
             window_plan.extend(made)
             last_window[r] = max([slot for slot, row, dj, bank in made] + [keep_slot[r]])
             vector_start[r] = start
             for t in range(len(vector_slots(r))):
                 vector_plan[start + t] = (r, t)
             clock = start + len(vector_slots(r))
+            plan_products(r + 1)
         vector_end = clock
-        product_start = {}
-        clock = -1000
-        for i in range(HEIGHT):
-            product_start[i] = max(clock, vector_start.get(i + REACH, vector_end) - EARLY)
-            clock = product_start[i] + len(set([di for di, dj in products_of(i)]))
+        plan_products(HEIGHT + REACH)
         for r in range(HEIGHT):
-            busy["side_a"].extend([(turn_slot[r], turn_slot[r] + 5)])
+            busy["side_a"].extend([(turn_slot[r], turn_slot[r] + 2 * pace(r) + 1)])
             busy["side_b"].extend([(q_slot[r], keep_slot[r] + 1)])
         busy["side_a"].extend([(turn_slot[HEIGHT - 1], 10000)])
         for n in range(2):
@@ -638,6 +684,8 @@ def tile_localcrf_kernel(tc, input_F, input_logit, compatibility, grad_out, out)
             nc.vector.memset(f_raw[:], 0.0)
             nc.vector.memset(f_wide[:, :, 0:PAD], 0.0)
             nc.vector.memset(f_wide[:, :, PAD + P :], 0.0)
+            early["zones"] = head.tile([P, IMAGES * len(GROUPS), ZONE], F32, name="all_zones")
+            nc.gpsimd.memset(early["zones"][:], 0.0)
             load_logits(0)
             load_band_weights(0)
             for b in range(IMAGES):
@@ -649,10 +697,10 @@ def tile_localcrf_kernel(tc, input_F, input_logit, compatibility, grad_out, out)
             load_logits(1)
 
         def open_bands(bands):
-            sources = bands.tile([P, IMAGES * len(GROUPS), CHANNELS], F32)
-            kept = bands.tile([P, CHUNKS, TARGETS, P], F32)
+            sources = bands.tile([P, SLICES, CHANNELS], F32)
+            patched = bands.tile([P, CHUNKS, TARGETS, P], F32)
             band_tiles["sources"] = sources
-            band_tiles["sums"] = kept
+            band_tiles["patched"] = patched
             nc.gpsimd.memset(sources[:], 0.0)
             clear_scratch()
 
@@ -672,16 +720,17 @@ def tile_localcrf_kernel(tc, input_F, input_logit, compatibility, grad_out, out)
             for b in range(IMAGES):
                 for di in range(KERNEL):
                     start = (b * KERNEL * KERNEL + di * KERNEL) * plane + (s - (di - REACH)) * WIDTH + REACH
-                    begin = min(start, total - KERNEL * (plane - 1))
-                    view = f_flat[begin : begin + KERNEL * (plane - 1)].rearrange("(d n) -> d n", n=plane - 1)
+                    many = EIGHT if start + EIGHT * plane <= total else KERNEL
+                    begin = min(start, total - many * (plane - 1))
+                    view = f_flat[begin : begin + many * (plane - 1)].rearrange("(d n) -> d n", n=plane - 1)
                     view = view[:, start - begin : start - begin + BAND * WIDTH].rearrange("d (i j) -> d i j", j=WIDTH)
-                    nc.sync.dma_start(out=f_band[di * KERNEL : (di + 1) * KERNEL, b, :, :], in_=view)
+                    nc.sync.dma_start(out=f_band[di * EIGHT : di * EIGHT + many, b, :, :], in_=view)
 
         def cut_band_weights(b):
             for n in range(len(GROUPS)):
                 columns = min(PATCH, WIDTH - STRIDE * n)
                 nc.gpsimd.tensor_copy(
-                    out=f_patch[:, b * len(GROUPS) + n, 0 : columns * BAND].rearrange("p (j i) -> p j i", i=BAND),
+                    out=f_patch[:, n, 0 : columns * BAND].rearrange("p (j i) -> p j i", i=BAND),
                     in_=f_band[:, b, :, STRIDE * n : STRIDE * n + columns].rearrange("p i j -> p j i"),
                 )
 
@@ -692,55 +741,72 @@ def tile_localcrf_kernel(tc, input_F, input_logit, compatibility, grad_out, out)
                 pending.remove(read)
                 read()
 
-        def turn_band_weights(a, first, bank):
-            f_turned = psum.tile([P, BATCH, P], BF16, name="f_turned", tag=bank)
-            for n in range(BATCH):
-                nc.tensor.transpose(f_turned[:, n, :], f_patch[:, first + n, :], ident_bf[:])
+        def turn_band_weights(a, first, many, tile, at_once, bank):
+            f_turned = psum.tile([P, many, P], BF16, name="f_turned", tag=bank)
+            for n in range(many):
+                nc.tensor.transpose(f_turned[:, n, :], f_patch[:, (first + n) % len(GROUPS), :], ident_bf[:])
+            offset = first % at_once
 
             def spread():
                 first_word = CENTRE - REACH * BAND - REACH
+                words = tile[:, offset : offset + many, first_word : first_word + KERNEL * BAND]
                 nc.vector.tensor_tensor(
-                    out=zones[first // BATCH % 2][:, :, first_word : first_word + KERNEL * BAND].rearrange("p g (e x) -> p g e x", x=BAND)[:, :, :, 0:KERNEL],
-                    in0=f_turned[:, :, KERNEL * KERNEL - 1 :: -1].rearrange("p g (d e) -> p g e d", e=KERNEL),
-                    in1=fits[:].unsqueeze(1).unsqueeze(1).to_broadcast([P, BATCH, KERNEL, KERNEL]),
+                    out=words.rearrange("p g (e x) -> p g e x", x=BAND)[:, :, :, 0:KERNEL],
+                    in0=f_turned[:, :, KERNEL * EIGHT - 1 :: -1].rearrange("p g (d e) -> p g e d", e=EIGHT)[:, :, 1:EIGHT, :],
+                    in1=fits[:].unsqueeze(1).unsqueeze(1).to_broadcast([P, many, KERNEL, KERNEL]),
                     op=ALU.mult,
                 )
-                after(1, "sync", skew)
+                if offset + many == at_once:
+                    after(1, "sync", skew)
 
+            row = at_once * ZONE
+            flat = out_flat[0 : P * row] if a == 0 else out_flat[zones_at : zones_at + P * row]
 
             def skew():
                 read_zones()
-                nc.sync.dma_start(
-                    out=zones_flat.rearrange("(p x) -> p x", x=zones_row), in_=zones[first // BATCH % 2][:].rearrange("p g z -> p (g z)")
-                )
+                nc.sync.dma_start(out=flat.rearrange("(p x) -> p x", x=row), in_=tile[:].rearrange("p g z -> p (g z)"))
                 pending.extend([unskew])
                 after(2, "sync", read_zones)
 
             def unskew():
                 assert not [n for n in BAND_STARTS if n < a and done.get(("multiplied", n), 0) < IMAGES * len(GROUPS)]
-                view = zones_flat[CENTRE : CENTRE + P * (zones_row - 1)].rearrange("(p x) -> p x", x=zones_row - 1)
-                for n in range(BATCH):
-                    nc.sync.dma_start(out=band_weights[:, first + n, 0 : BAND * PATCH], in_=view[:, n * ZONE : n * ZONE + BAND * PATCH])
+                view = flat[CENTRE : CENTRE + P * (row - 1)].rearrange("(p x) -> p x", x=row - 1)
+                for n in range(at_once):
+                    nc.sync.dma_start(out=band_weights[:, first - offset + n, 0 : BAND * PATCH], in_=view[:, n * ZONE : n * ZONE + BAND * PATCH])
                 part_ready(a)
 
-            after(2, "vector", spread)
+            after(HOLD - 1, "vector", spread)
+
+        def next_band_weights(a, first):
+            many = len(GROUPS) if a == 0 else BATCH
+            tile = early["zones"] if a == 0 else zones[first // BATCH % 2]
+            together = IMAGES * len(GROUPS) if a == 0 else BATCH
+
+            def turn(bank):
+                turn_band_weights(a, first, many, tile, together, bank)
+                following = first + many
+                if following == len(GROUPS):
+                    after(1, "gpsimd", lambda: cut_band_weights(1))
+                if following < IMAGES * len(GROUPS):
+                    after(FIRST_STEP if a == 0 else BAND_STEP, "plan", lambda: next_band_weights(a, following))
+
+            reserve(now[0] + 1, HOLD, turn)
 
         def clear_scratch():
-            for n in range(SCRATCH):
-                nc.sync.dma_start(out=out_rows[n * SCRATCH_ROW + P : (n + 1) * SCRATCH_ROW, :], in_=band_tiles["sources"][0 : SCRATCH_ROW - P, 0, :])
+            for n in range(SCRATCH * IMAGES):
+                nc.sync.dma_start(out=out_rows[n * IMAGE_ROW + WIDTH : (n + 1) * IMAGE_ROW, :], in_=band_tiles["sources"][0 : IMAGE_ROW - WIDTH, 0, :])
 
         def store_sources(r):
-            first = r % SCRATCH * SCRATCH_ROW
-            nc.sync.dma_start(out=out_rows[first : first + P, :], in_=q_px[r][:])
+            for b in range(IMAGES):
+                first = r % SCRATCH * SCRATCH_ROW + b * IMAGE_ROW
+                nc.sync.dma_start(out=out_rows[first : first + WIDTH, :], in_=q_px[r][b * WIDTH : (b + 1) * WIDTH, :])
 
         def gather_sources(s, r):
             sources = band_tiles["sources"][r - s : P : BAND, :, :]
-            patches = len(GROUPS)
-            for b in range(IMAGES):
-                first = r % SCRATCH * SCRATCH_ROW + b * WIDTH
-                for start, stop in ((0, STRIDE), (STRIDE, PATCH)):
-                    view = out_rows[first + start : first + start + patches * STRIDE, :].rearrange("(n j) c -> j n c", j=STRIDE)
-                    nc.sync.dma_start(out=sources[start:stop, b * patches : (b + 1) * patches, :], in_=view[0 : stop - start, :, :])
+            first = r % SCRATCH * SCRATCH_ROW
+            for start, stop in ((0, STRIDE), (STRIDE, PATCH)):
+                view = out_rows[first + start : first + start + SLICES * STRIDE, :].rearrange("(n j) c -> j n c", j=STRIDE)
+                nc.sync.dma_start(out=sources[start:stop, :, :], in_=view[0 : stop - start, :, :])
 
         def multiply_patch(a, b, n, bank):
             first_target, columns = GROUPS[n]
@@ -750,25 +816,23 @@ def tile_localcrf_kernel(tc, input_F, input_logit, compatibility, grad_out, out)
             for k in range(CHUNKS):
                 nc.tensor.matmul(
                     m_patch[:, k, :, :],
-                    lhsT=band_tiles["sources"][:, b * len(GROUPS) + n, k * P : (k + 1) * P],
+                    lhsT=band_tiles["sources"][:, b * (IMAGE_ROW // STRIDE) + n, k * P : (k + 1) * P],
                     rhs=band_weights[:, b * len(GROUPS) + n, 0 : BAND * PATCH].rearrange("p (j i) -> p j i", i=BAND)[:, first : first + columns, row : row + TARGETS],
                     start=True, stop=True,
                 )
 
             def finish():
                 targets_at = b * WIDTH + first_target
-                for g in range(a // PACK, (a + TARGETS - 1) // PACK + 1):
-                    i0, i1 = max(a, g * PACK), min(a + TARGETS, (g + 1) * PACK)
-                    nc.vector.tensor_tensor(
-                        out=turned_of(g)[:, :, i0 % PACK : i0 % PACK + i1 - i0, targets_at : targets_at + columns],
-                        in0=m_patch[:, :, :, i0 - a : i1 - a].rearrange("p k j i -> p k i j"),
-                        in1=band_tiles["sums"][:, :, i0 - a : i1 - a, targets_at : targets_at + columns],
-                        op=ALU.add,
-                    )
-                    row_done(g)
+                nc.scalar.copy(
+                    out=band_tiles["patched"][:, :, :, targets_at : targets_at + columns], in_=m_patch[:].rearrange("p k j i -> p k i j")
+                )
+                if count(("patched", a), IMAGES * len(GROUPS)):
+                    for i in range(a, a + TARGETS):
+                        if parts_in[i] == 0:
+                            after(1 + i - a, "gpsimd", lambda i=i: round_patched(i))
 
             count(("multiplied", a), 0)
-            after(2, "vector", finish)
+            after(HOLD - 1, "scalar", finish)
 
         def widen(dj):
             nc.vector.tensor_copy(
@@ -806,31 +870,25 @@ def tile_localcrf_kernel(tc, input_F, input_logit, compatibility, grad_out, out)
             at(first_slot + 20 * g, "sync", lambda g=g: load_grad(g))
         for r in range(HEIGHT):
             at(turn_slot[r], "tensor", lambda r=r: turn_logits(r))
-            at(turn_slot[r] + 2, "vector", lambda r=r: find_top(r))
-            at(turn_slot[r] + 4, "scalar", lambda r=r: exponentials(r))
-            at(turn_slot[r] + 6, "vector", lambda r=r: invert(r))
-            at(turn_slot[r] + 7, "gpsimd", lambda r=r: normalise(r))
+            at(turn_slot[r] + pace(r), "vector", lambda r=r: find_top(r))
+            at(turn_slot[r] + 2 * pace(r), "scalar", lambda r=r: exponentials(r))
+            at(turn_slot[r] + 3 * pace(r), "vector", lambda r=r: invert(r))
+            at(turn_slot[r] + 3 * pace(r) + 1, "gpsimd", lambda r=r: normalise(r))
             at(q_slot[r], "tensor", lambda r=r: turn_q(r))
             at(keep_slot[r], "scalar", lambda r=r: keep_q(r))
         for slot, r, dj, bank in window_plan:
             at(slot, "tensor", lambda r=r, dj=dj, bank=bank: make_window(r, dj, bank))
         moves = []
         for a in BAND_STARTS:
-            at(max(product_start[a] - 2, head_end + 1), "gpsimd", lambda a=a: clear_kept(a))
             begin = vector_start[a] - BAND_BEGIN
             s = sources_of(a)
             if a > 0:
                 at(begin, "sync", lambda s=s: load_band_weights(s))
             loaded = begin + BAND_LOAD if a > 0 else first_slot + FIRST_BAND
-            for b in range(IMAGES):
-                at(loaded + 2 * b, "gpsimd", lambda b=b: cut_band_weights(b))
-            for q in range(IMAGES * len(GROUPS) // BATCH):
-                at(
-                    loaded + 5 + (BAND_STEP if a > 0 else FIRST_STEP) * q, "tensor",
-                    lambda a=a, q=q: reserve(now[0] + 1, HOLD, lambda bank: turn_band_weights(a, q * BATCH, bank)),
-                )
+            at(loaded, "gpsimd", lambda: cut_band_weights(0))
+            at(loaded + 4, "plan", lambda a=a: next_band_weights(a, 0))
             for r in range(s, s + BAND):
-                slot = max(turn_slot[r] + 9, head_end + 1)
+                slot = max(turn_slot[r] + 3 * pace(r) + 3, head_end + 1)
                 moves.extend([(slot, a, lambda r=r: store_sources(r))])
                 if r > s:
                     moves.extend([(slot, a, lambda s=s, r=r: gather_sources(s, r - 1))])

@@ -25,12 +25,11 @@ PAD = 4
 SLOTS = 7
 GROUP = 4
 VECTOR_COLUMNS = (2, 3, 4)
-VECTOR_LEAVES = ((6, 4),)
-LATE = 58
-LATE_COLUMNS = (2, 3, 4)
+SEED_COLUMN = 3
+SEED_AHEAD = 3
 BAND = 8
-TARGETS = 6
-BAND_STARTS = (0, 20, 38, 58)
+BANDS = {0: 6, 20: 6, 38: 6, 57: 7}
+BAND_STARTS = tuple(BANDS)
 PATCH = 16
 STRIDE = PATCH - 2 * REACH
 GROUPS = ((0, 13), (13, 10), (23, 10), (33, 10), (43, 10), (53, 11))
@@ -43,7 +42,7 @@ SLICES = 13
 ZONE = 160
 CENTRE = REACH * BAND + REACH
 SCALAR_ROOM = 10
-GPSIMD_ROOM = 4
+GPSIMD_ROOM = 4.2
 MERGE_COLUMNS = (0,)
 ADDS = 6
 GRAD_DELAY = 48
@@ -53,7 +52,7 @@ BAND_STEP = 5
 FIRST_BAND = 8
 LEAST = 2
 FAST = 10
-MARGIN = 8
+MARGIN = 4
 FIRST_STEP = 3
 FIRST_PATCH = 28
 PATCH_DELAY = 6
@@ -61,8 +60,8 @@ HOLD = 2
 AHEAD = 3
 PATCH_SLOT = 3
 EARLY = 3
-Q_TILES = 16
-SUMS = 11
+Q_TILES = 15
+SUMS = 10
 PAIRED = 4
 PRODUCTS = 9
 TURNED = 3
@@ -110,11 +109,11 @@ def tile_localcrf_kernel(tc, input_F, input_logit, compatibility, grad_out, out)
             nc.vector.memset(q_ring[n][:], 0.0)
 
         def band_of(i):
-            found = [a for a in BAND_STARTS if a <= i < a + TARGETS]
+            found = [a for a in BAND_STARTS if a <= i < a + BANDS[a]]
             return found[0] if found else None
 
         def sources_of(a):
-            return min(max(a - (BAND - TARGETS) // 2, 0), HEIGHT - BAND)
+            return min(max(a - (BAND - BANDS[a]) // 2, 0), HEIGHT - BAND)
 
         def source_band(r):
             found = [a for a in BAND_STARTS if sources_of(a) <= r < sources_of(a) + BAND]
@@ -126,15 +125,15 @@ def tile_localcrf_kernel(tc, input_F, input_logit, compatibility, grad_out, out)
                 return None
             if source_band(r) is not None and source_band(r) == band_of(i):
                 return "matmul"
-            if LATE <= i < BAND_STARTS[-1]:
-                return "vector" if dj in LATE_COLUMNS else "product"
-            return "vector" if dj in VECTOR_COLUMNS and (di, dj) not in VECTOR_LEAVES else "product"
+            if dj not in VECTOR_COLUMNS:
+                return "product"
+            before = [n for n in range(di) if 0 <= i + n - REACH < HEIGHT and (band_of(i) is None or source_band(i + n - REACH) != band_of(i))]
+            return "seed" if dj == SEED_COLUMN and not before else "vector"
 
         tables = [("target", dj) for dj in VECTOR_COLUMNS]
-        tables.extend([("target", dj) for dj in LATE_COLUMNS if dj not in VECTOR_COLUMNS])
         targets = len(tables)
         for dj in range(KERNEL):
-            if [i for i in range(HEIGHT) for di in range(KERNEL) if engine_of(i, di, dj) == "product"]:
+            if [i for i in range(HEIGHT) for di in range(KERNEL) if engine_of(i, di, dj) in ("product", "seed")]:
                 tables.extend([("source", dj)])
         target_taps = keep.tile([P, targets, PAIRS, P], BF16)
         source_taps = keep.tile([P, len(tables) - targets, PAIRS, P], F32)
@@ -148,7 +147,7 @@ def tile_localcrf_kernel(tc, input_F, input_logit, compatibility, grad_out, out)
         p_sum = keep.tile([P, CHUNKS, CHANNELS], F32)
         band_weights = keep.tile([P, IMAGES * len(GROUPS), P], F32)
         zones = [keep.tile([P, BATCH, ZONE], F32, name="zones%d" % n) for n in range(2)]
-        f_band = keep.tile([P, IMAGES, BAND, WIDTH], BF16)
+        f_band = keep.tile([P, IMAGES, BAND, WIDTH + PATCH - STRIDE], BF16)
         f_patch = keep.tile([P, len(GROUPS), P], BF16)
         nc.gpsimd.memset(f_band[:], 0.0)
         nc.gpsimd.memset(f_patch[:], 0.0)
@@ -276,7 +275,7 @@ def tile_localcrf_kernel(tc, input_F, input_logit, compatibility, grad_out, out)
         def columns_of(r):
             return [
                 dj
-                for dj in LATE_COLUMNS
+                for dj in VECTOR_COLUMNS
                 if [di for di in range(KERNEL) if 0 <= r + REACH - di < HEIGHT and engine_of(r + REACH - di, di, dj) == "vector"]
             ]
 
@@ -502,18 +501,19 @@ def tile_localcrf_kernel(tc, input_F, input_logit, compatibility, grad_out, out)
             )
             nc.sync.dma_start(out=out_view[:, k, :], in_=factor[k][:])
 
+        def seed(i):
+            di = [di for di in range(KERNEL) if engine_of(i, di, SEED_COLUMN) == "seed"][0]
+            sum_slot[i] = free_sums[0]
+            free_sums.remove(sum_slot[i])
+            sum_vector[i] = sums.tile([P, CHANNELS], F32, name="sum_vector", tag="sum%d" % sum_slot[i])
+            nc.scalar.activation(out=sum_vector[i][:], in_=q_px[i + di - REACH][:], func=FUNC.Copy, scale=weight("source", di, SEED_COLUMN, i))
+
         def vector_taps(r, t):
             for di, dj, i in vector_slots(r)[t]:
-                if i not in sum_vector:
-                    sum_slot[i] = free_sums[0]
-                    free_sums.remove(sum_slot[i])
-                    sum_vector[i] = sums.tile([P, CHANNELS], F32, name="sum_vector", tag="sum%d" % sum_slot[i])
-                    nc.vector.tensor_scalar_mul(out=sum_vector[i][:], in0=window[r, dj][:], scalar1=weight("target", di, dj, i))
-                else:
-                    nc.vector.scalar_tensor_tensor(
-                        out=sum_vector[i][:], in0=window[r, dj][:], scalar=weight("target", di, dj, i), in1=sum_vector[i][:],
-                        op0=ALU.mult, op1=ALU.add,
-                    )
+                nc.vector.scalar_tensor_tensor(
+                    out=sum_vector[i][:], in0=window[r, dj][:], scalar=weight("target", di, dj, i), in1=sum_vector[i][:],
+                    op0=ALU.mult, op1=ALU.add,
+                )
                 vector_left[i] -= 1
                 if vector_left[i] == 0:
                     parts.extend([(max(now[0] + 2, product_start[i] + EARLY), i, sum_vector[i], 0)])
@@ -583,7 +583,7 @@ def tile_localcrf_kernel(tc, input_F, input_logit, compatibility, grad_out, out)
                     first_row.setdefault(i, r)
         product_start = {}
         product_end = {}
-        last_target = BAND_STARTS[0] + TARGETS - 1
+        last_target = BAND_STARTS[0] + BANDS[BAND_STARTS[0]] - 1
         ahead = [last_target + 1, last_target + 2]
         product_order = ahead + [i for i in range(HEIGHT) if i not in ahead]
 
@@ -687,6 +687,7 @@ def tile_localcrf_kernel(tc, input_F, input_logit, compatibility, grad_out, out)
             early["zones"] = head.tile([P, IMAGES * len(GROUPS), ZONE], F32, name="all_zones")
             nc.gpsimd.memset(early["zones"][:], 0.0)
             load_logits(0)
+            load_logits(1)
             load_band_weights(0)
             for b in range(IMAGES):
                 for di in range(KERNEL):
@@ -694,11 +695,10 @@ def tile_localcrf_kernel(tc, input_F, input_logit, compatibility, grad_out, out)
                         out=f_raw[WIDTH * (di % 2) : WIDTH * (di % 2) + WIDTH, di // 2 : KERNEL * PAIRS : PAIRS, b * WIDTH : (b + 1) * WIDTH],
                         in_=input_F[b, di * KERNEL : (di + 1) * KERNEL].rearrange("q i j -> i q j"),
                     )
-            load_logits(1)
 
         def open_bands(bands):
             sources = bands.tile([P, SLICES, CHANNELS], F32)
-            patched = bands.tile([P, CHUNKS, TARGETS, P], F32)
+            patched = bands.tile([P, CHUNKS, max(BANDS.values()), P], F32)
             band_tiles["sources"] = sources
             band_tiles["patched"] = patched
             nc.gpsimd.memset(sources[:], 0.0)
@@ -724,14 +724,13 @@ def tile_localcrf_kernel(tc, input_F, input_logit, compatibility, grad_out, out)
                     begin = min(start, total - many * (plane - 1))
                     view = f_flat[begin : begin + many * (plane - 1)].rearrange("(d n) -> d n", n=plane - 1)
                     view = view[:, start - begin : start - begin + BAND * WIDTH].rearrange("d (i j) -> d i j", j=WIDTH)
-                    nc.sync.dma_start(out=f_band[di * EIGHT : di * EIGHT + many, b, :, :], in_=view)
+                    nc.sync.dma_start(out=f_band[di * EIGHT : di * EIGHT + many, b, :, 0:WIDTH], in_=view)
 
         def cut_band_weights(b):
-            for n in range(len(GROUPS)):
-                columns = min(PATCH, WIDTH - STRIDE * n)
+            for start, stop in ((0, STRIDE), (STRIDE, PATCH)):
+                view = f_band[:, b, :, start : start + len(GROUPS) * STRIDE].rearrange("p i (n j) -> p n j i", j=STRIDE)
                 nc.gpsimd.tensor_copy(
-                    out=f_patch[:, n, 0 : columns * BAND].rearrange("p (j i) -> p j i", i=BAND),
-                    in_=f_band[:, b, :, STRIDE * n : STRIDE * n + columns].rearrange("p i j -> p j i"),
+                    out=f_patch[:, :, start * BAND : stop * BAND].rearrange("p n (j i) -> p n j i", i=BAND), in_=view[:, :, 0 : stop - start, :]
                 )
 
         pending = []
@@ -812,22 +811,22 @@ def tile_localcrf_kernel(tc, input_F, input_logit, compatibility, grad_out, out)
             first_target, columns = GROUPS[n]
             first = first_target - STRIDE * n
             row = a - sources_of(a)
-            m_patch = psum.tile([P, CHUNKS, columns, TARGETS], F32, name="m_patch", tag=bank)
+            m_patch = psum.tile([P, CHUNKS, columns, BANDS[a]], F32, name="m_patch", tag=bank)
             for k in range(CHUNKS):
                 nc.tensor.matmul(
                     m_patch[:, k, :, :],
                     lhsT=band_tiles["sources"][:, b * (IMAGE_ROW // STRIDE) + n, k * P : (k + 1) * P],
-                    rhs=band_weights[:, b * len(GROUPS) + n, 0 : BAND * PATCH].rearrange("p (j i) -> p j i", i=BAND)[:, first : first + columns, row : row + TARGETS],
+                    rhs=band_weights[:, b * len(GROUPS) + n, 0 : BAND * PATCH].rearrange("p (j i) -> p j i", i=BAND)[:, first : first + columns, row : row + BANDS[a]],
                     start=True, stop=True,
                 )
 
             def finish():
                 targets_at = b * WIDTH + first_target
                 nc.scalar.copy(
-                    out=band_tiles["patched"][:, :, :, targets_at : targets_at + columns], in_=m_patch[:].rearrange("p k j i -> p k i j")
+                    out=band_tiles["patched"][:, :, 0 : BANDS[a], targets_at : targets_at + columns], in_=m_patch[:].rearrange("p k j i -> p k i j")
                 )
                 if count(("patched", a), IMAGES * len(GROUPS)):
-                    for i in range(a, a + TARGETS):
+                    for i in range(a, a + BANDS[a]):
                         if parts_in[i] == 0:
                             after(1 + i - a, "gpsimd", lambda i=i: round_patched(i))
 
@@ -874,8 +873,16 @@ def tile_localcrf_kernel(tc, input_F, input_logit, compatibility, grad_out, out)
             at(turn_slot[r] + 2 * pace(r), "scalar", lambda r=r: exponentials(r))
             at(turn_slot[r] + 3 * pace(r), "vector", lambda r=r: invert(r))
             at(turn_slot[r] + 3 * pace(r) + 1, "gpsimd", lambda r=r: normalise(r))
-            at(q_slot[r], "tensor", lambda r=r: turn_q(r))
-            at(keep_slot[r], "scalar", lambda r=r: keep_q(r))
+            if columns_of(r):
+                at(q_slot[r], "tensor", lambda r=r: turn_q(r))
+                at(keep_slot[r], "scalar", lambda r=r: keep_q(r))
+        seeded = []
+        for slot in sorted(vector_plan):
+            r, t = vector_plan[slot]
+            for di, dj, i in vector_slots(r)[t]:
+                if i not in seeded:
+                    seeded.extend([i])
+                    at(max(slot - SEED_AHEAD, turn_slot[r] + 3 * pace(r) + 3), "scalar", lambda i=i: seed(i))
         for slot, r, dj, bank in window_plan:
             at(slot, "tensor", lambda r=r, dj=dj, bank=bank: make_window(r, dj, bank))
         moves = []

from contextlib import ExitStack

import concourse.mybir as mybir
from concourse.masks import make_identity

F32 = mybir.dt.float32
BF16 = mybir.dt.bfloat16
U32 = mybir.dt.uint32
U8 = mybir.dt.uint8
E4M3_X4 = mybir.dt.float8_e4m3fn_x4
E5M2_X4 = mybir.dt.float8_e5m2_x4
FUNC = mybir.ActivationFunctionType
ALU = mybir.AluOpType
AXIS = mybir.AxisListType

P = 128
IMAGES, CHANNELS, HEIGHT, WIDTH, KERNEL = 2, 512, 64, 64, 7
REACH = KERNEL // 2
CHUNKS = CHANNELS // P
PACK = 4
PASSES = HEIGHT // PACK
HALF = CHANNELS // 2
PAIRS = (KERNEL + 1) // 2
PAD = 4
SLOTS = 7
GROUP = 4
VECTOR_COLUMNS = (2, 3, 4)
SEED_COLUMN = 3
SEED_AHEAD = 3
BAND = 8
BANDS = {0: 6, 20: 6, 38: 6, 57: 7}
BAND_STARTS = tuple(BANDS)
PATCH = 16
STRIDE = PATCH - 2 * REACH
GROUPS = ((0, 13), (13, 10), (23, 10), (33, 10), (43, 10), (53, 11))
EIGHT = 8
BATCH = 2
SCRATCH = 3
IMAGE_ROW = WIDTH + 6
SCRATCH_ROW = 2 * IMAGE_ROW
SLICES = 13
ZONE = 160
CENTRE = REACH * BAND + REACH
SCALAR_ROOM = 10
GPSIMD_ROOM = 4.2
MERGE_COLUMNS = (0,)
ADDS = 6
GRAD_DELAY = 48
BAND_LOAD = 10
BAND_BEGIN = 60
BAND_STEP = 5
FIRST_BAND = 8
LEAST = 2
FAST = 10
MARGIN = 4
FIRST_STEP = 3
FIRST_PATCH = 28
PATCH_DELAY = 6
HOLD = 2
AHEAD = 3
PATCH_SLOT = 3
EARLY = 3
Q_TILES = 15
SUMS = 10
PAIRED = 4
PRODUCTS = 9
TURNED = 3
WINDOW_BANKS = 3
RING = 3

FLOPS = 2 * CHANNELS * CHANNELS * IMAGES * HEIGHT * WIDTH + 2 * KERNEL * KERNEL * CHANNELS * IMAGES * HEIGHT * WIDTH


def tile_localcrf_kernel(tc, input_F, input_logit, compatibility, grad_out, out):
    nc = tc.nc
    comp_view = compatibility.rearrange("(k o) c a b -> o k (c a b)", o=P)
    out_view = out.rearrange("(k o) c a b -> o k (c a b)", o=P)
    out_rows = out.rearrange("o c a b -> o (c a b)")
    out_flat = out.rearrange("o c a b -> (o c a b)")
    zones_at = SCRATCH * SCRATCH_ROW * CHANNELS
    f_flat = input_F.rearrange("b q i j -> (b q i j)")

    with ExitStack() as stack:
        stack.enter_context(tc.manual_schedule())
        keep = stack.enter_context(tc.tile_pool(name="keep", bufs=1))
        slabs = stack.enter_context(tc.tile_pool(name="slabs", bufs=2))
        soft = stack.enter_context(tc.tile_pool(name="soft", bufs=Q_TILES))
        stats = stack.enter_context(tc.tile_pool(name="stats", bufs=6))
        sums = stack.enter_context(tc.tile_pool(name="sums", bufs=1))
        products = stack.enter_context(tc.tile_pool(name="products", bufs=PRODUCTS))
        paired_products = stack.enter_context(tc.tile_pool(name="paired_products", bufs=PAIRED))
        turned = stack.enter_context(tc.tile_pool(name="turned", bufs=1))
        operands = stack.enter_context(tc.tile_pool(name="operands", bufs=1))
        codes = stack.enter_context(tc.tile_pool(name="codes", bufs=GROUP + 1))
        grad_codes = stack.enter_context(tc.tile_pool(name="grad_codes", bufs=GROUP + 1))
        psum = stack.enter_context(tc.psum_pool(name="psum", bufs=1))

        ident_bf = keep.tile([P, P], BF16)
        make_identity(nc, ident_bf[:])
        twice = keep.tile([P, 2 * P], F32)
        make_identity(nc, twice[:, 0:P])
        nc.vector.tensor_copy(out=twice[:, P : 2 * P], in_=twice[:, 0:P])
        ident_f32 = twice[:, 0:P]
        warm = keep.tile([P, 1], F32)
        nc.scalar.activation(out=warm[:], in_=twice[:, 0:1], func=FUNC.Exp)

        q_ring = [keep.tile([P, CHUNKS, PAD + P + PAD], F32, name="q_ring%d" % n) for n in range(RING)]
        for n in range(RING):
            nc.vector.memset(q_ring[n][:], 0.0)

        def band_of(i):
            found = [a for a in BAND_STARTS if a <= i < a + BANDS[a]]
            return found[0] if found else None

        def sources_of(a):
            return min(max(a - (BAND - BANDS[a]) // 2, 0), HEIGHT - BAND)

        def source_band(r):
            found = [a for a in BAND_STARTS if sources_of(a) <= r < sources_of(a) + BAND]
            return found[0] if found else None

        def engine_of(i, di, dj):
            r = i + di - REACH
            if not 0 <= r < HEIGHT:
                return None
            if source_band(r) is not None and source_band(r) == band_of(i):
                return "matmul"
            if dj not in VECTOR_COLUMNS:
                return "product"
            before = [n for n in range(di) if 0 <= i + n - REACH < HEIGHT and (band_of(i) is None or source_band(i + n - REACH) != band_of(i))]
            return "seed" if dj == SEED_COLUMN and not before else "vector"

        tables = [("target", dj) for dj in VECTOR_COLUMNS]
        targets = len(tables)
        for dj in range(KERNEL):
            if [i for i in range(HEIGHT) for di in range(KERNEL) if engine_of(i, di, dj) in ("product", "seed")]:
                tables.extend([("source", dj)])
        target_taps = keep.tile([P, targets, PAIRS, P], BF16)
        source_taps = keep.tile([P, len(tables) - targets, PAIRS, P], F32)

        def table(n):
            return target_taps[:, n, :, :] if n < targets else source_taps[:, n - targets, :, :]

        def weight(kind, di, dj, i):
            return table(tables.index((kind, dj)))[:, di // 2, WIDTH * (di % 2) + i : WIDTH * (di % 2) + i + 1]

        p_sum = keep.tile([P, CHUNKS, CHANNELS], F32)
        band_weights = keep.tile([P, IMAGES * len(GROUPS), P], F32)
        zones = [keep.tile([P, BATCH, ZONE], F32, name="zones%d" % n) for n in range(2)]
        f_band = keep.tile([P, IMAGES, BAND, WIDTH + PATCH - STRIDE], BF16)
        f_patch = keep.tile([P, len(GROUPS), P], BF16)
        nc.gpsimd.memset(f_band[:], 0.0)
        nc.gpsimd.memset(f_patch[:], 0.0)
        for n in range(2):
            nc.gpsimd.memset(zones[n][:], 0.0)
        early = {}
        band_tiles = {}
        factor = {}

        x_slab = {}
        x_px = {}
        minus_top = {}
        total = {}
        inverse = {}
        q_px = {}
        q_back = {}
        g_slab = {}
        g_words = {}
        g_grouped = {}
        grad_operand = {}

        def load(slab, source, g):
            for b in range(IMAGES):
                for k in range(CHUNKS):
                    nc.sync.dma_start(out=slab[:, k, :, b, :], in_=source[b, k * P : (k + 1) * P, g * PACK : (g + 1) * PACK, :])

        def load_logits(g):
            x_slab[g] = slabs.tile([P, CHUNKS, PACK, IMAGES, WIDTH], BF16, name="x_slab")
            load(x_slab[g], input_logit, g)

        def turn_logits(r):
            x_px[r] = psum.tile([P, CHANNELS], BF16, name="x_px", tag="side_a")
            if r % PACK == PACK - 1 and r // PACK + 2 < PASSES:
                after(1, "sync", lambda: load_logits(r // PACK + 2))
            for k in range(CHUNKS):
                nc.tensor.transpose(
                    x_px[r][:, k * P : (k + 1) * P], x_slab[r // PACK][:, k, r % PACK, :, :].rearrange("p b j -> p (b j)"), ident_bf[:]
                )

        def find_top(r):
            minus_top[r] = stats.tile([P, 1], F32, name="minus_top")
            nc.vector.reduce_max(out=minus_top[r][:], in_=x_px[r][:], axis=AXIS.X, negate=True)

        def exponentials(r):
            q_px[r] = soft.tile([P, CHANNELS], F32, name="q_px")
            total[r] = stats.tile([P, 1], F32, name="total")
            nc.scalar.activation(
                out=q_px[r][:], in_=x_px[r][:], func=FUNC.Exp, bias=minus_top[r][:], scale=1.0, accum_out=total[r][:]
            )

        def invert(r):
            inverse[r] = stats.tile([P, 1], F32, name="inverse")
            nc.vector.reciprocal(out=inverse[r][:], in_=total[r][:])

        def normalise(r):
            nc.gpsimd.tensor_scalar(out=q_px[r][:], in0=q_px[r][:], scalar1=inverse[r][:], scalar2=0.0, op0=ALU.mult, op1=ALU.add)

        def turn_q(r):
            q_back[r] = psum.tile([P, CHUNKS, P], F32, name="q_back", tag="side_b")
            for k in range(CHUNKS):
                nc.tensor.transpose(q_back[r][:, k, :], q_px[r][:, k * P : (k + 1) * P], ident_f32)

        def keep_q(r):
            nc.scalar.copy(out=q_ring[r % RING][:, :, PAD : PAD + P], in_=q_back[r][:])

        def load_grad(g):
            g_slab[g] = slabs.tile([P, CHUNKS, PACK, IMAGES, WIDTH], BF16, name="g_slab")
            load(g_slab[g], grad_out, g)

        def turn_words(bank, rows_of):
            for u in range(2):
                for k in range(HALF // P):
                    nc.tensor.transpose(bank[:, u, k * P : (k + 1) * P], rows_of(k, u).bitcast(F32), ident_f32)

        def group_words(grouped, h, bank):
            nc.scalar.copy(out=grouped[:].bitcast(F32)[:, h * HALF : (h + 1) * HALF, :], in_=bank[:].rearrange("p u c -> p c u"))

        def turn_grad(g, h, bank):
            g_words[g, h] = psum.tile([P, 2, HALF], F32, name="g_words", tag=bank)
            turn_words(
                g_words[g, h],
                lambda k, u: g_slab[g][:, h * (HALF // P) + k, 2 * u : 2 * u + 2, :, :].rearrange("p s b j -> p (s b j)"),
            )

        def quantise_grad(g):
            g_codes = grad_codes.tile([P, CHANNELS], U32, align_bytes=64)
            g_scales = grad_codes.tile([P, CHANNELS], U8, align_bytes=64)
            nc.vector.quantize_mx(
                out=g_codes[:].bitcast(E5M2_X4), scales=g_scales[:], in_=g_grouped[g][:].rearrange("p o t -> p (o t)")
            )
            grad_operand[g] = (g_codes, g_scales)

        now = [0]
        timed = {}

        def at(slot, engine, job):
            assert slot > now[0] or not timed
            timed.setdefault(slot, []).extend([(engine, job)])

        def after(delay, engine, job):
            at(now[0] + delay, engine, job)

        busy = {"side_c": [], "side_b": [], "side_a": [], "window0": [], "window1": []}

        def reserve(earliest, hold, job):
            choice = []
            for bank in busy:
                slot = max(earliest, now[0] + 1)
                for first, last in sorted(busy[bank]):
                    if slot < last and first < slot + hold:
                        slot = last
                choice.extend([(slot, bank)])
            slot, bank = min(choice)
            busy[bank].extend([(slot, slot + hold)])
            at(slot, "tensor", lambda: job(bank))
            return slot

        words_free = {"m": -1000, "g": -1000}

        def reserve_words(kind, job):
            for h in range(2):
                words_free[kind] = reserve(max(now[0] + 1, words_free[kind]), HOLD, lambda bank, h=h: job(h, bank))
            words_free[kind] += 3

        def columns_of(r):
            return [
                dj
                for dj in VECTOR_COLUMNS
                if [di for di in range(KERNEL) if 0 <= r + REACH - di < HEIGHT and engine_of(r + REACH - di, di, dj) == "vector"]
            ]

        def vector_slots(r):
            ops = [
                (di, dj, r + REACH - di)
                for dj in columns_of(r)
                for di in range(KERNEL - 1, -1, -1)
                if 0 <= r + REACH - di < HEIGHT and engine_of(r + REACH - di, di, dj) == "vector"
            ]
            slots = max(LEAST, len(set([i for di, dj, i in ops])), -(-len(ops) // len(VECTOR_COLUMNS)), len(columns_of(r)) if len(columns_of(r)) > WINDOW_BANKS else 0)
            return [ops[len(ops) * t // slots : len(ops) * (t + 1) // slots] for t in range(slots)]

        def products_of(i):
            return [(di, dj) for dj in range(KERNEL) for di in range(KERNEL) if engine_of(i, di, dj) == "product"]

        vector_left = {}
        for r in range(HEIGHT):
            for ops in vector_slots(r):
                for di, dj, i in ops:
                    vector_left[i] = vector_left.get(i, 0) + 1

        def merged_of(i):
            pairs = []
            for dj in MERGE_COLUMNS:
                column = [tap for tap in products_of(i) if tap[1] == dj]
                if len(column) > 1:
                    pairs.extend([(column[0], column[1])])
            return pairs

        parts_left = {}
        for i in range(HEIGHT):
            parts_left[i] = len(products_of(i)) - len(merged_of(i)) + (1 if i in vector_left else 0)
        parts_in = dict(parts_left)

        todo = []
        todo_pairs = []
        halves = {}
        merges = []
        credit = [0]
        credit_scalar = [0]
        parts = []
        finale = []
        window = {}
        sum_vector = {}
        sum_slot = {}
        free_sums = list(range(SUMS))
        m_total = {}
        total_bank = {}
        free_totals = ["total_a", "total_b"]
        turned_slot = {}
        free_turned = list(range(TURNED))
        m_turned = {}
        m_words = {}
        m_grouped = {}
        m_operand = {}
        p_group = {}
        done = {}
        last_pass = PASSES - 1
        ready_early = [g for g in range(PASSES - GROUP, PASSES) if (g + 1) * PACK <= BAND_STARTS[-1]]
        ready_late = [g for g in range(PASSES - GROUP, PASSES) if g not in ready_early]

        def count(key, goal):
            done[key] = done.get(key, 0) + 1
            return done[key] == goal

        def make_window(r, dj, bank):
            start = PAD + dj - REACH
            window[r, dj] = psum.tile([P, CHANNELS], F32, name="window", tag="window%d" % bank)
            for k in range(CHUNKS):
                nc.tensor.transpose(window[r, dj][:, k * P : (k + 1) * P], q_ring[r % RING][:, k, start : start + P], ident_f32)

        def add_parts():
            waiting = [entry for entry in parts if entry[0] <= now[0]]
            tiles = []
            for entry in waiting:
                if entry[1] not in m_total and entry[1] not in tiles and len(tiles) < len(free_totals):
                    tiles.extend([entry[1]])
            for entry in reversed([entry for entry in waiting if entry[1] in m_total or entry[1] in tiles][:ADDS]):
                ready, i, part, shift = entry
                if i not in m_total:
                    total_bank[i] = free_totals[0]
                    free_totals.remove(total_bank[i])
                    m_total[i] = psum.tile([P, CHUNKS, P], F32, name="m_total", tag=total_bank[i])
                    first = True
                else:
                    first = False
                parts.remove(entry)
                if part is sum_vector.get(i):
                    free_sums.extend([sum_slot[i]])
                gone = [part]
                for pair in halves.values():
                    if pair[0] is part:
                        gone = pair
                for kind in unadded:
                    unadded[kind] = [None if [tile for tile in gone if tile is product] else product for product in unadded[kind]]
                parts_left[i] -= 1
                for k in range(CHUNKS):
                    nc.tensor.matmul(
                        m_total[i][:, k, :], lhsT=part[:, k * P : (k + 1) * P], rhs=twice[:, shift : shift + P], is_transpose=True,
                        start=(first and k == 0), stop=(parts_left[i] == 0 and k == CHUNKS - 1),
                    )
                if parts_left[i] == 0:
                    after(2, "scalar" if band_of(i) is None else "vector", lambda i=i: round_m(i))

        def round_m(i):
            a = band_of(i)
            if (i // PACK not in m_turned and not free_turned) or (a is not None and done.get(("patched", a), 0) < IMAGES * len(GROUPS)):
                after(1, "wait", lambda: round_m(i))
            else:
                row = turned_of(i // PACK)[:, :, i % PACK, :]
                if a is None:
                    nc.scalar.copy(out=row, in_=m_total[i][:])
                else:
                    nc.vector.tensor_tensor(out=row, in0=m_total[i][:], in1=band_tiles["patched"][:, :, i - a, :], op=ALU.add)
                free_totals.extend([total_bank[i]])
                row_done(i // PACK)

        def part_ready(a):
            if count(("ready", a), (1 if a == 0 else IMAGES * len(GROUPS) // BATCH) + 1):
                for b in range(IMAGES):
                    for n in range(len(GROUPS)):
                        reserve(now[0] + (FIRST_PATCH if a == 0 else PATCH_DELAY), HOLD, lambda bank, b=b, n=n: multiply_patch(a, b, n, bank))

        def round_patched(i):
            if i // PACK not in m_turned and not free_turned:
                after(1, "wait", lambda: round_patched(i))
            else:
                nc.gpsimd.tensor_copy(out=turned_of(i // PACK)[:, :, i % PACK, :], in_=band_tiles["patched"][:, :, i - band_of(i), :])
                row_done(i // PACK)

        def turned_of(g):
            if g not in m_turned:
                turned_slot[g] = free_turned[0]
                free_turned.remove(turned_slot[g])
                m_turned[g] = turned.tile([P, CHUNKS, PACK, P], BF16, name="m_turned", tag="turned%d" % turned_slot[g])
            return m_turned[g]

        def row_done(g):
            if count(("rounded", g), PACK):
                reserve_words("m", lambda h, bank: turn_m(g, h, bank))

        def turn_m(g, h, bank):
            m_words[g, h] = psum.tile([P, 2, HALF], F32, name="m_words", tag=bank)
            count(("m turned", g), 2)
            turn_words(
                m_words[g, h], lambda k, u: m_turned[g][:, h * (HALF // P) + k, 2 * u : 2 * u + 2, :].rearrange("p s n -> p (s n)")
            )
            if h == 1:
                free_turned.extend([turned_slot[g]])
            after(HOLD - 1, "scalar", lambda: group_m(g, h))

        def group_m(g, h):
            if h == 0:
                m_grouped[g] = operands.tile(
                    [P, CHANNELS, PACK], BF16, name="m_grouped", align_bytes=64
                )
            group_words(m_grouped[g], h, m_words[g, h])
            if h == 1:
                after(2, "vector", lambda: quantise_m(g))

        def quantise_m(g):
            m_codes = codes.tile([P, CHANNELS], U32, align_bytes=64)
            m_scales = codes.tile([P, CHANNELS], U8, align_bytes=64)
            nc.vector.quantize_mx(
                out=m_codes[:].bitcast(E4M3_X4), scales=m_scales[:], in_=m_grouped[g][:].rearrange("p c t -> p (c t)")
            )
            m_operand[g] = (m_codes, m_scales)
            last = g - g % GROUP + GROUP - 1
            if count(("quantised", last), GROUP) and last != last_pass:
                for k in range(CHUNKS):
                    reserve(now[0] + 2, HOLD, lambda bank, k=k: early_group(last, k, bank))

        def grad_chain(g, h, bank):
            turn_grad(g, h, bank)
            if h == 1 and g + 2 < PASSES:
                after(1, "sync", lambda: load_grad(g + 2))

            def group():
                if h == 0:
                    g_grouped[g] = operands.tile([P, CHANNELS, PACK], BF16, name="g_grouped", align_bytes=64)
                group_words(g_grouped[g], h, g_words[g, h])
                if h == 1:
                    after(2, "vector", lambda: quantise_grad(g))

            after(HOLD - 1, "scalar", group)

        def multiply(bank, k, passes, start, stop):
            for g in passes:
                g_codes, g_scales = grad_operand[g]
                m_codes, m_scales = m_operand[g]
                nc.tensor.matmul_mx(
                    out=bank[:],
                    lhsT=g_codes[:, k * P : (k + 1) * P].bitcast(E5M2_X4),
                    lhsT_scale=g_scales[:, k * P : (k + 1) * P],
                    rhs=m_codes[:].bitcast(E4M3_X4),
                    rhs_scale=m_scales[:],
                    start=(start and g == passes[0]),
                    stop=(stop and g == passes[-1]),
                )

        def early_group(last, k, bank):
            p_early = psum.tile([P, CHANNELS], F32, name="p_early", tag=bank)
            multiply(p_early, k, list(range(last - GROUP + 1, last + 1)), True, True)

            def gather():
                if last == GROUP - 1:
                    nc.vector.tensor_copy(out=p_sum[:, k, :], in_=p_early[:])
                else:
                    nc.vector.tensor_tensor(out=p_sum[:, k, :], in0=p_early[:], in1=p_sum[:, k, :], op=ALU.add)

            after(HOLD - 1, "vector", gather)

        def open_last_group(k):
            p_group[k] = psum.tile([P, CHANNELS], F32, name="p_group", tag=("total_a", "total_b", "side_a", "window2")[k])
            multiply(p_group[k], k, ready_early, True, False)

        def close_last_group(k):
            multiply(p_group[k], k, ready_late, False, True)
            nc.vector.tensor_tensor(out=p_sum[:, k, :], in0=p_group[k][:], in1=p_sum[:, k, :], op=ALU.add)
            nc.vector.scalar_tensor_tensor(
                out=factor[k][:], in0=p_sum[:, k, :], scalar=-100.0, in1=factor[k][:], op0=ALU.mult, op1=ALU.mult
            )
            nc.sync.dma_start(out=out_view[:, k, :], in_=factor[k][:])

        def seed(i):
            di = [di for di in range(KERNEL) if engine_of(i, di, SEED_COLUMN) == "seed"][0]
            sum_slot[i] = free_sums[0]
            free_sums.remove(sum_slot[i])
            sum_vector[i] = sums.tile([P, CHANNELS], F32, name="sum_vector", tag="sum%d" % sum_slot[i])
            nc.scalar.activation(out=sum_vector[i][:], in_=q_px[i + di - REACH][:], func=FUNC.Copy, scale=weight("source", di, SEED_COLUMN, i))

        def vector_taps(r, t):
            for di, dj, i in vector_slots(r)[t]:
                nc.vector.scalar_tensor_tensor(
                    out=sum_vector[i][:], in0=window[r, dj][:], scalar=weight("target", di, dj, i), in1=sum_vector[i][:],
                    op0=ALU.mult, op1=ALU.add,
                )
                vector_left[i] -= 1
                if vector_left[i] == 0:
                    parts.extend([(max(now[0] + 2, product_start[i] + EARLY), i, sum_vector[i], 0)])

        unadded = {"scalar": [], "gpsimd": [], "pair": []}

        def has_room(kind, tiles):
            return len(unadded[kind]) < tiles or unadded[kind][-tiles] is None

        def make_products(scalar_room, gpsimd_room):
            credit[0] = min(credit[0], 0) + gpsimd_room
            while credit[0] > 0:
                if merges and merges[0][0] <= now[0]:
                    ready, i, dj = merges[0]
                    merges.remove(merges[0])
                    pair = halves[i, dj]
                    nc.gpsimd.tensor_tensor(out=pair[0][:], in0=pair[0][:], in1=pair[1][:], op=ALU.add)
                    parts.extend([(now[0] + 3, i, pair[0], (dj - REACH) % P)])
                    credit[0] -= 3
                elif todo and has_room("gpsimd", PRODUCTS):
                    i, di, dj = todo[0]
                    todo.remove(todo[0])
                    product_g = products.tile([P, CHANNELS], F32)
                    nc.gpsimd.tensor_scalar(
                        out=product_g[:], in0=q_px[i + di - REACH][:], scalar1=weight("source", di, dj, i), scalar2=0.0,
                        op0=ALU.mult, op1=ALU.add,
                    )
                    unadded["gpsimd"].extend([product_g])
                    parts.extend([(now[0] + 3, i, product_g, (dj - REACH) % P)])
                    credit[0] -= 2
                else:
                    credit[0] = 0
            credit_scalar[0] = min(credit_scalar[0], 2) + scalar_room
            while credit_scalar[0] >= 3:
                credit_scalar[0] -= 3
                paired = len(todo_pairs) > 0 and has_room("pair", PAIRED)
                if paired or (todo and has_room("scalar", PRODUCTS)):
                    queue = todo_pairs if paired else todo
                    i, di, dj = queue[0]
                    queue.remove(queue[0])
                    product = (paired_products if paired else products).tile([P, CHANNELS], F32, name="product")
                    nc.scalar.activation(out=product[:], in_=q_px[i + di - REACH][:], func=FUNC.Copy, scale=weight("source", di, dj, i))
                    unadded["pair" if paired else "scalar"].extend([product])
                    if paired:
                        halves.setdefault((i, dj), []).extend([product])
                        if len(halves[i, dj]) == 2:
                            merges.extend([(now[0] + 2, i, dj)])
                    else:
                        parts.extend([(now[0] + 2, i, product, (dj - REACH) % P)])

        nominal = [0]
        for r in range(HEIGHT):
            nominal.extend([nominal[r] + len(vector_slots(r))])

        def pace(r):
            return 1 if r < FAST else 2

        turn_slot = {}
        for r in reversed(range(HEIGHT)):
            turn_slot[r] = nominal[r] - 18 - AHEAD
            if r + 1 < HEIGHT:
                turn_slot[r] = min(turn_slot[r], turn_slot[r + 1] - 2 * pace(r) - 1)
        first_row = {}
        for r in range(HEIGHT):
            for ops in vector_slots(r):
                for di, dj, i in ops:
                    first_row.setdefault(i, r)
        product_start = {}
        product_end = {}
        last_target = BAND_STARTS[0] + BANDS[BAND_STARTS[0]] - 1
        ahead = [last_target + 1, last_target + 2]
        product_order = ahead + [i for i in range(HEIGHT) if i not in ahead]

        def plan_products(rows):
            while len(product_start) < HEIGHT and product_order[len(product_start)] + REACH < rows:
                i = product_order[len(product_start)]
                last = min(i + REACH, HEIGHT - 1)
                begin = vector_start.get(i + REACH, clock) - EARLY
                if i in ahead:
                    begin = turn_slot[last] + 3 * pace(last) + 3
                product_start[i] = max([begin] + [product_end[n] for n in product_end])
                product_end[i] = product_start[i] + len(set([di for di, dj in products_of(i)]))

        q_slot = {}
        keep_slot = {}
        vector_start = {}
        vector_plan = {}
        window_plan = []
        window_free = {}
        last_window = {}
        clock = 0
        for r in range(HEIGHT):
            uses = {}
            for t, ops in enumerate(vector_slots(r)):
                for di, dj, i in ops:
                    uses.setdefault(dj, []).extend([t])
            old = r - Q_TILES + REACH
            if old >= 0:
                turn_slot[r] = max(turn_slot[r], product_end[old] + MARGIN - 2 * pace(r))
            if r > 0:
                turn_slot[r] = max(turn_slot[r], turn_slot[r - 1] + 2 * pace(r - 1) + 1)
            begun = len([i for i in first_row if first_row[i] <= r])
            if begun > SUMS:
                clock = max(clock, sorted([product_start[i] for i in product_start if i in first_row])[begun - SUMS - 1] + EARLY + MARGIN)
            q_slot[r] = max(clock - 8, turn_slot[r] + 3 * pace(r) + 3, keep_slot.get(r - 1, -1000) + 1)
            keep_slot[r] = max(q_slot[r] + 2, last_window.get(r - RING, -1000) + 1)
            start = clock
            settled = False
            while not settled:
                free = dict(window_free)
                made = []
                later = start
                for n, dj in enumerate(uses):
                    bank = (len(window_plan) + n) % WINDOW_BANKS
                    slot = max(clock + uses[dj][0] - 3, keep_slot[r] + 2, free.get(bank, -1000) + 1)
                    later = max(later, slot + 1 - uses[dj][0])
                    free[bank] = start + uses[dj][-1]
                    made.extend([(slot, r, dj, bank)])
                settled = later == start
                start = later
            window_free = free
            window_plan.extend(made)
            last_window[r] = max([slot for slot, row, dj, bank in made] + [keep_slot[r]])
            vector_start[r] = start
            for t in range(len(vector_slots(r))):
                vector_plan[start + t] = (r, t)
            clock = start + len(vector_slots(r))
            plan_products(r + 1)
        vector_end = clock
        plan_products(HEIGHT + REACH)
        for r in range(HEIGHT):
            busy["side_a"].extend([(turn_slot[r], turn_slot[r] + 2 * pace(r) + 1)])
            busy["side_b"].extend([(q_slot[r], keep_slot[r] + 1)])
        busy["side_a"].extend([(turn_slot[HEIGHT - 1], 10000)])
        for n in range(2):
            busy["window%d" % n].extend([(-1000, vector_end + 1)])

        first_slot = turn_slot[0] - 2
        now[0] = first_slot - 1
        ident_cols = ident_f32.rearrange("p (h j) -> p h j", j=WIDTH)
        outside = keep.tile([P, 2, KERNEL], F32)
        nc.vector.memset(outside[:], 0.0)
        for dj in range(KERNEL):
            reach = abs(dj - REACH)
            if reach > 0:
                left, right = ident_cols[:, :, 0:reach], ident_cols[:, :, WIDTH - reach : WIDTH]
                nc.vector.tensor_reduce(out=outside[:, 0, dj : dj + 1], in_=(left if dj < REACH else right), axis=AXIS.XY, op=ALU.add)
                nc.vector.tensor_reduce(out=outside[:, 1, dj : dj + 1], in_=(right if dj < REACH else left), axis=AXIS.XY, op=ALU.add)
        inside = keep.tile([P, 2, KERNEL], F32)
        nc.vector.tensor_scalar(out=inside[:], in0=outside[:], scalar1=-1.0, scalar2=1.0, op0=ALU.mult, op1=ALU.add)

        ident_patch = ident_f32.rearrange("p (j i) -> p j i", i=BAND)
        leaves = keep.tile([P, KERNEL], F32)
        nc.vector.memset(leaves[:], 0.0)
        for d in range(KERNEL):
            reach = abs(d - REACH)
            if reach > 0:
                edge = ident_patch[:, :, BAND - reach : BAND] if d > REACH else ident_patch[:, :, 0:reach]
                nc.vector.tensor_reduce(out=leaves[:, d : d + 1], in_=edge, axis=AXIS.XY, op=ALU.add)
        fits = keep.tile([P, KERNEL], F32)
        nc.vector.tensor_scalar(out=fits[:], in0=leaves[:], scalar1=-1.0, scalar2=1.0, op0=ALU.mult, op1=ALU.add)

        def open_head(head):
            f_raw = head.tile([P, KERNEL * PAIRS, P], BF16)
            f_wide = head.tile([P, KERNEL * PAIRS, PAD + P + PAD], F32)
            early["f_raw"] = f_raw
            early["f_wide"] = f_wide
            nc.vector.memset(f_raw[:], 0.0)
            nc.vector.memset(f_wide[:, :, 0:PAD], 0.0)
            nc.vector.memset(f_wide[:, :, PAD + P :], 0.0)
            early["zones"] = head.tile([P, IMAGES * len(GROUPS), ZONE], F32, name="all_zones")
            nc.gpsimd.memset(early["zones"][:], 0.0)
            load_logits(0)
            load_logits(1)
            load_band_weights(0)
            for b in range(IMAGES):
                for di in range(KERNEL):
                    nc.sync.dma_start(
                        out=f_raw[WIDTH * (di % 2) : WIDTH * (di % 2) + WIDTH, di // 2 : KERNEL * PAIRS : PAIRS, b * WIDTH : (b + 1) * WIDTH],
                        in_=input_F[b, di * KERNEL : (di + 1) * KERNEL].rearrange("q i j -> i q j"),
                    )

        def open_bands(bands):
            sources = bands.tile([P, SLICES, CHANNELS], F32)
            patched = bands.tile([P, CHUNKS, max(BANDS.values()), P], F32)
            band_tiles["sources"] = sources
            band_tiles["patched"] = patched
            nc.gpsimd.memset(sources[:], 0.0)
            clear_scratch()

        def make_factor():
            comp_bf = slabs.tile([P, CHUNKS, CHANNELS], BF16, name="x_slab")
            nc.sync.dma_start(out=comp_bf[:], in_=comp_view)
            for k in range(CHUNKS):
                factor[k] = paired_products.tile([P, CHANNELS], F32, name="product")
                other = products.tile([P, CHANNELS], F32, name="product")
                nc.scalar.activation(out=factor[k][:], in_=comp_bf[:, k, :], func=FUNC.Sigmoid, scale=100.0)
                nc.scalar.activation(out=other[:], in_=comp_bf[:, k, :], func=FUNC.Sigmoid, scale=-100.0)
                nc.gpsimd.tensor_tensor(out=factor[k][:], in0=factor[k][:], in1=other[:], op=ALU.mult)

        def load_band_weights(s):
            plane = HEIGHT * WIDTH
            total = IMAGES * KERNEL * KERNEL * plane
            for b in range(IMAGES):
                for di in range(KERNEL):
                    start = (b * KERNEL * KERNEL + di * KERNEL) * plane + (s - (di - REACH)) * WIDTH + REACH
                    many = EIGHT if start + EIGHT * plane <= total else KERNEL
                    begin = min(start, total - many * (plane - 1))
                    view = f_flat[begin : begin + many * (plane - 1)].rearrange("(d n) -> d n", n=plane - 1)
                    view = view[:, start - begin : start - begin + BAND * WIDTH].rearrange("d (i j) -> d i j", j=WIDTH)
                    nc.sync.dma_start(out=f_band[di * EIGHT : di * EIGHT + many, b, :, 0:WIDTH], in_=view)

        def cut_band_weights(b):
            for start, stop in ((0, STRIDE), (STRIDE, PATCH)):
                view = f_band[:, b, :, start : start + len(GROUPS) * STRIDE].rearrange("p i (n j) -> p n j i", j=STRIDE)
                nc.gpsimd.tensor_copy(
                    out=f_patch[:, :, start * BAND : stop * BAND].rearrange("p n (j i) -> p n j i", i=BAND), in_=view[:, :, 0 : stop - start, :]
                )

        pending = []

        def read_zones():
            for read in list(pending):
                pending.remove(read)
                read()

        def turn_band_weights(a, first, many, tile, at_once, bank):
            f_turned = psum.tile([P, many, P], BF16, name="f_turned", tag=bank)
            for n in range(many):
                nc.tensor.transpose(f_turned[:, n, :], f_patch[:, (first + n) % len(GROUPS), :], ident_bf[:])
            offset = first % at_once

            def spread():
                first_word = CENTRE - REACH * BAND - REACH
                words = tile[:, offset : offset + many, first_word : first_word + KERNEL * BAND]
                nc.vector.tensor_tensor(
                    out=words.rearrange("p g (e x) -> p g e x", x=BAND)[:, :, :, 0:KERNEL],
                    in0=f_turned[:, :, KERNEL * EIGHT - 1 :: -1].rearrange("p g (d e) -> p g e d", e=EIGHT)[:, :, 1:EIGHT, :],
                    in1=fits[:].unsqueeze(1).unsqueeze(1).to_broadcast([P, many, KERNEL, KERNEL]),
                    op=ALU.mult,
                )
                if offset + many == at_once:
                    after(1, "sync", skew)

            row = at_once * ZONE
            flat = out_flat[0 : P * row] if a == 0 else out_flat[zones_at : zones_at + P * row]

            def skew():
                read_zones()
                nc.sync.dma_start(out=flat.rearrange("(p x) -> p x", x=row), in_=tile[:].rearrange("p g z -> p (g z)"))
                pending.extend([unskew])
                after(2, "sync", read_zones)

            def unskew():
                assert not [n for n in BAND_STARTS if n < a and done.get(("multiplied", n), 0) < IMAGES * len(GROUPS)]
                view = flat[CENTRE : CENTRE + P * (row - 1)].rearrange("(p x) -> p x", x=row - 1)
                for n in range(at_once):
                    nc.sync.dma_start(out=band_weights[:, first - offset + n, 0 : BAND * PATCH], in_=view[:, n * ZONE : n * ZONE + BAND * PATCH])
                part_ready(a)

            after(HOLD - 1, "vector", spread)

        def next_band_weights(a, first):
            many = len(GROUPS) if a == 0 else BATCH
            tile = early["zones"] if a == 0 else zones[first // BATCH % 2]
            together = IMAGES * len(GROUPS) if a == 0 else BATCH

            def turn(bank):
                turn_band_weights(a, first, many, tile, together, bank)
                following = first + many
                if following == len(GROUPS):
                    after(1, "gpsimd", lambda: cut_band_weights(1))
                if following < IMAGES * len(GROUPS):
                    after(FIRST_STEP if a == 0 else BAND_STEP, "plan", lambda: next_band_weights(a, following))

            reserve(now[0] + 1, HOLD, turn)

        def clear_scratch():
            for n in range(SCRATCH * IMAGES):
                nc.sync.dma_start(out=out_rows[n * IMAGE_ROW + WIDTH : (n + 1) * IMAGE_ROW, :], in_=band_tiles["sources"][0 : IMAGE_ROW - WIDTH, 0, :])

        def store_sources(r):
            for b in range(IMAGES):
                first = r % SCRATCH * SCRATCH_ROW + b * IMAGE_ROW
                nc.sync.dma_start(out=out_rows[first : first + WIDTH, :], in_=q_px[r][b * WIDTH : (b + 1) * WIDTH, :])

        def gather_sources(s, r):
            sources = band_tiles["sources"][r - s : P : BAND, :, :]
            first = r % SCRATCH * SCRATCH_ROW
            for start, stop in ((0, STRIDE), (STRIDE, PATCH)):
                view = out_rows[first + start : first + start + SLICES * STRIDE, :].rearrange("(n j) c -> j n c", j=STRIDE)
                nc.sync.dma_start(out=sources[start:stop, :, :], in_=view[0 : stop - start, :, :])

        def multiply_patch(a, b, n, bank):
            first_target, columns = GROUPS[n]
            first = first_target - STRIDE * n
            row = a - sources_of(a)
            m_patch = psum.tile([P, CHUNKS, columns, BANDS[a]], F32, name="m_patch", tag=bank)
            for k in range(CHUNKS):
                nc.tensor.matmul(
                    m_patch[:, k, :, :],
                    lhsT=band_tiles["sources"][:, b * (IMAGE_ROW // STRIDE) + n, k * P : (k + 1) * P],
                    rhs=band_weights[:, b * len(GROUPS) + n, 0 : BAND * PATCH].rearrange("p (j i) -> p j i", i=BAND)[:, first : first + columns, row : row + BANDS[a]],
                    start=True, stop=True,
                )

            def finish():
                targets_at = b * WIDTH + first_target
                nc.scalar.copy(
                    out=band_tiles["patched"][:, :, 0 : BANDS[a], targets_at : targets_at + columns], in_=m_patch[:].rearrange("p k j i -> p k i j")
                )
                if count(("patched", a), IMAGES * len(GROUPS)):
                    for i in range(a, a + BANDS[a]):
                        if parts_in[i] == 0:
                            after(1 + i - a, "gpsimd", lambda i=i: round_patched(i))

            count(("multiplied", a), 0)
            after(HOLD - 1, "scalar", finish)

        def widen(dj):
            nc.vector.tensor_copy(
                out=early["f_wide"][:, dj * PAIRS : (dj + 1) * PAIRS, PAD : PAD + P], in_=early["f_raw"][:, dj * PAIRS : (dj + 1) * PAIRS, :]
            )

        def make_table(n, bank):
            kind, dj = tables[n]
            if kind == "target":
                f_px = psum.tile([P, PAIRS, P], BF16, name="f_px", tag=bank)
                for a in range(PAIRS):
                    nc.tensor.transpose(f_px[:, a, :], early["f_raw"][:, dj * PAIRS + a, :], ident_bf[:])
            else:
                start = PAD - (dj - REACH)
                f_px = psum.tile([P, PAIRS, P], F32, name="f_px", tag=bank)
                for a in range(PAIRS):
                    nc.tensor.transpose(f_px[:, a, :], early["f_wide"][:, dj * PAIRS + a, start : start + P], ident_f32)
            after(
                1, "scalar",
                lambda: nc.scalar.activation(
                    out=table(n), in_=f_px[:], func=FUNC.Copy, scale=inside[:, (0 if kind == "target" else 1), dj : dj + 1]
                ),
            )

        first = len(VECTOR_COLUMNS)
        order = list(range(first)) + list(range(targets, len(tables))) + list(range(first, targets))
        for q, n in enumerate(order):
            kind, dj = tables[n]
            if q >= first and kind == "source":
                at(-8 + q, "vector", lambda dj=dj: widen(dj))
            at(-13 + 2 * q if q < first else -4 + q, "tensor", lambda n=n, q=q: make_table(n, ("total_a", "total_b")[q % 2]))
        head_end = -4 + len(order) + 2

        for g in range(2):
            at(first_slot + 20 * g, "sync", lambda g=g: load_grad(g))
        for r in range(HEIGHT):
            at(turn_slot[r], "tensor", lambda r=r: turn_logits(r))
            at(turn_slot[r] + pace(r), "vector", lambda r=r: find_top(r))
            at(turn_slot[r] + 2 * pace(r), "scalar", lambda r=r: exponentials(r))
            at(turn_slot[r] + 3 * pace(r), "vector", lambda r=r: invert(r))
            at(turn_slot[r] + 3 * pace(r) + 1, "gpsimd", lambda r=r: normalise(r))
            if columns_of(r):
                at(q_slot[r], "tensor", lambda r=r: turn_q(r))
                at(keep_slot[r], "scalar", lambda r=r: keep_q(r))
        seeded = []
        for slot in sorted(vector_plan):
            r, t = vector_plan[slot]
            for di, dj, i in vector_slots(r)[t]:
                if i not in seeded:
                    seeded.extend([i])
                    at(max(slot - SEED_AHEAD, turn_slot[r] + 3 * pace(r) + 3), "scalar", lambda i=i: seed(i))
        for slot, r, dj, bank in window_plan:
            at(slot, "tensor", lambda r=r, dj=dj, bank=bank: make_window(r, dj, bank))
        moves = []
        for a in BAND_STARTS:
            begin = vector_start[a] - BAND_BEGIN
            s = sources_of(a)
            if a > 0:
                at(begin, "sync", lambda s=s: load_band_weights(s))
            loaded = begin + BAND_LOAD if a > 0 else first_slot + FIRST_BAND
            at(loaded, "gpsimd", lambda: cut_band_weights(0))
            at(loaded + 4, "plan", lambda a=a: next_band_weights(a, 0))
            for r in range(s, s + BAND):
                slot = max(turn_slot[r] + 3 * pace(r) + 3, head_end + 1)
                moves.extend([(slot, a, lambda r=r: store_sources(r))])
                if r > s:
                    moves.extend([(slot, a, lambda s=s, r=r: gather_sources(s, r - 1))])
            moves.extend([(slot + 3, a, lambda s=s: gather_sources(s, s + BAND - 1)), (slot + 3, a, lambda a=a: part_ready(a))])
        finale.extend([(lambda: not parts and not todo and not todo_pairs and not merges, make_factor)])
        for k in range(CHUNKS):
            finale.extend([(lambda: len(free_totals) == 2 and not [g for g in ready_early if g not in m_operand or g not in grad_operand], lambda k=k: open_last_group(k))])
        for k in range(CHUNKS):
            finale.extend([(lambda: not [g for g in ready_late if g not in m_operand or g not in grad_operand], lambda k=k: close_last_group(k))])

        def write_slot(slot):
            now[0] = slot
            for i in [i for i in range(HEIGHT) if product_start[i] == slot]:
                pairs = merged_of(i)
                for pair in pairs:
                    todo_pairs.extend([(i, pair[0][0], pair[0][1]), (i, pair[1][0], pair[1][1])])
                todo.extend([(i, di, dj) for di, dj in products_of(i) if not [pair for pair in pairs if (di, dj) in pair]])
            for g in range(PASSES):
                if slot == vector_start[PACK * g] + (GRAD_DELAY if g < PASSES - 2 else 14):
                    reserve_words("g", lambda h, bank, g=g: grad_chain(g, h, bank))
            jobs = timed.get(slot, [])
            for engine, job in jobs:
                job()
            while moves and moves[0][0] <= slot and not [n for n in BAND_STARTS if n < moves[0][1] and done.get(("multiplied", n), 0) < IMAGES * len(GROUPS)]:
                move = moves[0]
                moves.remove(move)
                move[2]()
            add_parts()
            if slot >= vector_end and finale and finale[0][0]():
                job = finale[0]
                finale.remove(job)
                job[1]()
            make_products(
                SCALAR_ROOM - 3 * len([job for job in jobs if job[0] == "scalar"]), GPSIMD_ROOM - 2 * len([job for job in jobs if job[0] == "gpsimd"])
            )
            if slot in vector_plan:
                vector_taps(vector_plan[slot][0], vector_plan[slot][1])

        with tc.tile_pool(name="head", bufs=1) as head:
            open_head(head)
            for slot in range(first_slot, head_end):
                write_slot(slot)
        with tc.tile_pool(name="bands", bufs=1) as bands:
            open_bands(bands)
            for slot in range(head_end, vector_end + 12 * SLOTS):
                write_slot(slot)
        assert not (parts or todo or todo_pairs or merges or finale)
        assert max(timed) <= now[0]
